import numpy as np
import ml_dtypes


def mxq(x, axis, fmt="e4m3"):
    dtype, down = {"e4m3": (ml_dtypes.float8_e4m3fn, 7), "e5m2": (ml_dtypes.float8_e5m2, 14)}[fmt]
    v = np.moveaxis(np.asarray(x, np.float32).astype(ml_dtypes.bfloat16).astype(np.float64), axis, -1)
    blocks = v.reshape(v.shape[:-1] + (-1, 32))
    amax = np.abs(blocks).max(-1, keepdims=True)
    byte = np.maximum(np.where(amax > 0, np.frexp(amax)[1] - 1 + 127, 0) - down, 1)
    scale = np.exp2(byte - 127.0)
    codes = (blocks / scale).astype(np.float32).astype(dtype).astype(np.float64)
    return np.moveaxis((codes * scale).reshape(v.shape), -1, axis)


WIDE = False


def mx_kscale(k):
    if not WIDE:
        return np.ones(k)
    levels = np.array([10, -10, 5, -5, 0])
    a = np.random.permutation(np.resize(levels, k // 512 * 4)).reshape(k // 512, 4)
    idx = np.arange(k)
    return np.exp2(a[idx // 512, idx % 128 // 32])


BF16 = ml_dtypes.bfloat16


def bf(x):
    return np.asarray(x, np.float32).astype(BF16)


def f64(x):
    return np.asarray(x).astype(np.float64)


B, T, HID, QH, KVH, D, W = 1, 1024, 2048, 16, 4, 128, 512
R = QH // KVH
NB = T // W


def setup_inputs():
    s = mx_kscale(HID)
    return {"q_rot": bf(np.random.standard_normal((B, T, QH, D)) * 1.5),
            "k_rot": bf(np.random.standard_normal((B, T, KVH, D)) * 1.5),
            "x": bf(np.random.standard_normal((B, T, HID)) * s),
            "wv": bf(np.random.standard_normal((KVH * D, HID)) * 2.0 / np.sqrt(HID) / s)}


def reference(q_rot, k_rot, x, wv):
    v = (mxq(f64(x), 2, "e4m3") @ mxq(f64(wv), 1, "e4m3").T).reshape(B, T, KVH, D)
    vq = mxq(v, 1, "e4m3").transpose(0, 2, 1, 3)
    qg = f64(q_rot).reshape(B, T, KVH, R, D).transpose(0, 2, 3, 1, 4)
    kt = f64(k_rot).transpose(0, 2, 3, 1)
    outs = []
    for i in range(NB):
        lo, t0, t1 = max(i - 1, 0) * W, i * W, (i + 1) * W
        sc = qg[:, :, :, t0:t1].reshape(B, KVH, R * W, D) @ kt[:, :, :, lo:t1] / np.sqrt(D)
        dist = np.arange(t0, t1)[:, None] - np.arange(lo, t1)[None, :]
        allowed = np.tile((dist >= 0) & (dist <= W), (R, 1))
        sc = np.where(allowed, sc, -np.inf)
        e = np.exp(sc - sc.max(-1, keepdims=True))
        o = (mxq(e, 3, "e4m3") @ vq[:, :, lo:t1]) / e.sum(-1, keepdims=True)
        outs.append(o.reshape(B, KVH, R, W, D).transpose(0, 3, 1, 2, 4))
    return np.concatenate(outs, axis=1).reshape(B, T, QH * D)

@@ -1,0 +1,329 @@
+import math
+
+import concourse.mybir as mybir
+from concourse.masks import make_identity
+
+F32 = mybir.dt.float32
+BF16 = mybir.dt.bfloat16
+U32 = mybir.dt.uint32
+U8 = mybir.dt.uint8
+FP8X4 = mybir.dt.float8_e4m3fn_x4
+ALU = mybir.AluOpType
+ACT = mybir.ActivationFunctionType
+AXIS_X = mybir.AxisListType.X
+
+P = 128
+PACK = 4
+K_PASS = P * PACK
+HALF = K_PASS // 2
+
+T = 1024
+HID = 2048
+KVH = 4
+R = 4
+D = 128
+W = 512
+CH = P // R
+CHUNKS = T // CH
+FIRST_FULL = W // CH
+X_PASSES = HID // K_PASS
+S_PASSES = T // K_PASS
+E_COLS = 3 * HALF
+PATTERNS = HALF // CH
+SCALE = 1.0 / math.sqrt(D)
+MASKED = -1.0e30
+
+FLOPS = 2 * T * HID * KVH * D + 2 * 2 * (KVH * R) * D * (W * W + W * 2 * W)
+
+
+def quantise_k_last(nc, stage, bank_pool, ident32, rows32, codes, scales):
+    grouped = stage.tile([P, X_PASSES * P * PACK], BF16, align_bytes=64, tag="grouped")
+    grouped32 = grouped[:].bitcast(F32).rearrange("p (c r u) -> p c r u", c=X_PASSES, u=2)
+    for pair in range(X_PASSES // 2):
+        flipped = bank_pool.tile([P, 2 * 2, P], F32, tag="flip")
+        for i in range(2 * 2):
+            first = (2 * 2 * pair + i) * P
+            nc.tensor.transpose(flipped[:, i, :], rows32[:, first : first + P], ident32[:])
+        nc.scalar.copy(
+            out=grouped32[:, 2 * pair : 2 * pair + 2],
+            in_=flipped[:].rearrange("p (c u) r -> p c r u", u=2),
+        )
+    nc.vector.quantize_mx(
+        out=codes.bitcast(FP8X4),
+        scales=scales,
+        in_=grouped[:],
+    )
+
+
+def tile_localgqattention_pb_kernel(tc, q_rot, k_rot, x, wv, out):
+    nc = tc.nc
+    q_rows = q_rot.rearrange("b t h d -> (b t) (h d)")
+    k_rows = k_rot.rearrange("b t h d -> (b t) (h d)")
+    x_rows = x.rearrange("b t k -> (b t) k")
+    out_rows = out.rearrange("b t f -> (b t) f")
+
+    with tc.tile_pool(name="const", bufs=1) as const, tc.tile_pool(name="keep", bufs=1) as keep:
+        warm = const.tile([P, 1], F32)
+        nc.vector.memset(warm[:], 0.0)
+        nc.scalar.activation(out=warm[:], in_=warm[:], func=ACT.Exp)
+
+        ident_bf = const.tile([P, P], BF16)
+        make_identity(nc, ident_bf[:])
+        ident32 = const.tile([P, P], F32)
+        make_identity(nc, ident32[:])
+        zeros = const.tile([P, 2 * P], BF16)
+        nc.vector.memset(zeros[:], 0.0)
+
+        spread = const.tile([P, R, CH], BF16)
+        nc.vector.tensor_copy(
+            out=spread[:], in_=ident_bf[:, 0:CH].unsqueeze(1).to_broadcast([P, R, CH])
+        )
+        own_f32 = const.tile([P, P], F32)
+        nc.gpsimd.memset(own_f32[:], 0.0)
+        nc.gpsimd.affine_select(
+            out=own_f32[:], in_=own_f32[:], compare_op=ALU.is_ge, fill=MASKED,
+            base=0, pattern=[[-1, P]], channel_multiplier=1,
+        )
+        own_bias = const.tile([P, CH], BF16)
+        nc.vector.tensor_copy(out=own_bias[:], in_=own_f32[:, 0:CH])
+        old_f32 = const.tile([P, P], F32)
+        nc.gpsimd.memset(old_f32[:], 0.0)
+        nc.gpsimd.affine_select(
+            out=old_f32[:], in_=old_f32[:], compare_op=ALU.is_ge, fill=MASKED,
+            base=0, pattern=[[1, P]], channel_multiplier=-1,
+        )
+        old_bias = const.tile([P, W // CH, CH], BF16)
+        nc.vector.tensor_copy(
+            out=old_bias[:], in_=old_f32[:, 0:CH].unsqueeze(1).to_broadcast([P, W // CH, CH])
+        )
+
+        kT = keep.tile([P, KVH, T], BF16)
+        qT = keep.tile([P, KVH, CHUNKS, R, CH], BF16)
+        v_codes = keep.tile([P, S_PASSES, KVH * D], U32, align_bytes=64)
+        v_scales = keep.tile([P, S_PASSES, KVH * D], U8, align_bytes=64)
+        old_scores = keep.tile([P, CHUNKS - FIRST_FULL, KVH, CH], F32)
+        old_max = keep.tile([P, CHUNKS - FIRST_FULL, KVH], F32)
+
+        with tc.tile_pool(name="raw", bufs=1) as raw, tc.tile_pool(
+            name="stage", bufs=3
+        ) as stage, tc.psum_pool(name="flip", bufs=5) as flip, tc.psum_pool(
+            name="vsum", bufs=2
+        ) as vsum:
+            wv_raw = []
+            for g in range(KVH):
+                t_wv = raw.tile([P, HID], BF16, name="wv_raw%d" % g)
+                nc.sync.dma_start(out=t_wv[:], in_=wv[g * D : (g + 1) * D, :])
+                wv_raw.append(t_wv)
+            x_raw = []
+            for run in range(T // HALF):
+                t_x = raw.tile([P, 2 * HID], BF16, name="x_raw%d" % run)
+                nc.sync.dma_start(
+                    out=t_x[:],
+                    in_=x_rows[run * HALF : (run + 1) * HALF, :].rearrange("(p e) k -> p (e k)", e=2),
+                )
+                x_raw.append(t_x)
+            k_raw = raw.tile([P, T // P, KVH * D], BF16)
+            nc.sync.dma_start(out=k_raw[:], in_=k_rows.rearrange("(n p) f -> p n f", p=P))
+            q_raw = []
+            for n in range(T // P):
+                t_q = raw.tile([P, KVH * R * D], BF16, name="q_raw%d" % n)
+                nc.sync.dma_start(out=t_q[:], in_=q_rows[n * P : (n + 1) * P, :])
+                q_raw.append(t_q)
+
+            w_codes = raw.tile([P, KVH, X_PASSES * D], U32, align_bytes=64)
+            w_scales = raw.tile([P, KVH, X_PASSES * D], U8, align_bytes=64)
+            for g in range(KVH):
+                quantise_k_last(
+                    nc, stage, flip, ident32, wv_raw[g][:].bitcast(F32),
+                    w_codes[:, g, :], w_scales[:, g, :],
+                )
+            x_codes = raw.tile([P, T // P, X_PASSES * P], U32, align_bytes=64)
+            x_scales = raw.tile([P, T // P, X_PASSES * P], U8, align_bytes=64)
+            for run in range(T // HALF):
+                for odd in range(2):
+                    quantise_k_last(
+                        nc, stage, flip, ident32,
+                        x_raw[run][:].bitcast(F32)[:, odd * (HID // 2) : (odd + 1) * (HID // 2)],
+                        x_codes[:, 2 * run + odd, :], x_scales[:, 2 * run + odd, :],
+                    )
+            v_grouped = raw.tile([P, S_PASSES, KVH, D, PACK], BF16, align_bytes=64)
+            for sp in range(S_PASSES):
+                for g in range(KVH):
+                    v_sum = vsum.tile([P, PACK, D], F32)
+                    for j in range(PACK):
+                        for kp in range(X_PASSES):
+                            cols = slice(kp * P, (kp + 1) * P)
+                            nc.tensor.matmul_mx(
+                                out=v_sum[:, j, :],
+                                lhsT=x_codes[:, PACK * sp + j, cols].bitcast(FP8X4),
+                                lhsT_scale=x_scales[:, PACK * sp + j, cols],
+                                rhs=w_codes[:, g, cols].bitcast(FP8X4),
+                                rhs_scale=w_scales[:, g, cols],
+                                start=(kp == 0),
+                                stop=(kp == X_PASSES - 1),
+                            )
+                    nc.scalar.copy(
+                        out=v_grouped[:, sp, g, :, :], in_=v_sum[:].rearrange("p j d -> p d j")
+                    )
+                nc.vector.quantize_mx(
+                    out=v_codes[:, sp, :].bitcast(FP8X4),
+                    scales=v_scales[:, sp, :],
+                    in_=v_grouped[:, sp].rearrange("p g d j -> p (g d j)"),
+                )
+
+            for n in range(T // P):
+                k_flip = flip.tile([P, KVH, P], BF16, tag="flip")
+                for g in range(KVH):
+                    nc.tensor.transpose(k_flip[:, g, :], k_raw[:, n, g * D : (g + 1) * D], ident_bf[:])
+                nc.vector.tensor_copy(out=kT[:, :, n * P : (n + 1) * P], in_=k_flip[:])
+            for n in range(T // P):
+                for g in range(KVH):
+                    q_flip = flip.tile([P, R, P], BF16, tag="flip")
+                    for h in range(R):
+                        first = (g * R + h) * D
+                        nc.tensor.transpose(q_flip[:, h, :], q_raw[n][:, first : first + D], ident_bf[:])
+                    nc.vector.tensor_copy(
+                        out=qT[:, g, n * (P // CH) : (n + 1) * (P // CH), :, :],
+                        in_=q_flip[:].rearrange("d h (c i) -> d c h i", i=CH),
+                    )
+
+            per_bank = W // CH // KVH
+            for b in range((CHUNKS - FIRST_FULL) // per_bank):
+                old_ps = flip.tile([P, per_bank, KVH, CH], F32, tag="flip")
+                nc.tensor.matmul(
+                    out=old_ps[:].rearrange("p c g j -> p (c g j)"),
+                    lhsT=spread[:].rearrange("k h i -> k (h i)"),
+                    rhs=old_bias[:].rearrange("k n j -> k (n j)"),
+                    start=True,
+                    stop=False,
+                )
+                for i in range(per_bank):
+                    c = FIRST_FULL + b * per_bank + i
+                    for g in range(KVH):
+                        nc.tensor.matmul(
+                            out=old_ps[:, i, g, :],
+                            lhsT=qT[:, g, c].rearrange("d h i -> d (h i)"),
+                            rhs=kT[:, g, c * CH - W : c * CH - W + CH],
+                            start=False,
+                            stop=(i == per_bank - 1 and g == KVH - 1),
+                        )
+                rows = slice(b * per_bank, (b + 1) * per_bank)
+                nc.vector.tensor_reduce(out=old_max[:, rows, :], in_=old_ps[:], axis=AXIS_X, op=ALU.max)
+                nc.scalar.copy(out=old_scores[:, rows], in_=old_ps[:])
+
+        with tc.tile_pool(name="etiles", bufs=1, reuse_waits="tile") as etiles, tc.tile_pool(
+            name="work", bufs=4, reuse_waits="tile"
+        ) as work, tc.tile_pool(name="stat", bufs=4, reuse_waits="tile") as stat, tc.psum_pool(
+            name="score", bufs=4, reuse_waits="tile"
+        ) as score_pool, tc.psum_pool(name="eflip", bufs=2, reuse_waits="tile") as eflip, tc.psum_pool(
+            name="osum", bufs=2, reuse_waits="tile"
+        ) as osum:
+            e_tiles = []
+            for place in range(PATTERNS):
+                e_row = []
+                for g in range(KVH):
+                    t_e = etiles.tile([P, E_COLS], BF16, name="e_%d_%d" % (place, g))
+                    if place > 0:
+                        nc.gpsimd.memset(t_e[:, 0 : place * CH], 0.0)
+                    if place * CH + CH + W < E_COLS:
+                        nc.gpsimd.memset(t_e[:, place * CH + CH + W : E_COLS], 0.0)
+                    e_row.append(t_e)
+                e_tiles.append(e_row)
+
+            for c in range(CHUNKS):
+                full = c >= FIRST_FULL
+                new = min((c + 1) * CH, W)
+                end = (c % PATTERNS) * CH + CH + W
+                last_run = c // PATTERNS
+                passes = last_run // 2 + 1
+
+                top = stat.tile([P, KVH], F32)
+                shift = stat.tile([P, KVH], F32)
+                sums = stat.tile([P, 2, KVH], F32)
+                o_sum = osum.tile([P, KVH, D], F32)
+                for g in range(KVH):
+                    q_cols = qT[:, g, c].rearrange("d h i -> d (h i)")
+                    scores = score_pool.tile([P, W], F32)
+                    nc.tensor.matmul(
+                        out=scores[:, 0:new], lhsT=q_cols,
+                        rhs=kT[:, g, (c + 1) * CH - new : (c + 1) * CH], start=True, stop=False,
+                    )
+                    nc.tensor.matmul(
+                        out=scores[:, new - CH : new], lhsT=spread[:].rearrange("k h i -> k (h i)"),
+                        rhs=own_bias[:], start=False, stop=True,
+                    )
+                    nc.vector.tensor_reduce(
+                        out=top[:, g : g + 1], in_=scores[:, 0:new], axis=AXIS_X, op=ALU.max
+                    )
+                    if full:
+                        nc.vector.tensor_scalar(
+                            out=shift[:, g : g + 1], in0=top[:, g : g + 1],
+                            scalar1=old_max[:, c - FIRST_FULL, g : g + 1], scalar2=-SCALE,
+                            op0=ALU.max, op1=ALU.mult,
+                        )
+                    else:
+                        nc.vector.tensor_scalar(
+                            out=shift[:, g : g + 1], in0=top[:, g : g + 1],
+                            scalar1=-SCALE, scalar2=None, op0=ALU.mult,
+                        )
+                    e = e_tiles[c % PATTERNS][g]
+                    nc.scalar.activation(
+                        out=e[:, end - new : end], in_=scores[:, 0:new], func=ACT.Exp,
+                        bias=shift[:, g : g + 1], scale=SCALE, accum_out=sums[:, 0, g : g + 1],
+                    )
+                    if full:
+                        nc.scalar.activation(
+                            out=e[:, end - new - CH : end - new], in_=old_scores[:, c - FIRST_FULL, g, :],
+                            func=ACT.Exp, bias=shift[:, g : g + 1], scale=SCALE,
+                            accum_out=sums[:, 1, g : g + 1],
+                        )
+
+                    e32 = e[:].bitcast(F32)
+                    e_words = eflip.tile([P, 2 * S_PASSES, P], F32)
+                    for r in range(2 * passes):
+                        i = r - (last_run - 2)
+                        if 0 <= i < 3:
+                            nc.tensor.transpose(e_words[:, r, :], e32[:, i * P : (i + 1) * P], ident32[:])
+                        else:
+                            nc.tensor.transpose(e_words[:, r, :], zeros[:].bitcast(F32), ident32[:])
+                    e_grouped = work.tile([P, S_PASSES * P * PACK], BF16, align_bytes=64)
+                    e_grouped32 = e_grouped[:].bitcast(F32).rearrange("p (s t u) -> p s t u", s=S_PASSES, u=2)
+                    nc.scalar.copy(
+                        out=e_grouped32[:, 0:passes],
+                        in_=e_words[:, 0 : 2 * passes, :].rearrange("p (s u) t -> p s t u", u=2),
+                    )
+                    e_codes = work.tile([P, S_PASSES * P], U32, align_bytes=64)
+                    e_scales = work.tile([P, S_PASSES * P], U8, align_bytes=64)
+                    nc.vector.quantize_mx(
+                        out=e_codes[:, 0 : passes * P].bitcast(FP8X4),
+                        scales=e_scales[:, 0 : passes * P],
+                        in_=e_grouped[:, 0 : passes * P * PACK],
+                    )
+                    for sp in range(passes):
+                        nc.tensor.matmul_mx(
+                            out=o_sum[:, g, :],
+                            lhsT=e_codes[:, sp * P : (sp + 1) * P].bitcast(FP8X4),
+                            lhsT_scale=e_scales[:, sp * P : (sp + 1) * P],
+                            rhs=v_codes[:, sp, g * D : (g + 1) * D].bitcast(FP8X4),
+                            rhs_scale=v_scales[:, sp, g * D : (g + 1) * D],
+                            start=(sp == 0),
+                            stop=(sp == passes - 1),
+                        )
+
+                inverse = stat.tile([P, KVH], F32)
+                if full:
+                    total = stat.tile([P, KVH], F32)
+                    nc.vector.tensor_tensor(out=total[:], in0=sums[:, 0, :], in1=sums[:, 1, :], op=ALU.add)
+                    nc.vector.reciprocal(out=inverse[:], in_=total[:])
+                else:
+                    nc.vector.reciprocal(out=inverse[:], in_=sums[:, 0, :])
+                o_sb = work.tile([P, KVH, D], F32)
+                nc.vector.tensor_tensor(
+                    out=o_sb[:], in0=o_sum[:], in1=inverse[:].unsqueeze(2).to_broadcast([P, KVH, D]),
+                    op=ALU.mult,
+                )
+                chunk_rows = out_rows[c * CH : (c + 1) * CH, :].rearrange(
+                    "i (g h d) -> h i g d", g=KVH, h=R
+                )
+                for h in range(R):
+                    nc.sync.dma_start(out=chunk_rows[h], in_=o_sb[h * CH : (h + 1) * CH, :, :])

@@ -78,6 +78,7 @@ def tile_localgqattention_pb_kernel(tc, q_rot, k_rot, x, wv, out):
         nc.vector.tensor_copy(
             out=spread[:], in_=ident_bf[:, 0:CH].unsqueeze(1).to_broadcast([P, R, CH])
         )
+        spread_cols = spread[:].rearrange("k h i -> k (h i)")
         own_f32 = const.tile([P, P], F32)
         nc.gpsimd.memset(own_f32[:], 0.0)
         nc.gpsimd.affine_select(
@@ -97,6 +98,18 @@ def tile_localgqattention_pb_kernel(tc, q_rot, k_rot, x, wv, out):
             out=old_bias[:], in_=old_f32[:, 0:CH].unsqueeze(1).to_broadcast([P, W // CH, CH])
         )
 
+        e_tiles = []
+        for place in range(PATTERNS):
+            e_row = []
+            for g in range(KVH):
+                t_e = keep.tile([P, E_COLS], BF16, name="e_%d_%d" % (place, g))
+                if place > 0:
+                    nc.gpsimd.memset(t_e[:, 0 : place * CH], 0.0)
+                if place * CH + CH + W < E_COLS:
+                    nc.gpsimd.memset(t_e[:, place * CH + CH + W : E_COLS], 0.0)
+                e_row.append(t_e)
+            e_tiles.append(e_row)
+
         kT = keep.tile([P, KVH, T], BF16)
         qT = keep.tile([P, KVH, CHUNKS, R, CH], BF16)
         v_codes = keep.tile([P, S_PASSES, KVH * D], U32, align_bytes=64)
@@ -104,11 +117,18 @@ def tile_localgqattention_pb_kernel(tc, q_rot, k_rot, x, wv, out):
         old_scores = keep.tile([P, CHUNKS - FIRST_FULL, KVH, CH], F32)
         old_max = keep.tile([P, CHUNKS - FIRST_FULL, KVH], F32)
 
-        with tc.tile_pool(name="raw", bufs=1) as raw, tc.tile_pool(
+        with tc.tile_pool(name="raw", bufs=1) as raw, tc.tile_pool(name="qraw", bufs=4) as qraw, tc.tile_pool(
             name="stage", bufs=3
         ) as stage, tc.psum_pool(name="flip", bufs=5) as flip, tc.psum_pool(
             name="vsum", bufs=2
         ) as vsum:
+            k_raw = raw.tile([P, T // P, KVH * D], BF16)
+            nc.sync.dma_start(out=k_raw[:], in_=k_rows.rearrange("(n p) f -> p n f", p=P))
+            q_raw = []
+            for n in range(T // P):
+                t_q = qraw.tile([P, KVH * R * D], BF16, name="q_raw", tag="q_raw")
+                nc.sync.dma_start(out=t_q[:], in_=q_rows[n * P : (n + 1) * P, :])
+                q_raw.append(t_q)
             wv_raw = []
             for g in range(KVH):
                 t_wv = raw.tile([P, HID], BF16, name="wv_raw%d" % g)
@@ -122,13 +142,47 @@ def tile_localgqattention_pb_kernel(tc, q_rot, k_rot, x, wv, out):
                     in_=x_rows[run * HALF : (run + 1) * HALF, :].rearrange("(p e) k -> p (e k)", e=2),
                 )
                 x_raw.append(t_x)
-            k_raw = raw.tile([P, T // P, KVH * D], BF16)
-            nc.sync.dma_start(out=k_raw[:], in_=k_rows.rearrange("(n p) f -> p n f", p=P))
-            q_raw = []
+
             for n in range(T // P):
-                t_q = raw.tile([P, KVH * R * D], BF16, name="q_raw%d" % n)
-                nc.sync.dma_start(out=t_q[:], in_=q_rows[n * P : (n + 1) * P, :])
-                q_raw.append(t_q)
+                k_flip = flip.tile([P, KVH, P], BF16, tag="flip")
+                for g in range(KVH):
+                    nc.tensor.transpose(k_flip[:, g, :], k_raw[:, n, g * D : (g + 1) * D], ident_bf[:])
+                nc.vector.tensor_copy(out=kT[:, :, n * P : (n + 1) * P], in_=k_flip[:])
+            for n in range(T // P):
+                for g in range(KVH):
+                    q_flip = flip.tile([P, R, P], BF16, tag="flip")
+                    for h in range(R):
+                        first = (g * R + h) * D
+                        nc.tensor.transpose(q_flip[:, h, :], q_raw[n][:, first : first + D], ident_bf[:])
+                    copy = nc.vector.tensor_copy if g % 2 == 0 else nc.scalar.copy
+                    copy(
+                        out=qT[:, g, n * (P // CH) : (n + 1) * (P // CH), :, :],
+                        in_=q_flip[:].rearrange("d h (c i) -> d c h i", i=CH),
+                    )
+
+            per_bank = W // CH // KVH
+            for b in range((CHUNKS - FIRST_FULL) // per_bank):
+                old_ps = flip.tile([P, per_bank, KVH, CH], F32, tag="flip")
+                nc.tensor.matmul(
+                    out=old_ps[:].rearrange("p c g j -> p (c g j)"),
+                    lhsT=spread_cols,
+                    rhs=old_bias[:].rearrange("k n j -> k (n j)"),
+                    start=True,
+                    stop=False,
+                )
+                for i in range(per_bank):
+                    c = FIRST_FULL + b * per_bank + i
+                    for g in range(KVH):
+                        nc.tensor.matmul(
+                            out=old_ps[:, i, g, :],
+                            lhsT=qT[:, g, c].rearrange("d h i -> d (h i)"),
+                            rhs=kT[:, g, c * CH - W : c * CH - W + CH],
+                            start=False,
+                            stop=(i == per_bank - 1 and g == KVH - 1),
+                        )
+                rows = slice(b * per_bank, (b + 1) * per_bank)
+                nc.vector.tensor_reduce(out=old_max[:, rows, :], in_=old_ps[:], axis=AXIS_X, op=ALU.max)
+                nc.scalar.copy(out=old_scores[:, rows], in_=old_ps[:])
 
             w_codes = raw.tile([P, KVH, X_PASSES * D], U32, align_bytes=64)
             w_scales = raw.tile([P, KVH, X_PASSES * D], U8, align_bytes=64)
@@ -171,159 +225,155 @@ def tile_localgqattention_pb_kernel(tc, q_rot, k_rot, x, wv, out):
                     in_=v_grouped[:, sp].rearrange("p g d j -> p (g d j)"),
                 )
 
-            for n in range(T // P):
-                k_flip = flip.tile([P, KVH, P], BF16, tag="flip")
-                for g in range(KVH):
-                    nc.tensor.transpose(k_flip[:, g, :], k_raw[:, n, g * D : (g + 1) * D], ident_bf[:])
-                nc.vector.tensor_copy(out=kT[:, :, n * P : (n + 1) * P], in_=k_flip[:])
-            for n in range(T // P):
-                for g in range(KVH):
-                    q_flip = flip.tile([P, R, P], BF16, tag="flip")
-                    for h in range(R):
-                        first = (g * R + h) * D
-                        nc.tensor.transpose(q_flip[:, h, :], q_raw[n][:, first : first + D], ident_bf[:])
-                    nc.vector.tensor_copy(
-                        out=qT[:, g, n * (P // CH) : (n + 1) * (P // CH), :, :],
-                        in_=q_flip[:].rearrange("d h (c i) -> d c h i", i=CH),
-                    )
-
-            per_bank = W // CH // KVH
-            for b in range((CHUNKS - FIRST_FULL) // per_bank):
-                old_ps = flip.tile([P, per_bank, KVH, CH], F32, tag="flip")
-                nc.tensor.matmul(
-                    out=old_ps[:].rearrange("p c g j -> p (c g j)"),
-                    lhsT=spread[:].rearrange("k h i -> k (h i)"),
-                    rhs=old_bias[:].rearrange("k n j -> k (n j)"),
-                    start=True,
-                    stop=False,
-                )
-                for i in range(per_bank):
-                    c = FIRST_FULL + b * per_bank + i
-                    for g in range(KVH):
-                        nc.tensor.matmul(
-                            out=old_ps[:, i, g, :],
-                            lhsT=qT[:, g, c].rearrange("d h i -> d (h i)"),
-                            rhs=kT[:, g, c * CH - W : c * CH - W + CH],
-                            start=False,
-                            stop=(i == per_bank - 1 and g == KVH - 1),
-                        )
-                rows = slice(b * per_bank, (b + 1) * per_bank)
-                nc.vector.tensor_reduce(out=old_max[:, rows, :], in_=old_ps[:], axis=AXIS_X, op=ALU.max)
-                nc.scalar.copy(out=old_scores[:, rows], in_=old_ps[:])
-
-        with tc.tile_pool(name="etiles", bufs=1, reuse_waits="tile") as etiles, tc.tile_pool(
-            name="work", bufs=4, reuse_waits="tile"
-        ) as work, tc.tile_pool(name="stat", bufs=4, reuse_waits="tile") as stat, tc.psum_pool(
+        with tc.tile_pool(name="work", bufs=3, reuse_waits="tile") as work, tc.tile_pool(
+            name="packed", bufs=2 * KVH, reuse_waits="tile"
+        ) as packed, tc.tile_pool(name="stat", bufs=4, reuse_waits="tile") as stat, tc.psum_pool(
             name="score", bufs=4, reuse_waits="tile"
         ) as score_pool, tc.psum_pool(name="eflip", bufs=2, reuse_waits="tile") as eflip, tc.psum_pool(
             name="osum", bufs=2, reuse_waits="tile"
         ) as osum:
-            e_tiles = []
-            for place in range(PATTERNS):
-                e_row = []
-                for g in range(KVH):
-                    t_e = etiles.tile([P, E_COLS], BF16, name="e_%d_%d" % (place, g))
-                    if place > 0:
-                        nc.gpsimd.memset(t_e[:, 0 : place * CH], 0.0)
-                    if place * CH + CH + W < E_COLS:
-                        nc.gpsimd.memset(t_e[:, place * CH + CH + W : E_COLS], 0.0)
-                    e_row.append(t_e)
-                e_tiles.append(e_row)
+            of_chunk = {}
+            of_tile = {}
 
-            for c in range(CHUNKS):
-                full = c >= FIRST_FULL
+            def score(c, g):
+                if g == 0:
+                    of_chunk[c] = {
+                        "top": stat.tile([P, KVH], F32, name="top"),
+                        "shift": stat.tile([P, KVH], F32, name="shift"),
+                        "sums": stat.tile([P, 2, KVH], F32, name="sums"),
+                    }
+                new = min((c + 1) * CH, W)
+                scores = score_pool.tile([P, W], F32)
+                nc.tensor.matmul(
+                    out=scores[:, 0:new], lhsT=qT[:, g, c].rearrange("d h i -> d (h i)"),
+                    rhs=kT[:, g, (c + 1) * CH - new : (c + 1) * CH], start=True, stop=False,
+                )
+                nc.tensor.matmul(
+                    out=scores[:, new - CH : new], lhsT=spread_cols, rhs=own_bias[:],
+                    start=False, stop=True,
+                )
+                of_tile[c, g] = {"scores": scores}
+
+            def peak(c, g):
+                new = min((c + 1) * CH, W)
+                top = of_chunk[c]["top"][:, g : g + 1]
+                shift = of_chunk[c]["shift"][:, g : g + 1]
+                nc.vector.tensor_reduce(
+                    out=top, in_=of_tile[c, g]["scores"][:, 0:new], axis=AXIS_X, op=ALU.max
+                )
+                if c >= FIRST_FULL:
+                    nc.gpsimd.tensor_scalar(
+                        out=shift, in0=top, scalar1=old_max[:, c - FIRST_FULL, g : g + 1],
+                        scalar2=-SCALE, op0=ALU.max, op1=ALU.mult,
+                    )
+                else:
+                    nc.gpsimd.tensor_scalar(
+                        out=shift, in0=top, scalar1=-SCALE, scalar2=None, op0=ALU.mult
+                    )
+
+            def soften(c, g):
                 new = min((c + 1) * CH, W)
                 end = (c % PATTERNS) * CH + CH + W
+                shift = of_chunk[c]["shift"][:, g : g + 1]
+                sums = of_chunk[c]["sums"]
+                e = e_tiles[c % PATTERNS][g]
+                nc.scalar.activation(
+                    out=e[:, end - new : end], in_=of_tile[c, g]["scores"][:, 0:new], func=ACT.Exp,
+                    bias=shift, scale=SCALE, accum_out=sums[:, 0, g : g + 1],
+                )
+                if c >= FIRST_FULL:
+                    nc.scalar.activation(
+                        out=e[:, end - new - CH : end - new], in_=old_scores[:, c - FIRST_FULL, g, :],
+                        func=ACT.Exp, bias=shift, scale=SCALE, accum_out=sums[:, 1, g : g + 1],
+                    )
+                    if g == KVH - 1:
+                        total = stat.tile([P, KVH], F32, name="total")
+                        nc.gpsimd.tensor_tensor(out=total[:], in0=sums[:, 0, :], in1=sums[:, 1, :], op=ALU.add)
+                        of_chunk[c]["total"] = total[:]
+                elif g == KVH - 1:
+                    of_chunk[c]["total"] = sums[:, 0, :]
+
+            def flip_e(c, g):
                 last_run = c // PATTERNS
                 passes = last_run // 2 + 1
+                e32 = e_tiles[c % PATTERNS][g][:].bitcast(F32)
+                e_words = eflip.tile([P, 2 * S_PASSES, P], F32)
+                for r in range(2 * passes):
+                    i = r - (last_run - 2)
+                    if 0 <= i < 3:
+                        nc.tensor.transpose(e_words[:, r, :], e32[:, i * P : (i + 1) * P], ident32[:])
+                    else:
+                        nc.tensor.transpose(e_words[:, r, :], zeros[:].bitcast(F32), ident32[:])
+                of_tile[c, g]["e_words"] = e_words
 
-                top = stat.tile([P, KVH], F32)
-                shift = stat.tile([P, KVH], F32)
-                sums = stat.tile([P, 2, KVH], F32)
+            def regroup(c, g):
+                passes = c // PATTERNS // 2 + 1
+                e_grouped = work.tile([P, S_PASSES * P * PACK], BF16, align_bytes=64)
+                e_grouped32 = e_grouped[:].bitcast(F32).rearrange("p (s t u) -> p s t u", s=S_PASSES, u=2)
+                nc.scalar.copy(
+                    out=e_grouped32[:, 0:passes],
+                    in_=of_tile[c, g]["e_words"][:, 0 : 2 * passes, :].rearrange("p (s u) t -> p s t u", u=2),
+                )
+                of_tile[c, g]["e_grouped"] = e_grouped
+
+            def quantise(c, g):
+                passes = c // PATTERNS // 2 + 1
+                e_codes = packed.tile([P, S_PASSES * P], U32, align_bytes=64)
+                e_scales = packed.tile([P, S_PASSES * P], U8, align_bytes=64)
+                nc.vector.quantize_mx(
+                    out=e_codes[:, 0 : passes * P].bitcast(FP8X4),
+                    scales=e_scales[:, 0 : passes * P],
+                    in_=of_tile[c, g]["e_grouped"][:, 0 : passes * P * PACK],
+                )
+                of_tile[c, g]["e_codes"] = e_codes
+                of_tile[c, g]["e_scales"] = e_scales
+
+            def weigh(c):
+                passes = c // PATTERNS // 2 + 1
+                inverse = stat.tile([P, KVH], F32)
+                nc.vector.reciprocal(out=inverse[:], in_=of_chunk[c]["total"])
                 o_sum = osum.tile([P, KVH, D], F32)
                 for g in range(KVH):
-                    q_cols = qT[:, g, c].rearrange("d h i -> d (h i)")
-                    scores = score_pool.tile([P, W], F32)
-                    nc.tensor.matmul(
-                        out=scores[:, 0:new], lhsT=q_cols,
-                        rhs=kT[:, g, (c + 1) * CH - new : (c + 1) * CH], start=True, stop=False,
-                    )
-                    nc.tensor.matmul(
-                        out=scores[:, new - CH : new], lhsT=spread[:].rearrange("k h i -> k (h i)"),
-                        rhs=own_bias[:], start=False, stop=True,
-                    )
-                    nc.vector.tensor_reduce(
-                        out=top[:, g : g + 1], in_=scores[:, 0:new], axis=AXIS_X, op=ALU.max
-                    )
-                    if full:
-                        nc.vector.tensor_scalar(
-                            out=shift[:, g : g + 1], in0=top[:, g : g + 1],
-                            scalar1=old_max[:, c - FIRST_FULL, g : g + 1], scalar2=-SCALE,
-                            op0=ALU.max, op1=ALU.mult,
-                        )
-                    else:
-                        nc.vector.tensor_scalar(
-                            out=shift[:, g : g + 1], in0=top[:, g : g + 1],
-                            scalar1=-SCALE, scalar2=None, op0=ALU.mult,
-                        )
-                    e = e_tiles[c % PATTERNS][g]
-                    nc.scalar.activation(
-                        out=e[:, end - new : end], in_=scores[:, 0:new], func=ACT.Exp,
-                        bias=shift[:, g : g + 1], scale=SCALE, accum_out=sums[:, 0, g : g + 1],
-                    )
-                    if full:
-                        nc.scalar.activation(
-                            out=e[:, end - new - CH : end - new], in_=old_scores[:, c - FIRST_FULL, g, :],
-                            func=ACT.Exp, bias=shift[:, g : g + 1], scale=SCALE,
-                            accum_out=sums[:, 1, g : g + 1],
-                        )
-
-                    e32 = e[:].bitcast(F32)
-                    e_words = eflip.tile([P, 2 * S_PASSES, P], F32)
-                    for r in range(2 * passes):
-                        i = r - (last_run - 2)
-                        if 0 <= i < 3:
-                            nc.tensor.transpose(e_words[:, r, :], e32[:, i * P : (i + 1) * P], ident32[:])
-                        else:
-                            nc.tensor.transpose(e_words[:, r, :], zeros[:].bitcast(F32), ident32[:])
-                    e_grouped = work.tile([P, S_PASSES * P * PACK], BF16, align_bytes=64)
-                    e_grouped32 = e_grouped[:].bitcast(F32).rearrange("p (s t u) -> p s t u", s=S_PASSES, u=2)
-                    nc.scalar.copy(
-                        out=e_grouped32[:, 0:passes],
-                        in_=e_words[:, 0 : 2 * passes, :].rearrange("p (s u) t -> p s t u", u=2),
-                    )
-                    e_codes = work.tile([P, S_PASSES * P], U32, align_bytes=64)
-                    e_scales = work.tile([P, S_PASSES * P], U8, align_bytes=64)
-                    nc.vector.quantize_mx(
-                        out=e_codes[:, 0 : passes * P].bitcast(FP8X4),
-                        scales=e_scales[:, 0 : passes * P],
-                        in_=e_grouped[:, 0 : passes * P * PACK],
-                    )
                     for sp in range(passes):
                         nc.tensor.matmul_mx(
                             out=o_sum[:, g, :],
-                            lhsT=e_codes[:, sp * P : (sp + 1) * P].bitcast(FP8X4),
-                            lhsT_scale=e_scales[:, sp * P : (sp + 1) * P],
+                            lhsT=of_tile[c, g]["e_codes"][:, sp * P : (sp + 1) * P].bitcast(FP8X4),
+                            lhsT_scale=of_tile[c, g]["e_scales"][:, sp * P : (sp + 1) * P],
                             rhs=v_codes[:, sp, g * D : (g + 1) * D].bitcast(FP8X4),
                             rhs_scale=v_scales[:, sp, g * D : (g + 1) * D],
                             start=(sp == 0),
                             stop=(sp == passes - 1),
                         )
+                of_chunk[c]["inverse"] = inverse
+                of_chunk[c]["o_sum"] = o_sum
 
-                inverse = stat.tile([P, KVH], F32)
-                if full:
-                    total = stat.tile([P, KVH], F32)
-                    nc.vector.tensor_tensor(out=total[:], in0=sums[:, 0, :], in1=sums[:, 1, :], op=ALU.add)
-                    nc.vector.reciprocal(out=inverse[:], in_=total[:])
-                else:
-                    nc.vector.reciprocal(out=inverse[:], in_=sums[:, 0, :])
+            def finish(c):
                 o_sb = work.tile([P, KVH, D], F32)
                 nc.vector.tensor_tensor(
-                    out=o_sb[:], in0=o_sum[:], in1=inverse[:].unsqueeze(2).to_broadcast([P, KVH, D]),
-                    op=ALU.mult,
+                    out=o_sb[:], in0=of_chunk[c]["o_sum"][:],
+                    in1=of_chunk[c]["inverse"][:].unsqueeze(2).to_broadcast([P, KVH, D]), op=ALU.mult,
                 )
-                chunk_rows = out_rows[c * CH : (c + 1) * CH, :].rearrange(
-                    "i (g h d) -> h i g d", g=KVH, h=R
-                )
+                chunk_rows = out_rows[c * CH : (c + 1) * CH, :].rearrange("i (g h d) -> h i g d", g=KVH, h=R)
                 for h in range(R):
                     nc.sync.dma_start(out=chunk_rows[h], in_=o_sb[h * CH : (h + 1) * CH, :, :])
+
+            tiles = CHUNKS * KVH
+
+            def run(stage_of_tile, n):
+                if 0 <= n < tiles:
+                    stage_of_tile(n // KVH, n % KVH)
+
+            def run_chunk(stage_of_chunk, n):
+                if n % KVH == 0 and 0 <= n < tiles:
+                    stage_of_chunk(n // KVH)
+
+            with tc.manual_schedule():
+                for i in range(tiles + 2 * KVH + 1):
+                    run(score, i)
+                    run(flip_e, i - 2)
+                    run_chunk(weigh, i - 2 * KVH + 1)
+                    run(peak, i)
+                    run_chunk(finish, i - 2 * KVH)
+                    run(quantise, i - 3)
+                    run(soften, i - 1)
+                    run(regroup, i - 2)

@@ -78,7 +78,6 @@ def tile_localgqattention_pb_kernel(tc, q_rot, k_rot, x, wv, out):
         nc.vector.tensor_copy(
             out=spread[:], in_=ident_bf[:, 0:CH].unsqueeze(1).to_broadcast([P, R, CH])
         )
-        spread_cols = spread[:].rearrange("k h i -> k (h i)")
         own_f32 = const.tile([P, P], F32)
         nc.gpsimd.memset(own_f32[:], 0.0)
         nc.gpsimd.affine_select(
@@ -98,18 +97,6 @@ def tile_localgqattention_pb_kernel(tc, q_rot, k_rot, x, wv, out):
             out=old_bias[:], in_=old_f32[:, 0:CH].unsqueeze(1).to_broadcast([P, W // CH, CH])
         )
 
-        e_tiles = []
-        for place in range(PATTERNS):
-            e_row = []
-            for g in range(KVH):
-                t_e = keep.tile([P, E_COLS], BF16, name="e_%d_%d" % (place, g))
-                if place > 0:
-                    nc.gpsimd.memset(t_e[:, 0 : place * CH], 0.0)
-                if place * CH + CH + W < E_COLS:
-                    nc.gpsimd.memset(t_e[:, place * CH + CH + W : E_COLS], 0.0)
-                e_row.append(t_e)
-            e_tiles.append(e_row)
-
         kT = keep.tile([P, KVH, T], BF16)
         qT = keep.tile([P, KVH, CHUNKS, R, CH], BF16)
         v_codes = keep.tile([P, S_PASSES, KVH * D], U32, align_bytes=64)
@@ -117,18 +104,11 @@ def tile_localgqattention_pb_kernel(tc, q_rot, k_rot, x, wv, out):
         old_scores = keep.tile([P, CHUNKS - FIRST_FULL, KVH, CH], F32)
         old_max = keep.tile([P, CHUNKS - FIRST_FULL, KVH], F32)
 
-        with tc.tile_pool(name="raw", bufs=1) as raw, tc.tile_pool(name="qraw", bufs=4) as qraw, tc.tile_pool(
+        with tc.tile_pool(name="raw", bufs=1) as raw, tc.tile_pool(
             name="stage", bufs=3
         ) as stage, tc.psum_pool(name="flip", bufs=5) as flip, tc.psum_pool(
             name="vsum", bufs=2
         ) as vsum:
-            k_raw = raw.tile([P, T // P, KVH * D], BF16)
-            nc.sync.dma_start(out=k_raw[:], in_=k_rows.rearrange("(n p) f -> p n f", p=P))
-            q_raw = []
-            for n in range(T // P):
-                t_q = qraw.tile([P, KVH * R * D], BF16, name="q_raw", tag="q_raw")
-                nc.sync.dma_start(out=t_q[:], in_=q_rows[n * P : (n + 1) * P, :])
-                q_raw.append(t_q)
             wv_raw = []
             for g in range(KVH):
                 t_wv = raw.tile([P, HID], BF16, name="wv_raw%d" % g)
@@ -142,47 +122,13 @@ def tile_localgqattention_pb_kernel(tc, q_rot, k_rot, x, wv, out):
                     in_=x_rows[run * HALF : (run + 1) * HALF, :].rearrange("(p e) k -> p (e k)", e=2),
                 )
                 x_raw.append(t_x)
-
+            k_raw = raw.tile([P, T // P, KVH * D], BF16)
+            nc.sync.dma_start(out=k_raw[:], in_=k_rows.rearrange("(n p) f -> p n f", p=P))
+            q_raw = []
             for n in range(T // P):
-                k_flip = flip.tile([P, KVH, P], BF16, tag="flip")
-                for g in range(KVH):
-                    nc.tensor.transpose(k_flip[:, g, :], k_raw[:, n, g * D : (g + 1) * D], ident_bf[:])
-                nc.vector.tensor_copy(out=kT[:, :, n * P : (n + 1) * P], in_=k_flip[:])
-            for n in range(T // P):
-                for g in range(KVH):
-                    q_flip = flip.tile([P, R, P], BF16, tag="flip")
-                    for h in range(R):
-                        first = (g * R + h) * D
-                        nc.tensor.transpose(q_flip[:, h, :], q_raw[n][:, first : first + D], ident_bf[:])
-                    copy = nc.vector.tensor_copy if g % 2 == 0 else nc.scalar.copy
-                    copy(
-                        out=qT[:, g, n * (P // CH) : (n + 1) * (P // CH), :, :],
-                        in_=q_flip[:].rearrange("d h (c i) -> d c h i", i=CH),
-                    )
-
-            per_bank = W // CH // KVH
-            for b in range((CHUNKS - FIRST_FULL) // per_bank):
-                old_ps = flip.tile([P, per_bank, KVH, CH], F32, tag="flip")
-                nc.tensor.matmul(
-                    out=old_ps[:].rearrange("p c g j -> p (c g j)"),
-                    lhsT=spread_cols,
-                    rhs=old_bias[:].rearrange("k n j -> k (n j)"),
-                    start=True,
-                    stop=False,
-                )
-                for i in range(per_bank):
-                    c = FIRST_FULL + b * per_bank + i
-                    for g in range(KVH):
-                        nc.tensor.matmul(
-                            out=old_ps[:, i, g, :],
-                            lhsT=qT[:, g, c].rearrange("d h i -> d (h i)"),
-                            rhs=kT[:, g, c * CH - W : c * CH - W + CH],
-                            start=False,
-                            stop=(i == per_bank - 1 and g == KVH - 1),
-                        )
-                rows = slice(b * per_bank, (b + 1) * per_bank)
-                nc.vector.tensor_reduce(out=old_max[:, rows, :], in_=old_ps[:], axis=AXIS_X, op=ALU.max)
-                nc.scalar.copy(out=old_scores[:, rows], in_=old_ps[:])
+                t_q = raw.tile([P, KVH * R * D], BF16, name="q_raw%d" % n)
+                nc.sync.dma_start(out=t_q[:], in_=q_rows[n * P : (n + 1) * P, :])
+                q_raw.append(t_q)
 
             w_codes = raw.tile([P, KVH, X_PASSES * D], U32, align_bytes=64)
             w_scales = raw.tile([P, KVH, X_PASSES * D], U8, align_bytes=64)
@@ -225,13 +171,66 @@ def tile_localgqattention_pb_kernel(tc, q_rot, k_rot, x, wv, out):
                     in_=v_grouped[:, sp].rearrange("p g d j -> p (g d j)"),
                 )
 
-        with tc.tile_pool(name="work", bufs=3, reuse_waits="tile") as work, tc.tile_pool(
-            name="packed", bufs=2 * KVH, reuse_waits="tile"
-        ) as packed, tc.tile_pool(name="stat", bufs=4, reuse_waits="tile") as stat, tc.psum_pool(
-            name="score", bufs=4, reuse_waits="tile"
-        ) as score_pool, tc.psum_pool(name="eflip", bufs=2, reuse_waits="tile") as eflip, tc.psum_pool(
-            name="osum", bufs=2, reuse_waits="tile"
-        ) as osum:
+            for n in range(T // P):
+                k_flip = flip.tile([P, KVH, P], BF16, tag="flip")
+                for g in range(KVH):
+                    nc.tensor.transpose(k_flip[:, g, :], k_raw[:, n, g * D : (g + 1) * D], ident_bf[:])
+                nc.vector.tensor_copy(out=kT[:, :, n * P : (n + 1) * P], in_=k_flip[:])
+            for n in range(T // P):
+                for g in range(KVH):
+                    q_flip = flip.tile([P, R, P], BF16, tag="flip")
+                    for h in range(R):
+                        first = (g * R + h) * D
+                        nc.tensor.transpose(q_flip[:, h, :], q_raw[n][:, first : first + D], ident_bf[:])
+                    nc.vector.tensor_copy(
+                        out=qT[:, g, n * (P // CH) : (n + 1) * (P // CH), :, :],
+                        in_=q_flip[:].rearrange("d h (c i) -> d c h i", i=CH),
+                    )
+
+            per_bank = W // CH // KVH
+            for b in range((CHUNKS - FIRST_FULL) // per_bank):
+                old_ps = flip.tile([P, per_bank, KVH, CH], F32, tag="flip")
+                nc.tensor.matmul(
+                    out=old_ps[:].rearrange("p c g j -> p (c g j)"),
+                    lhsT=spread[:].rearrange("k h i -> k (h i)"),
+                    rhs=old_bias[:].rearrange("k n j -> k (n j)"),
+                    start=True,
+                    stop=False,
+                )
+                for i in range(per_bank):
+                    c = FIRST_FULL + b * per_bank + i
+                    for g in range(KVH):
+                        nc.tensor.matmul(
+                            out=old_ps[:, i, g, :],
+                            lhsT=qT[:, g, c].rearrange("d h i -> d (h i)"),
+                            rhs=kT[:, g, c * CH - W : c * CH - W + CH],
+                            start=False,
+                            stop=(i == per_bank - 1 and g == KVH - 1),
+                        )
+                rows = slice(b * per_bank, (b + 1) * per_bank)
+                nc.vector.tensor_reduce(out=old_max[:, rows, :], in_=old_ps[:], axis=AXIS_X, op=ALU.max)
+                nc.scalar.copy(out=old_scores[:, rows], in_=old_ps[:])
+
+        with tc.tile_pool(name="etiles", bufs=1, reuse_waits="tile") as etiles, tc.tile_pool(
+            name="work", bufs=4, reuse_waits="tile"
+        ) as work, tc.tile_pool(name="packed", bufs=2 * KVH, reuse_waits="tile") as packed, tc.tile_pool(
+            name="stat", bufs=5, reuse_waits="tile"
+        ) as stat, tc.psum_pool(name="score", bufs=KVH, reuse_waits="tile") as score_pool, tc.psum_pool(
+            name="eflip", bufs=3, reuse_waits="tile"
+        ) as eflip, tc.psum_pool(name="osum", bufs=1, reuse_waits="tile") as osum:
+            e_tiles = []
+            for place in range(PATTERNS):
+                e_row = []
+                for g in range(KVH):
+                    t_e = etiles.tile([P, E_COLS], BF16, name="e_%d_%d" % (place, g))
+                    if place > 0:
+                        nc.gpsimd.memset(t_e[:, 0 : place * CH], 0.0)
+                    if place * CH + CH + W < E_COLS:
+                        nc.gpsimd.memset(t_e[:, place * CH + CH + W : E_COLS], 0.0)
+                    e_row.append(t_e)
+                e_tiles.append(e_row)
+
+            spread_cols = spread[:].rearrange("k h i -> k (h i)")
             of_chunk = {}
             of_tile = {}
 
@@ -256,20 +255,21 @@ def tile_localgqattention_pb_kernel(tc, q_rot, k_rot, x, wv, out):
 
             def peak(c, g):
                 new = min((c + 1) * CH, W)
+                nc.vector.tensor_reduce(
+                    out=of_chunk[c]["top"][:, g : g + 1], in_=of_tile[c, g]["scores"][:, 0:new],
+                    axis=AXIS_X, op=ALU.max,
+                )
+
+            def set_shift(c, g):
                 top = of_chunk[c]["top"][:, g : g + 1]
                 shift = of_chunk[c]["shift"][:, g : g + 1]
-                nc.vector.tensor_reduce(
-                    out=top, in_=of_tile[c, g]["scores"][:, 0:new], axis=AXIS_X, op=ALU.max
-                )
                 if c >= FIRST_FULL:
-                    nc.gpsimd.tensor_scalar(
-                        out=shift, in0=top, scalar1=old_max[:, c - FIRST_FULL, g : g + 1],
-                        scalar2=-SCALE, op0=ALU.max, op1=ALU.mult,
+                    nc.vector.tensor_scalar(
+                        out=shift, in0=top, scalar1=old_max[:, c - FIRST_FULL, g : g + 1], scalar2=-SCALE,
+                        op0=ALU.max, op1=ALU.mult,
                     )
                 else:
-                    nc.gpsimd.tensor_scalar(
-                        out=shift, in0=top, scalar1=-SCALE, scalar2=None, op0=ALU.mult
-                    )
+                    nc.vector.tensor_scalar(out=shift, in0=top, scalar1=-SCALE, scalar2=None, op0=ALU.mult)
 
             def soften(c, g):
                 new = min((c + 1) * CH, W)
@@ -286,12 +286,14 @@ def tile_localgqattention_pb_kernel(tc, q_rot, k_rot, x, wv, out):
                         out=e[:, end - new - CH : end - new], in_=old_scores[:, c - FIRST_FULL, g, :],
                         func=ACT.Exp, bias=shift, scale=SCALE, accum_out=sums[:, 1, g : g + 1],
                     )
-                    if g == KVH - 1:
-                        total = stat.tile([P, KVH], F32, name="total")
-                        nc.gpsimd.tensor_tensor(out=total[:], in0=sums[:, 0, :], in1=sums[:, 1, :], op=ALU.add)
-                        of_chunk[c]["total"] = total[:]
-                elif g == KVH - 1:
-                    of_chunk[c]["total"] = sums[:, 0, :]
+
+            def invert(c):
+                sums = of_chunk[c]["sums"]
+                inverse = stat.tile([P, KVH], F32)
+                if c >= FIRST_FULL:
+                    nc.vector.tensor_tensor(out=sums[:, 0, :], in0=sums[:, 0, :], in1=sums[:, 1, :], op=ALU.add)
+                nc.vector.reciprocal(out=inverse[:], in_=sums[:, 0, :])
+                of_chunk[c]["inverse"] = inverse
 
             def flip_e(c, g):
                 last_run = c // PATTERNS
@@ -330,8 +332,6 @@ def tile_localgqattention_pb_kernel(tc, q_rot, k_rot, x, wv, out):
 
             def weigh(c):
                 passes = c // PATTERNS // 2 + 1
-                inverse = stat.tile([P, KVH], F32)
-                nc.vector.reciprocal(out=inverse[:], in_=of_chunk[c]["total"])
                 o_sum = osum.tile([P, KVH, D], F32)
                 for g in range(KVH):
                     for sp in range(passes):
@@ -344,7 +344,6 @@ def tile_localgqattention_pb_kernel(tc, q_rot, k_rot, x, wv, out):
                             start=(sp == 0),
                             stop=(sp == passes - 1),
                         )
-                of_chunk[c]["inverse"] = inverse
                 of_chunk[c]["o_sum"] = o_sum
 
             def finish(c):
@@ -368,12 +367,14 @@ def tile_localgqattention_pb_kernel(tc, q_rot, k_rot, x, wv, out):
                     stage_of_chunk(n // KVH)
 
             with tc.manual_schedule():
-                for i in range(tiles + 2 * KVH + 1):
+                for i in range(tiles + 3 * KVH + 1):
                     run(score, i)
-                    run(flip_e, i - 2)
-                    run_chunk(weigh, i - 2 * KVH + 1)
-                    run(peak, i)
-                    run_chunk(finish, i - 2 * KVH)
-                    run(quantise, i - 3)
-                    run(soften, i - 1)
-                    run(regroup, i - 2)
+                    run(flip_e, i - 4)
+                    run_chunk(weigh, i - (KVH - 1) - 6 - 2)
+                    run(peak, i - 1)
+                    run(quantise, i - 6)
+                    run(set_shift, i - 1)
+                    run_chunk(invert, i - (KVH - 1) - 2 - 2)
+                    run_chunk(finish, i - (KVH - 1) - 6 - 3)
+                    run(soften, i - 2)
+                    run(regroup, i - 5)

@@ -6,16 +6,19 @@ from concourse.masks import make_identity
 F32 = mybir.dt.float32
 BF16 = mybir.dt.bfloat16
 U32 = mybir.dt.uint32
+I32 = mybir.dt.int32
 U8 = mybir.dt.uint8
 FP8X4 = mybir.dt.float8_e4m3fn_x4
 ALU = mybir.AluOpType
 ACT = mybir.ActivationFunctionType
 AXIS_X = mybir.AxisListType.X
+AXIS_XY = mybir.AxisListType.XY
 
 P = 128
 PACK = 4
 K_PASS = P * PACK
-HALF = K_PASS // 2
+QUAD = 32
+BLK = 8
 
 T = 1024
 HID = 2048
@@ -25,34 +28,17 @@ D = 128
 W = 512
 CH = P // R
 CHUNKS = T // CH
-FIRST_FULL = W // CH
+FULL = W // CH
+DIAG = 12
 X_PASSES = HID // K_PASS
 S_PASSES = T // K_PASS
-E_COLS = 3 * HALF
-PATTERNS = HALF // CH
+HC = CH // 2
+HQ = 2 * QUAD
+PAIRS = CHUNKS * KVH // 2
 SCALE = 1.0 / math.sqrt(D)
 MASKED = -1.0e30
 
 FLOPS = 2 * T * HID * KVH * D + 2 * 2 * (KVH * R) * D * (W * W + W * 2 * W)
-
-
-def quantise_k_last(nc, stage, bank_pool, ident32, rows32, codes, scales):
-    grouped = stage.tile([P, X_PASSES * P * PACK], BF16, align_bytes=64, tag="grouped")
-    grouped32 = grouped[:].bitcast(F32).rearrange("p (c r u) -> p c r u", c=X_PASSES, u=2)
-    for pair in range(X_PASSES // 2):
-        flipped = bank_pool.tile([P, 2 * 2, P], F32, tag="flip")
-        for i in range(2 * 2):
-            first = (2 * 2 * pair + i) * P
-            nc.tensor.transpose(flipped[:, i, :], rows32[:, first : first + P], ident32[:])
-        nc.scalar.copy(
-            out=grouped32[:, 2 * pair : 2 * pair + 2],
-            in_=flipped[:].rearrange("p (c u) r -> p c r u", u=2),
-        )
-    nc.vector.quantize_mx(
-        out=codes.bitcast(FP8X4),
-        scales=scales,
-        in_=grouped[:],
-    )
 
 
 def tile_localgqattention_pb_kernel(tc, q_rot, k_rot, x, wv, out):
@@ -62,7 +48,17 @@ def tile_localgqattention_pb_kernel(tc, q_rot, k_rot, x, wv, out):
     x_rows = x.rearrange("b t k -> (b t) k")
     out_rows = out.rearrange("b t f -> (b t) f")
 
-    with tc.tile_pool(name="const", bufs=1) as const, tc.tile_pool(name="keep", bufs=1) as keep:
+    with tc.tile_pool(name="const", bufs=1) as const, tc.tile_pool(name="keep", bufs=1) as keep, tc.tile_pool(
+        name="rows", bufs=8
+    ) as rows_pool, tc.tile_pool(name="qraw", bufs=4) as qraw_pool, tc.tile_pool(
+        name="stage", bufs=3
+    ) as stage, tc.tile_pool(name="xq", bufs=6) as xq_pool, tc.tile_pool(
+        name="packed", bufs=18, reuse_waits="tile"
+    ) as packed, tc.tile_pool(name="work", bufs=3, reuse_waits="tile") as work, tc.tile_pool(
+        name="stat", bufs=16, reuse_waits="tile"
+    ) as stat, tc.psum_pool(name="score", bufs=4, reuse_waits="tile") as score_pool, tc.psum_pool(
+        name="flip", bufs=3, reuse_waits="tile"
+    ) as flip, tc.psum_pool(name="osum", bufs=1, reuse_waits="tile") as osum:
         warm = const.tile([P, 1], F32)
         nc.vector.memset(warm[:], 0.0)
         nc.scalar.activation(out=warm[:], in_=warm[:], func=ACT.Exp)
@@ -71,310 +67,537 @@ def tile_localgqattention_pb_kernel(tc, q_rot, k_rot, x, wv, out):
         make_identity(nc, ident_bf[:])
         ident32 = const.tile([P, P], F32)
         make_identity(nc, ident32[:])
-        zeros = const.tile([P, 2 * P], BF16)
-        nc.vector.memset(zeros[:], 0.0)
 
         spread = const.tile([P, R, CH], BF16)
-        nc.vector.tensor_copy(
-            out=spread[:], in_=ident_bf[:, 0:CH].unsqueeze(1).to_broadcast([P, R, CH])
-        )
+        nc.vector.tensor_copy(out=spread[:], in_=ident_bf[:, 0:CH].unsqueeze(1).to_broadcast([P, R, CH]))
         own_f32 = const.tile([P, P], F32)
         nc.gpsimd.memset(own_f32[:], 0.0)
         nc.gpsimd.affine_select(
             out=own_f32[:], in_=own_f32[:], compare_op=ALU.is_ge, fill=MASKED,
             base=0, pattern=[[-1, P]], channel_multiplier=1,
         )
-        own_bias = const.tile([P, CH], BF16)
-        nc.vector.tensor_copy(out=own_bias[:], in_=own_f32[:, 0:CH])
+        own_bias = const.tile([P, 2, HC], BF16)
+        nc.vector.tensor_copy(
+            out=own_bias[:].rearrange("k u (p e) -> k u p e", e=2),
+            in_=own_f32[:, 0:CH].rearrange("k (p u e) -> k u p e", u=2, e=2),
+        )
         old_f32 = const.tile([P, P], F32)
         nc.gpsimd.memset(old_f32[:], 0.0)
         nc.gpsimd.affine_select(
             out=old_f32[:], in_=old_f32[:], compare_op=ALU.is_ge, fill=MASKED,
             base=0, pattern=[[1, P]], channel_multiplier=-1,
         )
-        old_bias = const.tile([P, W // CH, CH], BF16)
+        old_one = const.tile([P, 2, HC], BF16)
         nc.vector.tensor_copy(
-            out=old_bias[:], in_=old_f32[:, 0:CH].unsqueeze(1).to_broadcast([P, W // CH, CH])
+            out=old_one[:].rearrange("k u (p e) -> k u p e", e=2),
+            in_=old_f32[:, 0:CH].rearrange("k (p u e) -> k u p e", u=2, e=2),
         )
+        old_bias = const.tile([P, FULL, CH], BF16)
+        nc.vector.tensor_copy(
+            out=old_bias[:],
+            in_=old_one[:].rearrange("k u c -> k (u c)").unsqueeze(1).to_broadcast([P, FULL, CH]),
+        )
+        spread_cols = spread[:].rearrange("k h i -> k (h i)")
 
-        kT = keep.tile([P, KVH, T], BF16)
+        kT = keep.tile([P, KVH, S_PASSES, 2, 2 * P], BF16)
         qT = keep.tile([P, KVH, CHUNKS, R, CH], BF16)
+        k_raw = keep.tile([P, T // P, KVH * D], BF16)
+        w_codes = keep.tile([P, KVH, X_PASSES * D], U32, align_bytes=64)
+        w_scales = keep.tile([P, KVH, X_PASSES * D], U8, align_bytes=64)
+        v_grouped = keep.tile([P, KVH, D, PACK], BF16, align_bytes=64)
         v_codes = keep.tile([P, S_PASSES, KVH * D], U32, align_bytes=64)
         v_scales = keep.tile([P, S_PASSES, KVH * D], U8, align_bytes=64)
-        old_scores = keep.tile([P, CHUNKS - FIRST_FULL, KVH, CH], F32)
-        old_max = keep.tile([P, CHUNKS - FIRST_FULL, KVH], F32)
+        diag_codes = []
+        diag_scales = []
+        roll_codes = []
+        roll_scales = []
+        e_diag = []
+        e_old = []
+        for n in range(4):
+            t_dc = keep.tile([P, KVH * D], U32, align_bytes=64, name="diag_codes%d" % n)
+            t_ds = keep.tile([P, KVH * D], U8, align_bytes=64, name="diag_scales%d" % n)
+            t_rc = keep.tile([P, KVH * D], U32, align_bytes=64, name="roll_codes%d" % n)
+            t_rs = keep.tile([P, KVH * D], U8, align_bytes=64, name="roll_scales%d" % n)
+            t_ed = keep.tile([P, 3 * 2 * KVH * HQ], BF16, name="e_diag%d" % n)
+            t_eo = keep.tile([P, 2 * KVH * HQ], BF16, name="e_old%d" % n)
+            nc.gpsimd.memset(t_ed[:], 0.0)
+            diag_codes.append(t_dc)
+            diag_scales.append(t_ds)
+            roll_codes.append(t_rc)
+            roll_scales.append(t_rs)
+            e_diag.append(t_ed)
+            e_old.append(t_eo)
+        e_row = []
+        for n in range(6):
+            t_er = keep.tile([P, 4 * P], BF16, name="e_row%d" % n)
+            e_row.append(t_er)
+        nc.gpsimd.memset(v_scales[:].rearrange("p s f -> p (s f)").bitcast(U32), 0)
+        for n in range(4):
+            nc.gpsimd.memset(diag_codes[n][:], 0)
+            nc.gpsimd.memset(diag_scales[n][:].bitcast(U32), 0)
+        for n in range(6):
+            nc.gpsimd.memset(e_row[n][:], 0.0)
+        for n in range(4):
+            nc.gpsimd.memset(e_old[n][:], 0.0)
 
-        with tc.tile_pool(name="raw", bufs=1) as raw, tc.tile_pool(
-            name="stage", bufs=3
-        ) as stage, tc.psum_pool(name="flip", bufs=5) as flip, tc.psum_pool(
-            name="vsum", bufs=2
-        ) as vsum:
-            wv_raw = []
-            for g in range(KVH):
-                t_wv = raw.tile([P, HID], BF16, name="wv_raw%d" % g)
-                nc.sync.dma_start(out=t_wv[:], in_=wv[g * D : (g + 1) * D, :])
-                wv_raw.append(t_wv)
-            x_raw = []
-            for run in range(T // HALF):
-                t_x = raw.tile([P, 2 * HID], BF16, name="x_raw%d" % run)
+        def load_rows(in_):
+            t_rows = rows_pool.tile([P, HID], BF16, name="rows")
+            nc.sync.dma_start(out=t_rows[:], in_=in_)
+            return t_rows
+
+        def load_q(n):
+            t_q = qraw_pool.tile([P, KVH * R * D], BF16, name="q_raw")
+            nc.sync.dma_start(out=t_q[:], in_=q_rows[n * P : (n + 1) * P, :])
+            q_raw[n] = t_q
+
+        def turn_rows(op, half):
+            bank = flip.tile([P, 4, P], F32, tag="flip")
+            words = op["rows"][:].bitcast(F32)
+            for n in range(4):
+                first = (4 * half + n) * P
+                nc.tensor.transpose(bank[:, n, :], words[:, first : first + P], ident32[:])
+            op["bank"] = bank
+
+        def lay_rows(op, half):
+            if half == 0:
+                grouped = stage.tile([P, X_PASSES * P * PACK], BF16, align_bytes=64)
+                op["grouped"] = grouped
+            grouped32 = op["grouped"][:].bitcast(F32).rearrange("p (c r u) -> p c r u", c=X_PASSES, u=2)
+            nc.scalar.copy(
+                out=grouped32[:, 2 * half : 2 * half + 2],
+                in_=op["bank"][:].rearrange("p (c u) r -> p c r u", u=2),
+            )
+
+        def quantise_rows(op):
+            nc.vector.quantize_mx(out=op["codes"].bitcast(FP8X4), scales=op["scales"], in_=op["grouped"][:])
+
+        def project(sp, g):
+            bank = flip.tile([P, PACK, D], F32, tag="flip")
+            for t in range(PACK):
+                for kp in range(X_PASSES):
+                    cols = slice(kp * P, (kp + 1) * P)
+                    nc.tensor.matmul_mx(
+                        out=bank[:, t, :],
+                        lhsT=x_ops[PACK * sp + t]["codes"][:, cols].bitcast(FP8X4),
+                        lhsT_scale=x_ops[PACK * sp + t]["scales"][:, cols],
+                        rhs=w_codes[:, g, cols].bitcast(FP8X4),
+                        rhs_scale=w_scales[:, g, cols],
+                        start=(kp == 0),
+                        stop=(kp == X_PASSES - 1),
+                    )
+            v_bank[g] = bank
+
+        def lay_v(g):
+            nc.scalar.copy(out=v_grouped[:, g, :, :], in_=v_bank[g][:].rearrange("p t d -> p d t"))
+
+        def quantise_v(sp):
+            nc.vector.quantize_mx(
+                out=v_codes[:, sp, :].bitcast(FP8X4),
+                scales=v_scales[:, sp, :],
+                in_=v_grouped[:].rearrange("p g d t -> p (g d t)"),
+            )
+
+        def move(dst_codes, dst_scales, dst_block, sp, block, blocks, cols):
+            nc.sync.dma_start(
+                out=dst_codes[dst_block * BLK : (dst_block + blocks) * BLK, cols].bitcast(I32),
+                in_=v_codes[block * BLK : (block + blocks) * BLK, sp, cols].bitcast(I32),
+            )
+            for quad in range(block // 4, (block + blocks - 1) // 4 + 1):
+                low = max(block, 4 * quad)
+                count = min(block + blocks, 4 * quad + 4) - low
+                there = low + dst_block - block
+                a = there // 4 * QUAD + there % 4
+                b = quad * QUAD + low % 4
                 nc.sync.dma_start(
-                    out=t_x[:],
-                    in_=x_rows[run * HALF : (run + 1) * HALF, :].rearrange("(p e) k -> p (e k)", e=2),
+                    out=dst_scales[a : a + count, cols].bitcast(I32),
+                    in_=v_scales[b : b + count, sp, cols].bitcast(I32),
                 )
-                x_raw.append(t_x)
-            k_raw = raw.tile([P, T // P, KVH * D], BF16)
-            nc.sync.dma_start(out=k_raw[:], in_=k_rows.rearrange("(n p) f -> p n f", p=P))
-            q_raw = []
-            for n in range(T // P):
-                t_q = raw.tile([P, KVH * R * D], BF16, name="q_raw%d" % n)
-                nc.sync.dma_start(out=t_q[:], in_=q_rows[n * P : (n + 1) * P, :])
-                q_raw.append(t_q)
 
-            w_codes = raw.tile([P, KVH, X_PASSES * D], U32, align_bytes=64)
-            w_scales = raw.tile([P, KVH, X_PASSES * D], U8, align_bytes=64)
+        def make_diag():
+            for quad in range(4):
+                for g in range(KVH):
+                    move(diag_codes[quad], diag_scales[quad], 4 * g, 0, 4 * quad, 4, slice(g * D, (g + 1) * D))
+
+        def make_roll():
+            for n in range(4):
+                nc.sync.dma_start(out=roll_codes[n][:].bitcast(I32), in_=v_codes[:, 0, :].bitcast(I32))
+                nc.sync.dma_start(out=roll_scales[n][:].bitcast(I32), in_=v_scales[:, 0, :].bitcast(I32))
+
+        def advance_roll(j):
+            first = max(j - 3, 0)
+            move(roll_codes[j % 4], roll_scales[j % 4], first, 1, first, j + 1 - first, slice(0, KVH * D))
+
+        def turn_k(n):
+            bank = flip.tile([P, KVH, P], BF16, tag="flip")
             for g in range(KVH):
-                quantise_k_last(
-                    nc, stage, flip, ident32, wv_raw[g][:].bitcast(F32),
-                    w_codes[:, g, :], w_scales[:, g, :],
-                )
-            x_codes = raw.tile([P, T // P, X_PASSES * P], U32, align_bytes=64)
-            x_scales = raw.tile([P, T // P, X_PASSES * P], U8, align_bytes=64)
-            for run in range(T // HALF):
-                for odd in range(2):
-                    quantise_k_last(
-                        nc, stage, flip, ident32,
-                        x_raw[run][:].bitcast(F32)[:, odd * (HID // 2) : (odd + 1) * (HID // 2)],
-                        x_codes[:, 2 * run + odd, :], x_scales[:, 2 * run + odd, :],
-                    )
-            v_grouped = raw.tile([P, S_PASSES, KVH, D, PACK], BF16, align_bytes=64)
-            for sp in range(S_PASSES):
+                nc.tensor.transpose(bank[:, g, :], k_raw[:, n, g * D : (g + 1) * D], ident_bf[:])
+            return bank
+
+        def lay_k(copy, n, bank):
+            copy(
+                out=kT[:].rearrange("d g s u c -> d (g s u c)").bitcast(F32).rearrange(
+                    "d (g s u c) -> d g s u c", g=KVH, s=S_PASSES, u=2
+                )[:, :, n // 4, :, (n % 4) * QUAD : (n % 4 + 1) * QUAD],
+                in_=bank[:].rearrange("d g t -> d (g t)").bitcast(F32).rearrange(
+                    "d (g p u) -> d g u p", g=KVH, u=2
+                ),
+            )
+
+        def turn_q(n, g):
+            bank = flip.tile([P, R, P], BF16, tag="flip")
+            for h in range(R):
+                first = (g * R + h) * D
+                nc.tensor.transpose(bank[:, h, :], q_raw[n][:, first : first + D], ident_bf[:])
+            return bank
+
+        def lay_q(copy, n, g, bank):
+            copy(
+                out=qT[:, g, n * (P // CH) : (n + 1) * (P // CH), :, :],
+                in_=bank[:].rearrange("d h (c i) -> d c h i", i=CH),
+            )
+
+        def score_old(quad):
+            bank = flip.tile([P, 4, KVH, CH], F32, tag="flip")
+            nc.tensor.matmul(
+                out=bank[:].rearrange("p c g j -> p (c g j)"), lhsT=spread_cols,
+                rhs=old_bias[:].rearrange("k n j -> k (n j)"), start=True, stop=False,
+            )
+            for b in range(4):
+                j = 4 * quad + b
                 for g in range(KVH):
-                    v_sum = vsum.tile([P, PACK, D], F32)
-                    for j in range(PACK):
-                        for kp in range(X_PASSES):
-                            cols = slice(kp * P, (kp + 1) * P)
-                            nc.tensor.matmul_mx(
-                                out=v_sum[:, j, :],
-                                lhsT=x_codes[:, PACK * sp + j, cols].bitcast(FP8X4),
-                                lhsT_scale=x_scales[:, PACK * sp + j, cols],
-                                rhs=w_codes[:, g, cols].bitcast(FP8X4),
-                                rhs_scale=w_scales[:, g, cols],
-                                start=(kp == 0),
-                                stop=(kp == X_PASSES - 1),
-                            )
-                    nc.scalar.copy(
-                        out=v_grouped[:, sp, g, :, :], in_=v_sum[:].rearrange("p j d -> p d j")
+                    nc.tensor.matmul(
+                        out=bank[:, b, g, :].rearrange("p (u c) -> p u c", u=2),
+                        lhsT=qT[:, g, FULL + j].rearrange("d h i -> d (h i)"),
+                        rhs=kT[:, g, 0, :, j * HC : (j + 1) * HC],
+                        start=False,
+                        stop=(b == 3 and g == KVH - 1),
                     )
-                nc.vector.quantize_mx(
-                    out=v_codes[:, sp, :].bitcast(FP8X4),
-                    scales=v_scales[:, sp, :],
-                    in_=v_grouped[:, sp].rearrange("p g d j -> p (g d j)"),
-                )
+            old_max = stat.tile([P, 4, KVH], F32, name="old_max")
+            nc.vector.tensor_reduce(out=old_max[:], in_=bank[:], axis=AXIS_X, op=ALU.max)
+            neg_old = stat.tile([P, 4, KVH], F32, name="neg_old")
+            old_scores = work.tile([P, 4, KVH, CH], F32, name="old_scores")
+            nc.scalar.copy(out=old_scores[:], in_=bank[:])
+            of_quad[quad] = {"max": old_max, "neg": neg_old, "scores": old_scores}
 
-            for n in range(T // P):
-                k_flip = flip.tile([P, KVH, P], BF16, tag="flip")
-                for g in range(KVH):
-                    nc.tensor.transpose(k_flip[:, g, :], k_raw[:, n, g * D : (g + 1) * D], ident_bf[:])
-                nc.vector.tensor_copy(out=kT[:, :, n * P : (n + 1) * P], in_=k_flip[:])
-            for n in range(T // P):
-                for g in range(KVH):
-                    q_flip = flip.tile([P, R, P], BF16, tag="flip")
-                    for h in range(R):
-                        first = (g * R + h) * D
-                        nc.tensor.transpose(q_flip[:, h, :], q_raw[n][:, first : first + D], ident_bf[:])
-                    nc.vector.tensor_copy(
-                        out=qT[:, g, n * (P // CH) : (n + 1) * (P // CH), :, :],
-                        in_=q_flip[:].rearrange("d h (c i) -> d c h i", i=CH),
-                    )
+        def negate_old(quad):
+            nc.vector.tensor_scalar(
+                out=of_quad[quad]["neg"][:], in0=of_quad[quad]["max"][:], scalar1=-SCALE, scalar2=None, op0=ALU.mult
+            )
 
-            per_bank = W // CH // KVH
-            for b in range((CHUNKS - FIRST_FULL) // per_bank):
-                old_ps = flip.tile([P, per_bank, KVH, CH], F32, tag="flip")
-                nc.tensor.matmul(
-                    out=old_ps[:].rearrange("p c g j -> p (c g j)"),
-                    lhsT=spread[:].rearrange("k h i -> k (h i)"),
-                    rhs=old_bias[:].rearrange("k n j -> k (n j)"),
-                    start=True,
-                    stop=False,
-                )
-                for i in range(per_bank):
-                    c = FIRST_FULL + b * per_bank + i
-                    for g in range(KVH):
-                        nc.tensor.matmul(
-                            out=old_ps[:, i, g, :],
-                            lhsT=qT[:, g, c].rearrange("d h i -> d (h i)"),
-                            rhs=kT[:, g, c * CH - W : c * CH - W + CH],
-                            start=False,
-                            stop=(i == per_bank - 1 and g == KVH - 1),
-                        )
-                rows = slice(b * per_bank, (b + 1) * per_bank)
-                nc.vector.tensor_reduce(out=old_max[:, rows, :], in_=old_ps[:], axis=AXIS_X, op=ALU.max)
-                nc.scalar.copy(out=old_scores[:, rows], in_=old_ps[:])
-
-        with tc.tile_pool(name="etiles", bufs=1, reuse_waits="tile") as etiles, tc.tile_pool(
-            name="work", bufs=4, reuse_waits="tile"
-        ) as work, tc.tile_pool(name="packed", bufs=2 * KVH, reuse_waits="tile") as packed, tc.tile_pool(
-            name="stat", bufs=5, reuse_waits="tile"
-        ) as stat, tc.psum_pool(name="score", bufs=KVH, reuse_waits="tile") as score_pool, tc.psum_pool(
-            name="eflip", bufs=3, reuse_waits="tile"
-        ) as eflip, tc.psum_pool(name="osum", bufs=1, reuse_waits="tile") as osum:
-            e_tiles = []
-            for place in range(PATTERNS):
-                e_row = []
-                for g in range(KVH):
-                    t_e = etiles.tile([P, E_COLS], BF16, name="e_%d_%d" % (place, g))
-                    if place > 0:
-                        nc.gpsimd.memset(t_e[:, 0 : place * CH], 0.0)
-                    if place * CH + CH + W < E_COLS:
-                        nc.gpsimd.memset(t_e[:, place * CH + CH + W : E_COLS], 0.0)
-                    e_row.append(t_e)
-                e_tiles.append(e_row)
-
-            spread_cols = spread[:].rearrange("k h i -> k (h i)")
-            of_chunk = {}
-            of_tile = {}
-
-            def score(c, g):
-                if g == 0:
-                    of_chunk[c] = {
-                        "top": stat.tile([P, KVH], F32, name="top"),
-                        "shift": stat.tile([P, KVH], F32, name="shift"),
-                        "sums": stat.tile([P, 2, KVH], F32, name="sums"),
-                    }
-                new = min((c + 1) * CH, W)
-                scores = score_pool.tile([P, W], F32)
-                nc.tensor.matmul(
-                    out=scores[:, 0:new], lhsT=qT[:, g, c].rearrange("d h i -> d (h i)"),
-                    rhs=kT[:, g, (c + 1) * CH - new : (c + 1) * CH], start=True, stop=False,
-                )
-                nc.tensor.matmul(
-                    out=scores[:, new - CH : new], lhsT=spread_cols, rhs=own_bias[:],
-                    start=False, stop=True,
-                )
-                of_tile[c, g] = {"scores": scores}
-
-            def peak(c, g):
-                new = min((c + 1) * CH, W)
-                nc.vector.tensor_reduce(
-                    out=of_chunk[c]["top"][:, g : g + 1], in_=of_tile[c, g]["scores"][:, 0:new],
-                    axis=AXIS_X, op=ALU.max,
-                )
-
-            def set_shift(c, g):
-                top = of_chunk[c]["top"][:, g : g + 1]
-                shift = of_chunk[c]["shift"][:, g : g + 1]
-                if c >= FIRST_FULL:
-                    nc.vector.tensor_scalar(
-                        out=shift, in0=top, scalar1=old_max[:, c - FIRST_FULL, g : g + 1], scalar2=-SCALE,
-                        op0=ALU.max, op1=ALU.mult,
-                    )
+        def score(i):
+            c, half = i // 2, i % 2
+            if half == 0:
+                of_chunk[c] = {
+                    "top": stat.tile([P, KVH], F32, name="top"),
+                    "shift": stat.tile([P, KVH], F32, name="shift"),
+                    "sums": stat.tile([P, 2, KVH], F32, name="sums"),
+                    "units": [],
+                    "jobs": [],
+                }
+            banks = []
+            if c < FULL // 2:
+                both = score_pool.tile([P, 2, 2, P], F32, tag="score")
+                of_both[i] = both
+            for t in range(2):
+                g = 2 * half + t
+                if c < FULL // 2:
+                    bank = both[:, t]
                 else:
-                    nc.vector.tensor_scalar(out=shift, in0=top, scalar1=-SCALE, scalar2=None, op0=ALU.mult)
-
-            def soften(c, g):
-                new = min((c + 1) * CH, W)
-                end = (c % PATTERNS) * CH + CH + W
-                shift = of_chunk[c]["shift"][:, g : g + 1]
-                sums = of_chunk[c]["sums"]
-                e = e_tiles[c % PATTERNS][g]
-                nc.scalar.activation(
-                    out=e[:, end - new : end], in_=of_tile[c, g]["scores"][:, 0:new], func=ACT.Exp,
-                    bias=shift, scale=SCALE, accum_out=sums[:, 0, g : g + 1],
+                    own = score_pool.tile([P, 2, 2 * P], F32, tag="score")
+                    bank = own[:]
+                lhsT = qT[:, g, c].rearrange("d h i -> d (h i)")
+                j = c % FULL
+                live = (j + 1) * HC
+                if c >= FULL and live < 2 * P:
+                    nc.tensor.matmul(
+                        out=bank[:, :, live : 2 * P], lhsT=lhsT, rhs=kT[:, g, 0, :, live : 2 * P],
+                        start=True, stop=True,
+                    )
+                nc.tensor.matmul(
+                    out=bank[:, :, 0:live], lhsT=lhsT, rhs=kT[:, g, c // FULL, :, 0:live], start=True, stop=False
                 )
-                if c >= FIRST_FULL:
-                    nc.scalar.activation(
-                        out=e[:, end - new - CH : end - new], in_=old_scores[:, c - FIRST_FULL, g, :],
-                        func=ACT.Exp, bias=shift, scale=SCALE, accum_out=sums[:, 1, g : g + 1],
+                nc.tensor.matmul(
+                    out=bank[:, :, live - HC : live], lhsT=spread_cols, rhs=own_bias[:], start=False, stop=True
+                )
+                banks.append(bank)
+            of_pair[i] = banks
+
+        def peak(i):
+            c, half = i // 2, i % 2
+            live = (c % FULL + 1) * HC if c < FULL else 2 * P
+            top = of_chunk[c]["top"]
+            if c < FULL // 2:
+                nc.vector.tensor_reduce(
+                    out=top[:, 2 * half : 2 * half + 2], in_=of_both[i][:, :, :, 0:live],
+                    axis=AXIS_XY, op=ALU.max,
+                )
+            else:
+                for t in range(2):
+                    g = 2 * half + t
+                    nc.vector.tensor_reduce(
+                        out=top[:, g : g + 1], in_=of_pair[i][t][:, :, 0:live], axis=AXIS_XY, op=ALU.max
                     )
 
-            def invert(c):
-                sums = of_chunk[c]["sums"]
-                inverse = stat.tile([P, KVH], F32)
-                if c >= FIRST_FULL:
-                    nc.vector.tensor_tensor(out=sums[:, 0, :], in0=sums[:, 0, :], in1=sums[:, 1, :], op=ALU.add)
-                nc.vector.reciprocal(out=inverse[:], in_=sums[:, 0, :])
-                of_chunk[c]["inverse"] = inverse
-
-            def flip_e(c, g):
-                last_run = c // PATTERNS
-                passes = last_run // 2 + 1
-                e32 = e_tiles[c % PATTERNS][g][:].bitcast(F32)
-                e_words = eflip.tile([P, 2 * S_PASSES, P], F32)
-                for r in range(2 * passes):
-                    i = r - (last_run - 2)
-                    if 0 <= i < 3:
-                        nc.tensor.transpose(e_words[:, r, :], e32[:, i * P : (i + 1) * P], ident32[:])
-                    else:
-                        nc.tensor.transpose(e_words[:, r, :], zeros[:].bitcast(F32), ident32[:])
-                of_tile[c, g]["e_words"] = e_words
-
-            def regroup(c, g):
-                passes = c // PATTERNS // 2 + 1
-                e_grouped = work.tile([P, S_PASSES * P * PACK], BF16, align_bytes=64)
-                e_grouped32 = e_grouped[:].bitcast(F32).rearrange("p (s t u) -> p s t u", s=S_PASSES, u=2)
-                nc.scalar.copy(
-                    out=e_grouped32[:, 0:passes],
-                    in_=of_tile[c, g]["e_words"][:, 0 : 2 * passes, :].rearrange("p (s u) t -> p s t u", u=2),
+        def set_shift(i):
+            c, half = i // 2, i % 2
+            cols = slice(2 * half, 2 * half + 2)
+            top = of_chunk[c]["top"][:, cols]
+            shift = of_chunk[c]["shift"][:, cols]
+            if c < FULL:
+                nc.vector.tensor_scalar(out=shift, in0=top, scalar1=-SCALE, scalar2=None, op0=ALU.mult)
+            else:
+                nc.vector.scalar_tensor_tensor(
+                    out=shift, in0=top, scalar=-SCALE, in1=of_quad[(c - FULL) // 4]["neg"][:, c % 4, cols],
+                    op0=ALU.mult, op1=ALU.min,
                 )
-                of_tile[c, g]["e_grouped"] = e_grouped
 
-            def quantise(c, g):
-                passes = c // PATTERNS // 2 + 1
-                e_codes = packed.tile([P, S_PASSES * P], U32, align_bytes=64)
-                e_scales = packed.tile([P, S_PASSES * P], U8, align_bytes=64)
-                nc.vector.quantize_mx(
-                    out=e_codes[:, 0 : passes * P].bitcast(FP8X4),
-                    scales=e_scales[:, 0 : passes * P],
-                    in_=of_tile[c, g]["e_grouped"][:, 0 : passes * P * PACK],
-                )
-                of_tile[c, g]["e_codes"] = e_codes
-                of_tile[c, g]["e_scales"] = e_scales
+        def soften_some(out_ap, in_ap, c, g, slot):
+            nc.scalar.activation(
+                out=out_ap, in_=in_ap, func=ACT.Exp, bias=of_chunk[c]["shift"][:, g : g + 1], scale=SCALE,
+                accum_out=of_chunk[c]["sums"][:, slot, g : g + 1],
+            )
 
-            def weigh(c):
-                passes = c // PATTERNS // 2 + 1
-                o_sum = osum.tile([P, KVH, D], F32)
-                for g in range(KVH):
-                    for sp in range(passes):
-                        nc.tensor.matmul_mx(
-                            out=o_sum[:, g, :],
-                            lhsT=of_tile[c, g]["e_codes"][:, sp * P : (sp + 1) * P].bitcast(FP8X4),
-                            lhsT_scale=of_tile[c, g]["e_scales"][:, sp * P : (sp + 1) * P],
-                            rhs=v_codes[:, sp, g * D : (g + 1) * D].bitcast(FP8X4),
-                            rhs_scale=v_scales[:, sp, g * D : (g + 1) * D],
-                            start=(sp == 0),
-                            stop=(sp == passes - 1),
+        def diag_view(tile_, quads):
+            return tile_[:].rearrange("q (j u g w) -> q j u g w", j=quads, u=2, g=KVH)
+
+        def soften(i):
+            c, half = i // 2, i % 2
+            for t in range(2):
+                g = 2 * half + t
+                bank = of_pair[i][t]
+                if c < DIAG:
+                    e = diag_view(e_diag[c % 4], 3)
+                    quads, rest = (c + 1) // 4, (c + 1) % 4
+                    if quads > 0:
+                        soften_some(
+                            e[:, 0:quads, :, g, :],
+                            bank[:, :, 0 : quads * HQ].rearrange("q u (j w) -> q j u w", w=HQ),
+                            c, g, 0,
                         )
-                of_chunk[c]["o_sum"] = o_sum
+                    if rest > 0:
+                        soften_some(
+                            e[:, quads, :, g, 0 : rest * HC],
+                            bank[:, :, quads * HQ : quads * HQ + rest * HC],
+                            c, g, 1 if quads > 0 else 0,
+                        )
+                else:
+                    live = (c + 1) * HC if c < FULL else 2 * P
+                    e = e_row[2 * (i % 3) + t][:].rearrange("q (u c) -> q u c", u=2)
+                    soften_some(e[:, :, 0:live], bank[:, :, 0:live], c, g, 0)
+                    if c >= FULL:
+                        b = c % 4
+                        soften_some(
+                            diag_view(e_old[b], 1)[:, 0, :, g, b * HC : (b + 1) * HC],
+                            of_quad[(c - FULL) // 4]["scores"][:, b, g, :].rearrange("q (u c) -> q u c", u=2),
+                            c, g, 1,
+                        )
 
-            def finish(c):
-                o_sb = work.tile([P, KVH, D], F32)
-                nc.vector.tensor_tensor(
-                    out=o_sb[:], in0=of_chunk[c]["o_sum"][:],
-                    in1=of_chunk[c]["inverse"][:].unsqueeze(2).to_broadcast([P, KVH, D]), op=ALU.mult,
+        def invert(c):
+            sums = of_chunk[c]["sums"]
+            inverse = stat.tile([P, KVH], F32, name="inverse")
+            if c >= FULL or (c < DIAG and c >= 4 and c % 4 != 3):
+                nc.vector.tensor_tensor(out=sums[:, 0, :], in0=sums[:, 0, :], in1=sums[:, 1, :], op=ALU.add)
+            nc.vector.reciprocal(out=inverse[:], in_=sums[:, 0, :])
+            of_chunk[c]["inverse"] = inverse
+
+        def jobs_of(i):
+            c, half = i // 2, i % 2
+            if c < DIAG:
+                if half == 0:
+                    return []
+                words = e_diag[c % 4][:].bitcast(F32)
+                units = [words[:, j * 2 * P : (j + 1) * 2 * P] for j in range(c // 4 + 1)]
+                return [units[n : n + 2] for n in range(0, len(units), 2)]
+            jobs = [[e_row[2 * (i % 3) + t][:].bitcast(F32) for t in range(2)]]
+            if c >= FULL and half == 1:
+                jobs.append([e_old[c % 4][:].bitcast(F32)])
+            return jobs
+
+        def flip_e(c, units):
+            bank = flip.tile([P, 2, 2, P], F32, tag="flip")
+            for n in range(len(units)):
+                for u in range(2):
+                    nc.tensor.transpose(bank[:, n, u, :], units[n][:, u * P : (u + 1) * P], ident32[:])
+            return {"c": c, "n": len(units), "bank": bank}
+
+        def regroup(job):
+            n = job["n"]
+            grouped = work.tile([P, 2 * P * PACK], BF16, align_bytes=64, name="e_grouped")
+            nc.scalar.copy(
+                out=grouped[:].bitcast(F32).rearrange("p (n t u) -> p n t u", n=2, u=2)[:, 0:n],
+                in_=job["bank"][:, 0:n].rearrange("p n u t -> p n t u"),
+            )
+            job["grouped"] = grouped
+
+        def quantise(job):
+            n = job["n"]
+            codes = packed.tile([P, 2 * P], U32, align_bytes=64, name="e_codes")
+            scales = packed.tile([P, 2 * P], U8, align_bytes=64, name="e_scales")
+            nc.vector.quantize_mx(
+                out=codes[:, 0 : n * P].bitcast(FP8X4), scales=scales[:, 0 : n * P],
+                in_=job["grouped"][:, 0 : n * P * PACK],
+            )
+            for m in range(n):
+                of_chunk[job["c"]]["units"].append(
+                    (codes[:, m * P : (m + 1) * P], scales[:, m * P : (m + 1) * P])
                 )
-                chunk_rows = out_rows[c * CH : (c + 1) * CH, :].rearrange("i (g h d) -> h i g d", g=KVH, h=R)
-                for h in range(R):
-                    nc.sync.dma_start(out=chunk_rows[h], in_=o_sb[h * CH : (h + 1) * CH, :, :])
 
-            tiles = CHUNKS * KVH
+        def mx(out_ap, unit, codes, scales, start, stop):
+            nc.tensor.matmul_mx(
+                out=out_ap, lhsT=unit[0].bitcast(FP8X4), lhsT_scale=unit[1],
+                rhs=codes.bitcast(FP8X4), rhs_scale=scales, start=start, stop=stop,
+            )
 
-            def run(stage_of_tile, n):
-                if 0 <= n < tiles:
-                    stage_of_tile(n // KVH, n % KVH)
+        def weigh(c):
+            o_sum = osum.tile([P, KVH, D], F32)
+            units = of_chunk[c]["units"]
+            flat = o_sum[:].rearrange("p g d -> p (g d)")
+            if c < DIAG:
+                for j in range(len(units)):
+                    mx(flat, units[j], diag_codes[j][:], diag_scales[j][:], j == 0, j == len(units) - 1)
+            else:
+                if c >= FULL:
+                    quad = (c - FULL) // 4
+                    mx(flat, units[4], diag_codes[quad][:], diag_scales[quad][:], True, False)
+                    codes, scales = roll_codes[c % 4][:], roll_scales[c % 4][:]
+                else:
+                    codes, scales = v_codes[:, 0, :], v_scales[:, 0, :]
+                for g in range(KVH):
+                    cols = slice(g * D, (g + 1) * D)
+                    mx(o_sum[:, g, :], units[g], codes[:, cols], scales[:, cols], c < FULL, c < FULL or g == KVH - 1)
+            of_chunk[c]["o_sum"] = o_sum
 
-            def run_chunk(stage_of_chunk, n):
-                if n % KVH == 0 and 0 <= n < tiles:
-                    stage_of_chunk(n // KVH)
+        def finish(c):
+            o_sb = work.tile([P, KVH, D], F32, name="o_sb")
+            nc.vector.tensor_tensor(
+                out=o_sb[:], in0=of_chunk[c]["o_sum"][:],
+                in1=of_chunk[c]["inverse"][:].unsqueeze(2).to_broadcast([P, KVH, D]), op=ALU.mult,
+            )
+            chunk_rows = out_rows[c * CH : (c + 1) * CH, :].rearrange("i (g h d) -> h i g d", g=KVH, h=R)
+            for h in range(R):
+                nc.sync.dma_start(out=chunk_rows[h], in_=o_sb[h * CH : (h + 1) * CH, :, :])
 
-            with tc.manual_schedule():
-                for i in range(tiles + 3 * KVH + 1):
-                    run(score, i)
-                    run(flip_e, i - 4)
-                    run_chunk(weigh, i - (KVH - 1) - 6 - 2)
-                    run(peak, i - 1)
-                    run(quantise, i - 6)
-                    run(set_shift, i - 1)
-                    run_chunk(invert, i - (KVH - 1) - 2 - 2)
-                    run_chunk(finish, i - (KVH - 1) - 6 - 3)
-                    run(soften, i - 2)
-                    run(regroup, i - 5)
+        of_chunk = {}
+        of_pair = {}
+        of_both = {}
+        of_quad = {}
+        q_raw = {}
+        v_bank = {}
+        with tc.manual_schedule():
+            for n in range(2):
+                nc.sync.dma_start(
+                    out=k_raw[:, 4 * n : 4 * n + 4, :],
+                    in_=k_rows[n * W : (n + 1) * W, :].rearrange("(n p) f -> p n f", p=P),
+                )
+            load_q(0)
+            w_ops = []
+            x_ops = []
+            for g in range(KVH):
+                w_ops.append({
+                    "rows": load_rows(wv[g * D : (g + 1) * D, :]),
+                    "codes": w_codes[:, g, :], "scales": w_scales[:, g, :],
+                })
+            load_q(1)
+
+            def load_x(n):
+                in_ = x_rows[n // PACK * K_PASS : (n // PACK + 1) * K_PASS, :].rearrange("(p t) k -> t p k", t=PACK)
+                x_ops.append({"rows": load_rows(in_[n % PACK])})
+
+            for n in range(PACK):
+                load_x(n)
+            load_q(2)
+            load_q(3)
+
+            copies = (nc.scalar.copy, nc.vector.tensor_copy)
+            for n in range(T // P):
+                lay_k(copies[n % 2], n, turn_k(n))
+            for g in range(KVH):
+                lay_q(copies[g % 2], 0, g, turn_q(0, g))
+
+            lead = 2
+            prep = [("rows", w_ops[g], half) for g in range(KVH) for half in range(2)]
+            prep += [("rows", n, half) for n in range(PACK + 1) for half in range(2)]
+            prep += [("v", 0, g) for g in range(KVH)]
+            prep += [("rows", n, half) for n in range(PACK + 1, 2 * PACK) for half in range(2)]
+            prep += [None]
+            prep += [("v", 1, g) for g in range(KVH)]
+            to_quantise = []
+            rows_done = []
+            weighed = 0
+            for i in range(-lead, PAIRS + 3):
+                finishing = []
+                if weighed < CHUNKS and i >= 2 * weighed + 4 and i >= 23:
+                    weigh(weighed)
+                    finishing.append(weighed)
+                    weighed += 1
+                jobs = []
+                if 0 <= i - 1 < PAIRS:
+                    for units in jobs_of(i - 1):
+                        jobs.append(flip_e((i - 1) // 2, units))
+                piece = prep[i + lead] if i + lead < len(prep) else None
+                if piece is not None and piece[0] == "rows":
+                    op = piece[1]
+                    if not isinstance(op, dict):
+                        op = x_ops[op]
+                        if "codes" not in op:
+                            codes = xq_pool.tile([P, X_PASSES * P], U32, align_bytes=64, name="x_codes")
+                            scales = xq_pool.tile([P, X_PASSES * P], U8, align_bytes=64, name="x_scales")
+                            op["codes"] = codes[:]
+                            op["scales"] = scales[:]
+                    turn_rows(op, piece[2])
+                elif piece is not None:
+                    project(piece[1], piece[2])
+                nq, gq = divmod((i + 10) // 2, KVH)
+                turn = i % 2 == 0 and nq < T // P
+                if turn:
+                    q_bank = turn_q(nq, gq)
+                if 0 <= i < PAIRS:
+                    soften(i)
+                for job in jobs:
+                    regroup(job)
+                if piece is not None and piece[0] == "rows":
+                    lay_rows(op, piece[2])
+                elif piece is not None:
+                    lay_v(piece[2])
+                if 0 <= i + 2 < PAIRS:
+                    score(i + 2)
+                if 0 <= i + 1 < PAIRS:
+                    peak(i + 1)
+                for job in to_quantise:
+                    quantise(job)
+                to_quantise = jobs
+                if 0 <= i + 1 < PAIRS:
+                    set_shift(i + 1)
+                for op_done in rows_done:
+                    if op_done[0] == "rows":
+                        quantise_rows(op_done[1])
+                    else:
+                        quantise_v(op_done[1])
+                        if op_done[1] == 0:
+                            make_diag()
+                            make_roll()
+                        else:
+                            for j in range(4):
+                                advance_roll(j)
+                rows_done = []
+                if piece is not None and piece[0] == "rows" and piece[2] == 1:
+                    rows_done.append(("rows", op))
+                elif piece is not None and piece[0] == "v" and piece[2] == KVH - 1:
+                    rows_done.append(("v", piece[1]))
+                for c in finishing:
+                    finish(c)
+                    if FULL <= c < CHUNKS - 4:
+                        advance_roll(c - FULL + 4)
+                if turn:
+                    lay_q(nc.vector.tensor_copy, nq, gq, q_bank)
+                    if gq == KVH - 1 and nq + 3 < T // P:
+                        load_q(nq + 3)
+                if i >= 2 and i % 2 == 0 and i // 2 - 1 < CHUNKS:
+                    invert(i // 2 - 1)
+                quad = (i + 3) // 8 - 4
+                if (i + 3) % 8 == 0 and 0 <= quad < 4:
+                    score_old(quad)
+                if (i + 2) % 8 == 0 and 0 <= (i + 2) // 8 - 4 < 4:
+                    negate_old((i + 2) // 8 - 4)
+                if -lead <= i < 2 * PACK and i % 2 == 0 and i >= 0:
+                    load_x(PACK + i // 2)

@@ -55,6 +55,8 @@ def tile_localgqattention_pb_kernel(tc, q_rot, k_rot, x, wv, out):
     ) as stage, tc.tile_pool(name="xq", bufs=6) as xq_pool, tc.tile_pool(
         name="packed", bufs=18, reuse_waits="tile"
     ) as packed, tc.tile_pool(name="work", bufs=3, reuse_waits="tile") as work, tc.tile_pool(
+        name="rest", bufs=2, reuse_waits="tile"
+    ) as rest_pool, tc.tile_pool(name="store", bufs=5, reuse_waits="tile") as store_pool, tc.tile_pool(
         name="stat", bufs=16, reuse_waits="tile"
     ) as stat, tc.psum_pool(name="score", bufs=4, reuse_waits="tile") as score_pool, tc.psum_pool(
         name="flip", bufs=3, reuse_waits="tile"
@@ -230,7 +232,9 @@ def tile_localgqattention_pb_kernel(tc, q_rot, k_rot, x, wv, out):
         def turn_k(n):
             bank = flip.tile([P, KVH, P], BF16, tag="flip")
             for g in range(KVH):
-                nc.tensor.transpose(bank[:, g, :], k_raw[:, n, g * D : (g + 1) * D], ident_bf[:])
+                nc.tensor.matmul(
+                    out=bank[:, g, :], lhsT=k_raw[:, n, g * D : (g + 1) * D], rhs=ident_bf[:], start=True, stop=True
+                )
             return bank
 
         def lay_k(copy, n, bank):
@@ -247,7 +251,9 @@ def tile_localgqattention_pb_kernel(tc, q_rot, k_rot, x, wv, out):
             bank = flip.tile([P, R, P], BF16, tag="flip")
             for h in range(R):
                 first = (g * R + h) * D
-                nc.tensor.transpose(bank[:, h, :], q_raw[n][:, first : first + D], ident_bf[:])
+                nc.tensor.matmul(
+                    out=bank[:, h, :], lhsT=q_raw[n][:, first : first + D], rhs=ident_bf[:], start=True, stop=True
+                )
             return bank
 
         def lay_q(copy, n, g, bank):
@@ -272,10 +278,14 @@ def tile_localgqattention_pb_kernel(tc, q_rot, k_rot, x, wv, out):
                         start=False,
                         stop=(b == 3 and g == KVH - 1),
                     )
+            of_quad[quad] = {"bank": bank}
+
+        def old_peak(quad):
+            bank = of_quad[quad]["bank"]
             old_max = stat.tile([P, 4, KVH], F32, name="old_max")
             nc.vector.tensor_reduce(out=old_max[:], in_=bank[:], axis=AXIS_X, op=ALU.max)
             neg_old = stat.tile([P, 4, KVH], F32, name="neg_old")
-            old_scores = work.tile([P, 4, KVH, CH], F32, name="old_scores")
+            old_scores = rest_pool.tile([P, 4, KVH, CH], F32, name="old_scores")
             nc.scalar.copy(out=old_scores[:], in_=bank[:])
             of_quad[quad] = {"max": old_max, "neg": neg_old, "scores": old_scores}
 
@@ -313,8 +323,9 @@ def tile_localgqattention_pb_kernel(tc, q_rot, k_rot, x, wv, out):
                         out=bank[:, :, live : 2 * P], lhsT=lhsT, rhs=kT[:, g, 0, :, live : 2 * P],
                         start=True, stop=True,
                     )
+                wide = live if c >= FULL else P if c < FULL // 2 else 2 * P
                 nc.tensor.matmul(
-                    out=bank[:, :, 0:live], lhsT=lhsT, rhs=kT[:, g, c // FULL, :, 0:live], start=True, stop=False
+                    out=bank[:, :, 0:wide], lhsT=lhsT, rhs=kT[:, g, c // FULL, :, 0:wide], start=True, stop=False
                 )
                 nc.tensor.matmul(
                     out=bank[:, :, live - HC : live], lhsT=spread_cols, rhs=own_bias[:], start=False, stop=True
@@ -468,7 +479,7 @@ def tile_localgqattention_pb_kernel(tc, q_rot, k_rot, x, wv, out):
             of_chunk[c]["o_sum"] = o_sum
 
         def finish(c):
-            o_sb = work.tile([P, KVH, D], F32, name="o_sb")
+            o_sb = store_pool.tile([P, KVH, D], F32, name="o_sb")
             nc.vector.tensor_tensor(
                 out=o_sb[:], in0=of_chunk[c]["o_sum"][:],
                 in1=of_chunk[c]["inverse"][:].unsqueeze(2).to_broadcast([P, KVH, D]), op=ALU.mult,
@@ -497,7 +508,8 @@ def tile_localgqattention_pb_kernel(tc, q_rot, k_rot, x, wv, out):
                     "rows": load_rows(wv[g * D : (g + 1) * D, :]),
                     "codes": w_codes[:, g, :], "scales": w_scales[:, g, :],
                 })
-            load_q(1)
+                if g == 1:
+                    load_q(1)
 
             def load_x(n):
                 in_ = x_rows[n // PACK * K_PASS : (n // PACK + 1) * K_PASS, :].rearrange("(p t) k -> t p k", t=PACK)
@@ -522,19 +534,17 @@ def tile_localgqattention_pb_kernel(tc, q_rot, k_rot, x, wv, out):
             prep += [None]
             prep += [("v", 1, g) for g in range(KVH)]
             to_quantise = []
+            to_lay = []
             rows_done = []
+            rows_next = []
+            finishing = []
             weighed = 0
-            for i in range(-lead, PAIRS + 3):
-                finishing = []
-                if weighed < CHUNKS and i >= 2 * weighed + 4 and i >= 23:
-                    weigh(weighed)
-                    finishing.append(weighed)
-                    weighed += 1
+            for i in range(-lead, PAIRS + 4):
+                piece = prep[i + lead] if i + lead < len(prep) else None
                 jobs = []
                 if 0 <= i - 1 < PAIRS:
                     for units in jobs_of(i - 1):
                         jobs.append(flip_e((i - 1) // 2, units))
-                piece = prep[i + lead] if i + lead < len(prep) else None
                 if piece is not None and piece[0] == "rows":
                     op = piece[1]
                     if not isinstance(op, dict):
@@ -545,32 +555,52 @@ def tile_localgqattention_pb_kernel(tc, q_rot, k_rot, x, wv, out):
                             op["codes"] = codes[:]
                             op["scales"] = scales[:]
                     turn_rows(op, piece[2])
-                elif piece is not None:
-                    project(piece[1], piece[2])
-                nq, gq = divmod((i + 10) // 2, KVH)
-                turn = i % 2 == 0 and nq < T // P
-                if turn:
-                    q_bank = turn_q(nq, gq)
                 if 0 <= i < PAIRS:
                     soften(i)
                 for job in jobs:
                     regroup(job)
+                for g in to_lay:
+                    lay_v(g)
+                to_lay = []
                 if piece is not None and piece[0] == "rows":
                     lay_rows(op, piece[2])
-                elif piece is not None:
-                    lay_v(piece[2])
+                nq, gq = divmod((i + 9) // 2, KVH)
+                turn = i % 2 == 1 and nq < T // P
+                if turn:
+                    q_bank = turn_q(nq, gq)
+                quad = (i + 2) // 8 - 4
+                with_old = i % 8 == 6 and 0 <= quad < 4
+                if with_old:
+                    score_old(quad)
                 if 0 <= i + 2 < PAIRS:
                     score(i + 2)
                 if 0 <= i + 1 < PAIRS:
                     peak(i + 1)
+                if i % 8 == 7 and 0 <= (i + 1) // 8 - 4 < 4:
+                    negate_old((i + 1) // 8 - 4)
                 for job in to_quantise:
                     quantise(job)
                 to_quantise = jobs
                 if 0 <= i + 1 < PAIRS:
                     set_shift(i + 1)
+                done = finishing
+                finishing = []
+                if weighed < CHUNKS and i >= 2 * weighed + 3 and i >= 23:
+                    weigh(weighed)
+                    finishing.append(weighed)
+                    weighed += 1
+                if piece is not None and piece[0] == "v":
+                    project(piece[1], piece[2])
+                    to_lay.append(piece[2])
+                for c in done:
+                    finish(c)
+                    if FULL <= c < CHUNKS - 4:
+                        advance_roll(c - FULL + 4)
                 for op_done in rows_done:
                     if op_done[0] == "rows":
                         quantise_rows(op_done[1])
+                    elif op_done[2] == 1:
+                        rows_next.append(("v", op_done[1], 0))
                     else:
                         quantise_v(op_done[1])
                         if op_done[1] == 0:
@@ -579,25 +609,19 @@ def tile_localgqattention_pb_kernel(tc, q_rot, k_rot, x, wv, out):
                         else:
                             for j in range(4):
                                 advance_roll(j)
-                rows_done = []
+                rows_done = rows_next
+                rows_next = []
                 if piece is not None and piece[0] == "rows" and piece[2] == 1:
                     rows_done.append(("rows", op))
                 elif piece is not None and piece[0] == "v" and piece[2] == KVH - 1:
-                    rows_done.append(("v", piece[1]))
-                for c in finishing:
-                    finish(c)
-                    if FULL <= c < CHUNKS - 4:
-                        advance_roll(c - FULL + 4)
+                    rows_done.append(("v", piece[1], 1))
+                if with_old:
+                    old_peak(quad)
                 if turn:
                     lay_q(nc.vector.tensor_copy, nq, gq, q_bank)
                     if gq == KVH - 1 and nq + 3 < T // P:
                         load_q(nq + 3)
                 if i >= 2 and i % 2 == 0 and i // 2 - 1 < CHUNKS:
                     invert(i // 2 - 1)
-                quad = (i + 3) // 8 - 4
-                if (i + 3) % 8 == 0 and 0 <= quad < 4:
-                    score_old(quad)
-                if (i + 2) % 8 == 0 and 0 <= (i + 2) // 8 - 4 < 4:
-                    negate_old((i + 2) // 8 - 4)
-                if -lead <= i < 2 * PACK and i % 2 == 0 and i >= 0:
+                if 0 <= i < 2 * PACK and i % 2 == 0:
                     load_x(PACK + i // 2)

@@ -29,7 +29,7 @@ W = 512
 CH = P // R
 CHUNKS = T // CH
 FULL = W // CH
-DIAG = 12
+DIAG = 8
 X_PASSES = HID // K_PASS
 S_PASSES = T // K_PASS
 HC = CH // 2
@@ -53,7 +53,7 @@ def tile_localgqattention_pb_kernel(tc, q_rot, k_rot, x, wv, out):
     ) as rows_pool, tc.tile_pool(name="qraw", bufs=4) as qraw_pool, tc.tile_pool(
         name="stage", bufs=3
     ) as stage, tc.tile_pool(name="xq", bufs=6) as xq_pool, tc.tile_pool(
-        name="packed", bufs=18, reuse_waits="tile"
+        name="packed", bufs=22, reuse_waits="tile"
     ) as packed, tc.tile_pool(name="work", bufs=3, reuse_waits="tile") as work, tc.tile_pool(
         name="rest", bufs=2, reuse_waits="tile"
     ) as rest_pool, tc.tile_pool(name="store", bufs=5, reuse_waits="tile") as store_pool, tc.tile_pool(
@@ -120,7 +120,7 @@ def tile_localgqattention_pb_kernel(tc, q_rot, k_rot, x, wv, out):
             t_ds = keep.tile([P, KVH * D], U8, align_bytes=64, name="diag_scales%d" % n)
             t_rc = keep.tile([P, KVH * D], U32, align_bytes=64, name="roll_codes%d" % n)
             t_rs = keep.tile([P, KVH * D], U8, align_bytes=64, name="roll_scales%d" % n)
-            t_ed = keep.tile([P, 3 * 2 * KVH * HQ], BF16, name="e_diag%d" % n)
+            t_ed = keep.tile([P, 2 * 2 * KVH * HQ], BF16, name="e_diag%d" % n)
             t_eo = keep.tile([P, 2 * KVH * HQ], BF16, name="e_old%d" % n)
             nc.gpsimd.memset(t_ed[:], 0.0)
             diag_codes.append(t_dc)
@@ -160,12 +160,12 @@ def tile_localgqattention_pb_kernel(tc, q_rot, k_rot, x, wv, out):
                 nc.tensor.transpose(bank[:, n, :], words[:, first : first + P], ident32[:])
             op["bank"] = bank
 
-        def lay_rows(op, half):
+        def lay_rows(op, half, copy):
             if half == 0:
                 grouped = stage.tile([P, X_PASSES * P * PACK], BF16, align_bytes=64)
                 op["grouped"] = grouped
             grouped32 = op["grouped"][:].bitcast(F32).rearrange("p (c r u) -> p c r u", c=X_PASSES, u=2)
-            nc.scalar.copy(
+            copy(
                 out=grouped32[:, 2 * half : 2 * half + 2],
                 in_=op["bank"][:].rearrange("p (c u) r -> p c r u", u=2),
             )
@@ -189,8 +189,8 @@ def tile_localgqattention_pb_kernel(tc, q_rot, k_rot, x, wv, out):
                     )
             v_bank[g] = bank
 
-        def lay_v(g):
-            nc.scalar.copy(out=v_grouped[:, g, :, :], in_=v_bank[g][:].rearrange("p t d -> p d t"))
+        def lay_v(g, copy):
+            copy(out=v_grouped[:, g, :, :], in_=v_bank[g][:].rearrange("p t d -> p d t"))
 
         def quantise_v(sp):
             nc.vector.quantize_mx(
@@ -256,19 +256,36 @@ def tile_localgqattention_pb_kernel(tc, q_rot, k_rot, x, wv, out):
                 )
             return bank
 
+        def turn_q_keep(n, g):
+            q_bank[n, g] = turn_q(n, g)
+
+        def row_op(n):
+            if n < KVH:
+                return w_ops[n]
+            op = x_ops[n - KVH]
+            if "codes" not in op:
+                codes = xq_pool.tile([P, X_PASSES * P], U32, align_bytes=64, name="x_codes")
+                scales = xq_pool.tile([P, X_PASSES * P], U8, align_bytes=64, name="x_scales")
+                op["codes"] = codes[:]
+                op["scales"] = scales[:]
+            return op
+
         def lay_q(copy, n, g, bank):
             copy(
                 out=qT[:, g, n * (P // CH) : (n + 1) * (P // CH), :, :],
                 in_=bank[:].rearrange("d h (c i) -> d c h i", i=CH),
             )
 
-        def score_old(quad):
-            bank = flip.tile([P, 4, KVH, CH], F32, tag="flip")
-            nc.tensor.matmul(
-                out=bank[:].rearrange("p c g j -> p (c g j)"), lhsT=spread_cols,
-                rhs=old_bias[:].rearrange("k n j -> k (n j)"), start=True, stop=False,
-            )
-            for b in range(4):
+        def score_old(quad, part):
+            if part == 0:
+                bank = flip.tile([P, 4, KVH, CH], F32, tag="flip")
+                nc.tensor.matmul(
+                    out=bank[:].rearrange("p c g j -> p (c g j)"), lhsT=spread_cols,
+                    rhs=old_bias[:].rearrange("k n j -> k (n j)"), start=True, stop=False,
+                )
+                of_quad[quad] = {"bank": bank}
+            bank = of_quad[quad]["bank"]
+            for b in (2 * part, 2 * part + 1):
                 j = 4 * quad + b
                 for g in range(KVH):
                     nc.tensor.matmul(
@@ -278,16 +295,18 @@ def tile_localgqattention_pb_kernel(tc, q_rot, k_rot, x, wv, out):
                         start=False,
                         stop=(b == 3 and g == KVH - 1),
                     )
-            of_quad[quad] = {"bank": bank}
 
         def old_peak(quad):
             bank = of_quad[quad]["bank"]
             old_max = stat.tile([P, 4, KVH], F32, name="old_max")
             nc.vector.tensor_reduce(out=old_max[:], in_=bank[:], axis=AXIS_X, op=ALU.max)
             neg_old = stat.tile([P, 4, KVH], F32, name="neg_old")
+            of_quad[quad].update({"max": old_max, "neg": neg_old})
+
+        def old_copy(quad):
             old_scores = rest_pool.tile([P, 4, KVH, CH], F32, name="old_scores")
-            nc.scalar.copy(out=old_scores[:], in_=bank[:])
-            of_quad[quad] = {"max": old_max, "neg": neg_old, "scores": old_scores}
+            nc.scalar.copy(out=old_scores[:], in_=of_quad[quad]["bank"][:])
+            of_quad[quad]["scores"] = old_scores
 
         def negate_old(quad):
             nc.vector.tensor_scalar(
@@ -323,7 +342,7 @@ def tile_localgqattention_pb_kernel(tc, q_rot, k_rot, x, wv, out):
                         out=bank[:, :, live : 2 * P], lhsT=lhsT, rhs=kT[:, g, 0, :, live : 2 * P],
                         start=True, stop=True,
                     )
-                wide = live if c >= FULL else P if c < FULL // 2 else 2 * P
+                wide = live
                 nc.tensor.matmul(
                     out=bank[:, :, 0:wide], lhsT=lhsT, rhs=kT[:, g, c // FULL, :, 0:wide], start=True, stop=False
                 )
@@ -377,7 +396,7 @@ def tile_localgqattention_pb_kernel(tc, q_rot, k_rot, x, wv, out):
                 g = 2 * half + t
                 bank = of_pair[i][t]
                 if c < DIAG:
-                    e = diag_view(e_diag[c % 4], 3)
+                    e = diag_view(e_diag[c % 4], 2)
                     quads, rest = (c + 1) // 4, (c + 1) % 4
                     if quads > 0:
                         soften_some(
@@ -407,7 +426,7 @@ def tile_localgqattention_pb_kernel(tc, q_rot, k_rot, x, wv, out):
             sums = of_chunk[c]["sums"]
             inverse = stat.tile([P, KVH], F32, name="inverse")
             if c >= FULL or (c < DIAG and c >= 4 and c % 4 != 3):
-                nc.vector.tensor_tensor(out=sums[:, 0, :], in0=sums[:, 0, :], in1=sums[:, 1, :], op=ALU.add)
+                nc.gpsimd.tensor_tensor(out=sums[:, 0, :], in0=sums[:, 0, :], in1=sums[:, 1, :], op=ALU.add)
             nc.vector.reciprocal(out=inverse[:], in_=sums[:, 0, :])
             of_chunk[c]["inverse"] = inverse
 
@@ -493,6 +512,7 @@ def tile_localgqattention_pb_kernel(tc, q_rot, k_rot, x, wv, out):
         of_both = {}
         of_quad = {}
         q_raw = {}
+        q_bank = {}
         v_bank = {}
         with tc.manual_schedule():
             for n in range(2):
@@ -525,102 +545,103 @@ def tile_localgqattention_pb_kernel(tc, q_rot, k_rot, x, wv, out):
                 lay_k(copies[n % 2], n, turn_k(n))
             for g in range(KVH):
                 lay_q(copies[g % 2], 0, g, turn_q(0, g))
+            load_q(4)
 
             lead = 2
-            prep = [("rows", w_ops[g], half) for g in range(KVH) for half in range(2)]
-            prep += [("rows", n, half) for n in range(PACK + 1) for half in range(2)]
-            prep += [("v", 0, g) for g in range(KVH)]
-            prep += [("rows", n, half) for n in range(PACK + 1, 2 * PACK) for half in range(2)]
-            prep += [None]
-            prep += [("v", 1, g) for g in range(KVH)]
+            prep = [("rows", n, half) for n in range(KVH + PACK) for half in range(2)] + [None]
+            for g in range(KVH):
+                prep += [("v", 0, g), ("rows", KVH + PACK + g // 2, g % 2)]
+            for n in range(KVH + PACK + 2, KVH + 2 * PACK):
+                prep += [("rows", n, 0), None, ("rows", n, 1), None]
+            for g in range(KVH):
+                prep += [("v", 1, g), None]
+            due = []
             to_quantise = []
-            to_lay = []
-            rows_done = []
-            rows_next = []
-            finishing = []
             weighed = 0
+            of_step = {}
+
+            def later(step, what, fn):
+                of_step.setdefault((step, what), []).append(fn)
+
+            def run_now(step, what):
+                for fn in of_step.get((step, what), []):
+                    fn()
+
+            for k in range(len(prep)):
+                piece = prep[k]
+                at = k - lead
+                if piece is None:
+                    continue
+                if piece[0] == "rows":
+                    n, half = piece[1], piece[2]
+                    later(at, "T", lambda n=n, half=half: turn_rows(row_op(n), half))
+                    on_v = False
+                    later(at + 0, "V copy" if on_v else "S copy", lambda n=n, half=half, on_v=on_v: lay_rows(row_op(n), half, nc.vector.tensor_copy if on_v else nc.scalar.copy))
+                    if half == 1:
+                        later(at + 1, "V quantise", lambda n=n: quantise_rows(row_op(n)))
+                else:
+                    sp, g = piece[1], piece[2]
+                    later(at, "MX", lambda sp=sp, g=g: project(sp, g))
+                    on_v = False
+                    later(at, "V copy" if on_v else "S copy", lambda g=g, on_v=on_v: lay_v(g, nc.vector.tensor_copy if on_v else nc.scalar.copy))
+                    if g == KVH - 1:
+                        later(at + 1, "V quantise", lambda sp=sp: quantise_v(sp))
+                        if sp == 0:
+                            later(at + 1, "V quantise", make_diag)
+                            later(at + 1, "V quantise", make_roll)
+                        else:
+                            for j in range(4):
+                                later(at + 1, "V quantise", lambda j=j: advance_roll(j))
+            for n in range(1, T // P):
+                for g in range(KVH):
+                    at = 4 * (n - 1) + g + 2
+                    later(at, "plain", lambda n=n, g=g: turn_q_keep(n, g))
+                    on_s = False
+                    later(at, "S copy" if on_s else "V copy", lambda n=n, g=g, on_s=on_s: lay_q(nc.scalar.copy if on_s else nc.vector.tensor_copy, n, g, q_bank[n, g]))
+                    if g == KVH - 1 and n + 4 < T // P:
+                        later(at, "V copy", lambda n=n: load_q(n + 4))
+            for quad in range(4):
+                at = 8 * quad + 29
+                later(at - 2, "plain", lambda quad=quad: score_old(quad, 0))
+                later(at, "plain", lambda quad=quad: score_old(quad, 1))
+                later(at, "V copy", lambda quad=quad: old_peak(quad))
+                later(at, "S copy", lambda quad=quad: old_copy(quad))
+                later(at + 1, "V early", lambda quad=quad: negate_old(quad))
+
             for i in range(-lead, PAIRS + 4):
-                piece = prep[i + lead] if i + lead < len(prep) else None
                 jobs = []
                 if 0 <= i - 1 < PAIRS:
                     for units in jobs_of(i - 1):
                         jobs.append(flip_e((i - 1) // 2, units))
-                if piece is not None and piece[0] == "rows":
-                    op = piece[1]
-                    if not isinstance(op, dict):
-                        op = x_ops[op]
-                        if "codes" not in op:
-                            codes = xq_pool.tile([P, X_PASSES * P], U32, align_bytes=64, name="x_codes")
-                            scales = xq_pool.tile([P, X_PASSES * P], U8, align_bytes=64, name="x_scales")
-                            op["codes"] = codes[:]
-                            op["scales"] = scales[:]
-                    turn_rows(op, piece[2])
+                run_now(i, "T")
+                done = []
+                if weighed < CHUNKS and i >= max(2 * weighed + 4, 27 + 5 * weighed // 4):
+                    weigh(weighed)
+                    done.append(weighed)
+                    weighed += 1
+                run_now(i, "MX")
                 if 0 <= i < PAIRS:
                     soften(i)
                 for job in jobs:
                     regroup(job)
-                for g in to_lay:
-                    lay_v(g)
-                to_lay = []
-                if piece is not None and piece[0] == "rows":
-                    lay_rows(op, piece[2])
-                nq, gq = divmod((i + 9) // 2, KVH)
-                turn = i % 2 == 1 and nq < T // P
-                if turn:
-                    q_bank = turn_q(nq, gq)
-                quad = (i + 2) // 8 - 4
-                with_old = i % 8 == 6 and 0 <= quad < 4
-                if with_old:
-                    score_old(quad)
+                run_now(i, "plain")
                 if 0 <= i + 2 < PAIRS:
                     score(i + 2)
                 if 0 <= i + 1 < PAIRS:
                     peak(i + 1)
-                if i % 8 == 7 and 0 <= (i + 1) // 8 - 4 < 4:
-                    negate_old((i + 1) // 8 - 4)
+                run_now(i, "V early")
                 for job in to_quantise:
                     quantise(job)
                 to_quantise = jobs
                 if 0 <= i + 1 < PAIRS:
                     set_shift(i + 1)
-                done = finishing
-                finishing = []
-                if weighed < CHUNKS and i >= 2 * weighed + 3 and i >= 23:
-                    weigh(weighed)
-                    finishing.append(weighed)
-                    weighed += 1
-                if piece is not None and piece[0] == "v":
-                    project(piece[1], piece[2])
-                    to_lay.append(piece[2])
                 for c in done:
                     finish(c)
                     if FULL <= c < CHUNKS - 4:
                         advance_roll(c - FULL + 4)
-                for op_done in rows_done:
-                    if op_done[0] == "rows":
-                        quantise_rows(op_done[1])
-                    elif op_done[2] == 1:
-                        rows_next.append(("v", op_done[1], 0))
-                    else:
-                        quantise_v(op_done[1])
-                        if op_done[1] == 0:
-                            make_diag()
-                            make_roll()
-                        else:
-                            for j in range(4):
-                                advance_roll(j)
-                rows_done = rows_next
-                rows_next = []
-                if piece is not None and piece[0] == "rows" and piece[2] == 1:
-                    rows_done.append(("rows", op))
-                elif piece is not None and piece[0] == "v" and piece[2] == KVH - 1:
-                    rows_done.append(("v", piece[1], 1))
-                if with_old:
-                    old_peak(quad)
-                if turn:
-                    lay_q(nc.vector.tensor_copy, nq, gq, q_bank)
-                    if gq == KVH - 1 and nq + 3 < T // P:
-                        load_q(nq + 3)
+                run_now(i, "V quantise")
+                run_now(i, "V copy")
+                run_now(i, "S copy")
                 if i >= 2 and i % 2 == 0 and i // 2 - 1 < CHUNKS:
                     invert(i // 2 - 1)
                 if 0 <= i < 2 * PACK and i % 2 == 0:

@@ -102,7 +102,7 @@ def tile_localgqattention_pb_kernel(tc, q_rot, k_rot, x, wv, out):
         spread_cols = spread[:].rearrange("k h i -> k (h i)")
 
         kT = keep.tile([P, KVH, S_PASSES, 2, 2 * P], BF16)
-        qT = keep.tile([P, KVH, CHUNKS, R, CH], BF16)
+        qT = keep.tile([P, CHUNKS, KVH, R, CH], BF16)
         k_raw = keep.tile([P, T // P, KVH * D], BF16)
         w_codes = keep.tile([P, KVH, X_PASSES * D], U32, align_bytes=64)
         w_scales = keep.tile([P, KVH, X_PASSES * D], U8, align_bytes=64)
@@ -248,8 +248,8 @@ def tile_localgqattention_pb_kernel(tc, q_rot, k_rot, x, wv, out):
             )
 
         def turn_q(n, g):
-            bank = flip.tile([P, R, P], BF16, tag="flip")
-            for h in range(R):
+            bank = flip.tile([P, 2 * R, P], BF16, tag="flip")
+            for h in range(2 * R):
                 first = (g * R + h) * D
                 nc.tensor.matmul(
                     out=bank[:, h, :], lhsT=q_raw[n][:, first : first + D], rhs=ident_bf[:], start=True, stop=True
@@ -272,7 +272,7 @@ def tile_localgqattention_pb_kernel(tc, q_rot, k_rot, x, wv, out):
 
         def lay_q(copy, n, g, bank):
             copy(
-                out=qT[:, g, n * (P // CH) : (n + 1) * (P // CH), :, :],
+                out=qT[:, n * (P // CH) : (n + 1) * (P // CH), g : g + 2, :, :].rearrange("d c g h i -> d c (g h) i"),
                 in_=bank[:].rearrange("d h (c i) -> d c h i", i=CH),
             )
 
@@ -290,7 +290,7 @@ def tile_localgqattention_pb_kernel(tc, q_rot, k_rot, x, wv, out):
                 for g in range(KVH):
                     nc.tensor.matmul(
                         out=bank[:, b, g, :].rearrange("p (u c) -> p u c", u=2),
-                        lhsT=qT[:, g, FULL + j].rearrange("d h i -> d (h i)"),
+                        lhsT=qT[:, FULL + j, g].rearrange("d h i -> d (h i)"),
                         rhs=kT[:, g, 0, :, j * HC : (j + 1) * HC],
                         start=False,
                         stop=(b == 3 and g == KVH - 1),
@@ -316,12 +316,14 @@ def tile_localgqattention_pb_kernel(tc, q_rot, k_rot, x, wv, out):
         def score(i):
             c, half = i // 2, i % 2
             if half == 0:
+                if c % 2 == 0:
+                    t_sums = stat.tile([P, 2, 2, KVH], F32, name="sums")
+                    of_chunk["sums"] = t_sums
                 of_chunk[c] = {
                     "top": stat.tile([P, KVH], F32, name="top"),
                     "shift": stat.tile([P, KVH], F32, name="shift"),
-                    "sums": stat.tile([P, 2, KVH], F32, name="sums"),
+                    "sums": of_chunk["sums"],
                     "units": [],
-                    "jobs": [],
                 }
             banks = []
             if c < FULL // 2:
@@ -334,7 +336,7 @@ def tile_localgqattention_pb_kernel(tc, q_rot, k_rot, x, wv, out):
                 else:
                     own = score_pool.tile([P, 2, 2 * P], F32, tag="score")
                     bank = own[:]
-                lhsT = qT[:, g, c].rearrange("d h i -> d (h i)")
+                lhsT = qT[:, c, g].rearrange("d h i -> d (h i)")
                 j = c % FULL
                 live = (j + 1) * HC
                 if c >= FULL and live < 2 * P:
@@ -384,7 +386,7 @@ def tile_localgqattention_pb_kernel(tc, q_rot, k_rot, x, wv, out):
         def soften_some(out_ap, in_ap, c, g, slot):
             nc.scalar.activation(
                 out=out_ap, in_=in_ap, func=ACT.Exp, bias=of_chunk[c]["shift"][:, g : g + 1], scale=SCALE,
-                accum_out=of_chunk[c]["sums"][:, slot, g : g + 1],
+                accum_out=of_chunk[c]["sums"][:, slot, c % 2, g : g + 1],
             )
 
         def diag_view(tile_, quads):
@@ -424,11 +426,14 @@ def tile_localgqattention_pb_kernel(tc, q_rot, k_rot, x, wv, out):
 
         def invert(c):
             sums = of_chunk[c]["sums"]
-            inverse = stat.tile([P, KVH], F32, name="inverse")
-            if c >= FULL or (c < DIAG and c >= 4 and c % 4 != 3):
-                nc.gpsimd.tensor_tensor(out=sums[:, 0, :], in0=sums[:, 0, :], in1=sums[:, 1, :], op=ALU.add)
-            nc.vector.reciprocal(out=inverse[:], in_=sums[:, 0, :])
-            of_chunk[c]["inverse"] = inverse
+            inverse = stat.tile([P, 2, KVH], F32, name="inverse")
+            if c >= FULL or c < DIAG and c >= 4 and c % 4 == 1:
+                nc.gpsimd.tensor_tensor(out=sums[:, 0], in0=sums[:, 0], in1=sums[:, 1], op=ALU.add)
+            elif c < DIAG and c >= 4:
+                nc.gpsimd.tensor_tensor(out=sums[:, 0, 0, :], in0=sums[:, 0, 0, :], in1=sums[:, 1, 0, :], op=ALU.add)
+            nc.vector.reciprocal(out=inverse[:], in_=sums[:, 0])
+            of_chunk[c - 1]["inverse"] = inverse[:, 0]
+            of_chunk[c]["inverse"] = inverse[:, 1]
 
         def jobs_of(i):
             c, half = i // 2, i % 2
@@ -499,10 +504,17 @@ def tile_localgqattention_pb_kernel(tc, q_rot, k_rot, x, wv, out):
 
         def finish(c):
             o_sb = store_pool.tile([P, KVH, D], F32, name="o_sb")
-            nc.vector.tensor_tensor(
-                out=o_sb[:], in0=of_chunk[c]["o_sum"][:],
-                in1=of_chunk[c]["inverse"][:].unsqueeze(2).to_broadcast([P, KVH, D]), op=ALU.mult,
-            )
+            if c % 4 == 1:
+                for g in range(KVH):
+                    nc.scalar.activation(
+                        out=o_sb[:, g, :], in_=of_chunk[c]["o_sum"][:, g, :], func=ACT.Copy,
+                        scale=of_chunk[c]["inverse"][:, g : g + 1],
+                    )
+            else:
+                nc.vector.tensor_tensor(
+                    out=o_sb[:], in0=of_chunk[c]["o_sum"][:],
+                    in1=of_chunk[c]["inverse"].unsqueeze(2).to_broadcast([P, KVH, D]), op=ALU.mult,
+                )
             chunk_rows = out_rows[c * CH : (c + 1) * CH, :].rearrange("i (g h d) -> h i g d", g=KVH, h=R)
             for h in range(R):
                 nc.sync.dma_start(out=chunk_rows[h], in_=o_sb[h * CH : (h + 1) * CH, :, :])
@@ -543,18 +555,20 @@ def tile_localgqattention_pb_kernel(tc, q_rot, k_rot, x, wv, out):
             copies = (nc.scalar.copy, nc.vector.tensor_copy)
             for n in range(T // P):
                 lay_k(copies[n % 2], n, turn_k(n))
-            for g in range(KVH):
-                lay_q(copies[g % 2], 0, g, turn_q(0, g))
+            for g in range(0, KVH, 2):
+                lay_q(copies[g // 2], 0, g, turn_q(0, g))
             load_q(4)
 
             lead = 2
-            prep = [("rows", n, half) for n in range(KVH + PACK) for half in range(2)] + [None]
+            prep = []
+            for r in range(2 * (KVH + PACK)):
+                prep.append((r - lead, ("rows", r // 2, r % 2)))
             for g in range(KVH):
-                prep += [("v", 0, g), ("rows", KVH + PACK + g // 2, g % 2)]
-            for n in range(KVH + PACK + 2, KVH + 2 * PACK):
-                prep += [("rows", n, 0), None, ("rows", n, 1), None]
+                prep.append((15 + 2 * g, ("v", 0, g)))
+            for r in range(2 * PACK):
+                prep.append((16 + r * 4 // 2, ("rows", KVH + PACK + r // 2, r % 2)))
             for g in range(KVH):
-                prep += [("v", 1, g), None]
+                prep.append((32 + 2 * g, ("v", 1, g)))
             due = []
             to_quantise = []
             weighed = 0
@@ -567,11 +581,7 @@ def tile_localgqattention_pb_kernel(tc, q_rot, k_rot, x, wv, out):
                 for fn in of_step.get((step, what), []):
                     fn()
 
-            for k in range(len(prep)):
-                piece = prep[k]
-                at = k - lead
-                if piece is None:
-                    continue
+            for at, piece in prep:
                 if piece[0] == "rows":
                     n, half = piece[1], piece[2]
                     later(at, "T", lambda n=n, half=half: turn_rows(row_op(n), half))
@@ -593,20 +603,21 @@ def tile_localgqattention_pb_kernel(tc, q_rot, k_rot, x, wv, out):
                             for j in range(4):
                                 later(at + 1, "V quantise", lambda j=j: advance_roll(j))
             for n in range(1, T // P):
-                for g in range(KVH):
-                    at = 4 * (n - 1) + g + 2
+                for g in range(0, KVH, 2):
+                    at = 2 + (2 * n - 2 + g // 2) * 4 // 2
+                    assert at <= 8 * n - 3
                     later(at, "plain", lambda n=n, g=g: turn_q_keep(n, g))
                     on_s = False
                     later(at, "S copy" if on_s else "V copy", lambda n=n, g=g, on_s=on_s: lay_q(nc.scalar.copy if on_s else nc.vector.tensor_copy, n, g, q_bank[n, g]))
-                    if g == KVH - 1 and n + 4 < T // P:
+                    if g == KVH - 2 and n + 4 < T // P:
                         later(at, "V copy", lambda n=n: load_q(n + 4))
             for quad in range(4):
-                at = 8 * quad + 29
-                later(at - 2, "plain", lambda quad=quad: score_old(quad, 0))
-                later(at, "plain", lambda quad=quad: score_old(quad, 1))
-                later(at, "V copy", lambda quad=quad: old_peak(quad))
-                later(at, "S copy", lambda quad=quad: old_copy(quad))
-                later(at + 1, "V early", lambda quad=quad: negate_old(quad))
+                at = 8 * quad
+                later(at + 29, "plain", lambda quad=quad: score_old(quad, 0))
+                later(at + 29, "plain", lambda quad=quad: score_old(quad, 1))
+                later(at + 29, "V copy", lambda quad=quad: old_peak(quad))
+                later(at + 29 + 1, "S copy", lambda quad=quad: old_copy(quad))
+                later(at + 29 + 1, "V early", lambda quad=quad: negate_old(quad))
 
             for i in range(-lead, PAIRS + 4):
                 jobs = []
@@ -635,6 +646,8 @@ def tile_localgqattention_pb_kernel(tc, q_rot, k_rot, x, wv, out):
                 to_quantise = jobs
                 if 0 <= i + 1 < PAIRS:
                     set_shift(i + 1)
+                if i >= 4 and i % 4 == 0 and i // 2 <= CHUNKS:
+                    invert(i // 2 - 1)
                 for c in done:
                     finish(c)
                     if FULL <= c < CHUNKS - 4:
@@ -642,7 +655,5 @@ def tile_localgqattention_pb_kernel(tc, q_rot, k_rot, x, wv, out):
                 run_now(i, "V quantise")
                 run_now(i, "V copy")
                 run_now(i, "S copy")
-                if i >= 2 and i % 2 == 0 and i // 2 - 1 < CHUNKS:
-                    invert(i // 2 - 1)
                 if 0 <= i < 2 * PACK and i % 2 == 0:
                     load_x(PACK + i // 2)

@@ -38,6 +38,9 @@ PAIRS = CHUNKS * KVH // 2
 SCALE = 1.0 / math.sqrt(D)
 MASKED = -1.0e30
 
+POOLS = [(16, 17, 18, 19), (20, 21, 22, 23), (24, 25, 26, 27), (28, 29), (30,), (31,)]
+POOL_OF = {c: n for n in range(len(POOLS)) for c in POOLS[n]}
+
 FLOPS = 2 * T * HID * KVH * D + 2 * 2 * (KVH * R) * D * (W * W + W * 2 * W)
 
 
@@ -53,7 +56,7 @@ def tile_localgqattention_pb_kernel(tc, q_rot, k_rot, x, wv, out):
     ) as rows_pool, tc.tile_pool(name="qraw", bufs=4) as qraw_pool, tc.tile_pool(
         name="stage", bufs=3
     ) as stage, tc.tile_pool(name="xq", bufs=6) as xq_pool, tc.tile_pool(
-        name="packed", bufs=22, reuse_waits="tile"
+        name="packed", bufs=20, reuse_waits="tile"
     ) as packed, tc.tile_pool(name="work", bufs=3, reuse_waits="tile") as work, tc.tile_pool(
         name="rest", bufs=2, reuse_waits="tile"
     ) as rest_pool, tc.tile_pool(name="store", bufs=5, reuse_waits="tile") as store_pool, tc.tile_pool(
@@ -110,24 +113,27 @@ def tile_localgqattention_pb_kernel(tc, q_rot, k_rot, x, wv, out):
         v_codes = keep.tile([P, S_PASSES, KVH * D], U32, align_bytes=64)
         v_scales = keep.tile([P, S_PASSES, KVH * D], U8, align_bytes=64)
         diag_codes = []
-        diag_scales = []
+        diag_scales = keep.tile([P, 4, KVH * D], U8, align_bytes=64)
         roll_codes = []
         roll_scales = []
         e_diag = []
         e_old = []
         for n in range(4):
             t_dc = keep.tile([P, KVH * D], U32, align_bytes=64, name="diag_codes%d" % n)
-            t_ds = keep.tile([P, KVH * D], U8, align_bytes=64, name="diag_scales%d" % n)
             t_rc = keep.tile([P, KVH * D], U32, align_bytes=64, name="roll_codes%d" % n)
             t_rs = keep.tile([P, KVH * D], U8, align_bytes=64, name="roll_scales%d" % n)
             t_ed = keep.tile([P, 2 * 2 * KVH * HQ], BF16, name="e_diag%d" % n)
-            t_eo = keep.tile([P, 2 * KVH * HQ], BF16, name="e_old%d" % n)
             nc.gpsimd.memset(t_ed[:], 0.0)
             diag_codes.append(t_dc)
-            diag_scales.append(t_ds)
             roll_codes.append(t_rc)
             roll_scales.append(t_rs)
             e_diag.append(t_ed)
+        old_planes = []
+        for n in range(4):
+            t_op = keep.tile([P, 4, KVH * D], U8, align_bytes=64, name="old_planes%d" % n)
+            old_planes.append(t_op)
+        for n in range(2):
+            t_eo = keep.tile([P, 2 * KVH * HQ], BF16, name="e_old%d" % n)
             e_old.append(t_eo)
         e_row = []
         for n in range(6):
@@ -136,11 +142,11 @@ def tile_localgqattention_pb_kernel(tc, q_rot, k_rot, x, wv, out):
         nc.gpsimd.memset(v_scales[:].rearrange("p s f -> p (s f)").bitcast(U32), 0)
         for n in range(4):
             nc.gpsimd.memset(diag_codes[n][:], 0)
-            nc.gpsimd.memset(diag_scales[n][:].bitcast(U32), 0)
+            nc.gpsimd.memset(diag_scales[:, n, :].bitcast(U32), 0)
         for n in range(6):
             nc.gpsimd.memset(e_row[n][:], 0.0)
         for n in range(4):
-            nc.gpsimd.memset(e_old[n][:], 0.0)
+            nc.gpsimd.memset(old_planes[n][:].rearrange("p j f -> p (j f)").bitcast(U32), 0)
 
         def load_rows(in_):
             t_rows = rows_pool.tile([P, HID], BF16, name="rows")
@@ -218,7 +224,13 @@ def tile_localgqattention_pb_kernel(tc, q_rot, k_rot, x, wv, out):
         def make_diag():
             for quad in range(4):
                 for g in range(KVH):
-                    move(diag_codes[quad], diag_scales[quad], 4 * g, 0, 4 * quad, 4, slice(g * D, (g + 1) * D))
+                    move(diag_codes[quad], diag_scales[:, quad, :], 4 * g, 0, 4 * quad, 4, slice(g * D, (g + 1) * D))
+
+        def make_old(b):
+            nc.sync.dma_start(
+                out=old_planes[b][b : P : QUAD].rearrange("p j f -> p (j f)").bitcast(I32),
+                in_=diag_scales[b : P : QUAD].rearrange("p j f -> p (j f)").bitcast(I32),
+            )
 
         def make_roll():
             for n in range(4):
@@ -419,7 +431,7 @@ def tile_localgqattention_pb_kernel(tc, q_rot, k_rot, x, wv, out):
                     if c >= FULL:
                         b = c % 4
                         soften_some(
-                            diag_view(e_old[b], 1)[:, 0, :, g, b * HC : (b + 1) * HC],
+                            diag_view(e_old[POOL_OF[c] % 2], 1)[:, 0, :, g, b * HC : (b + 1) * HC],
                             of_quad[(c - FULL) // 4]["scores"][:, b, g, :].rearrange("q (u c) -> q u c", u=2),
                             c, g, 1,
                         )
@@ -444,8 +456,8 @@ def tile_localgqattention_pb_kernel(tc, q_rot, k_rot, x, wv, out):
                 units = [words[:, j * 2 * P : (j + 1) * 2 * P] for j in range(c // 4 + 1)]
                 return [units[n : n + 2] for n in range(0, len(units), 2)]
             jobs = [[e_row[2 * (i % 3) + t][:].bitcast(F32) for t in range(2)]]
-            if c >= FULL and half == 1:
-                jobs.append([e_old[c % 4][:].bitcast(F32)])
+            if c >= FULL and half == 1 and c == POOLS[POOL_OF[c]][-1]:
+                jobs.append([e_old[POOL_OF[c] % 2][:].bitcast(F32)])
             return jobs
 
         def flip_e(c, units):
@@ -472,10 +484,12 @@ def tile_localgqattention_pb_kernel(tc, q_rot, k_rot, x, wv, out):
                 out=codes[:, 0 : n * P].bitcast(FP8X4), scales=scales[:, 0 : n * P],
                 in_=job["grouped"][:, 0 : n * P * PACK],
             )
-            for m in range(n):
-                of_chunk[job["c"]]["units"].append(
-                    (codes[:, m * P : (m + 1) * P], scales[:, m * P : (m + 1) * P])
-                )
+            units = [(codes[:, m * P : (m + 1) * P], scales[:, m * P : (m + 1) * P]) for m in range(n)]
+            if job["c"] >= FULL and n == 1:
+                for c in POOLS[POOL_OF[job["c"]]]:
+                    of_chunk[c]["old"] = units[0]
+            else:
+                of_chunk[job["c"]]["units"] += units
 
         def mx(out_ap, unit, codes, scales, start, stop):
             nc.tensor.matmul_mx(
@@ -489,11 +503,11 @@ def tile_localgqattention_pb_kernel(tc, q_rot, k_rot, x, wv, out):
             flat = o_sum[:].rearrange("p g d -> p (g d)")
             if c < DIAG:
                 for j in range(len(units)):
-                    mx(flat, units[j], diag_codes[j][:], diag_scales[j][:], j == 0, j == len(units) - 1)
+                    mx(flat, units[j], diag_codes[j][:], diag_scales[:, j, :], j == 0, j == len(units) - 1)
             else:
                 if c >= FULL:
-                    quad = (c - FULL) // 4
-                    mx(flat, units[4], diag_codes[quad][:], diag_scales[quad][:], True, False)
+                    quad, b = (c - FULL) // 4, c % 4
+                    mx(flat, of_chunk[c]["old"], diag_codes[quad][:], old_planes[b][:, quad, :], True, False)
                     codes, scales = roll_codes[c % 4][:], roll_scales[c % 4][:]
                 else:
                     codes, scales = v_codes[:, 0, :], v_scales[:, 0, :]
@@ -599,6 +613,8 @@ def tile_localgqattention_pb_kernel(tc, q_rot, k_rot, x, wv, out):
                         if sp == 0:
                             later(at + 1, "V quantise", make_diag)
                             later(at + 1, "V quantise", make_roll)
+                            for b in range(4):
+                                later(at + 3, "V quantise", lambda b=b: make_old(b))
                         else:
                             for j in range(4):
                                 later(at + 1, "V quantise", lambda j=j: advance_roll(j))
@@ -626,7 +642,7 @@ def tile_localgqattention_pb_kernel(tc, q_rot, k_rot, x, wv, out):
                         jobs.append(flip_e((i - 1) // 2, units))
                 run_now(i, "T")
                 done = []
-                if weighed < CHUNKS and i >= max(2 * weighed + 4, 27 + 5 * weighed // 4):
+                if weighed < CHUNKS and i >= max(2 * (POOLS[POOL_OF[weighed]][-1] if weighed >= FULL else weighed) + 4, 27 + 5 * weighed // 4):
                     weigh(weighed)
                     done.append(weighed)
                     weighed += 1

@@ -61,9 +61,7 @@ def tile_localgqattention_pb_kernel(tc, q_rot, k_rot, x, wv, out):
         name="rest", bufs=2, reuse_waits="tile"
     ) as rest_pool, tc.tile_pool(name="store", bufs=5, reuse_waits="tile") as store_pool, tc.tile_pool(
         name="stat", bufs=16, reuse_waits="tile"
-    ) as stat, tc.psum_pool(name="score", bufs=4, reuse_waits="tile") as score_pool, tc.psum_pool(
-        name="flip", bufs=3, reuse_waits="tile"
-    ) as flip, tc.psum_pool(name="osum", bufs=1, reuse_waits="tile") as osum:
+    ) as stat, tc.psum_pool(name="banks", bufs=8, reuse_waits="tile") as banks_pool:
         warm = const.tile([P, 1], F32)
         nc.vector.memset(warm[:], 0.0)
         nc.scalar.activation(out=warm[:], in_=warm[:], func=ACT.Exp)
@@ -159,7 +157,7 @@ def tile_localgqattention_pb_kernel(tc, q_rot, k_rot, x, wv, out):
             q_raw[n] = t_q
 
         def turn_rows(op, half):
-            bank = flip.tile([P, 4, P], F32, tag="flip")
+            bank = banks_pool.tile([P, 4, P], F32, tag="bank")
             words = op["rows"][:].bitcast(F32)
             for n in range(4):
                 first = (4 * half + n) * P
@@ -180,7 +178,7 @@ def tile_localgqattention_pb_kernel(tc, q_rot, k_rot, x, wv, out):
             nc.vector.quantize_mx(out=op["codes"].bitcast(FP8X4), scales=op["scales"], in_=op["grouped"][:])
 
         def project(sp, g):
-            bank = flip.tile([P, PACK, D], F32, tag="flip")
+            bank = banks_pool.tile([P, PACK, D], F32, tag="bank")
             for t in range(PACK):
                 for kp in range(X_PASSES):
                     cols = slice(kp * P, (kp + 1) * P)
@@ -242,7 +240,7 @@ def tile_localgqattention_pb_kernel(tc, q_rot, k_rot, x, wv, out):
             move(roll_codes[j % 4], roll_scales[j % 4], first, 1, first, j + 1 - first, slice(0, KVH * D))
 
         def turn_k(n):
-            bank = flip.tile([P, KVH, P], BF16, tag="flip")
+            bank = banks_pool.tile([P, KVH, P], BF16, tag="bank")
             for g in range(KVH):
                 nc.tensor.matmul(
                     out=bank[:, g, :], lhsT=k_raw[:, n, g * D : (g + 1) * D], rhs=ident_bf[:], start=True, stop=True
@@ -259,17 +257,15 @@ def tile_localgqattention_pb_kernel(tc, q_rot, k_rot, x, wv, out):
                 ),
             )
 
-        def turn_q(n, g):
-            bank = flip.tile([P, 2 * R, P], BF16, tag="flip")
-            for h in range(2 * R):
+        def turn_q(n, g, half):
+            if half == 0:
+                bank = banks_pool.tile([P, 2 * R, P], BF16, tag="bank")
+                q_bank[n, g] = bank
+            for h in range(half * R, (half + 1) * R):
                 first = (g * R + h) * D
                 nc.tensor.matmul(
-                    out=bank[:, h, :], lhsT=q_raw[n][:, first : first + D], rhs=ident_bf[:], start=True, stop=True
+                    out=q_bank[n, g][:, h, :], lhsT=q_raw[n][:, first : first + D], rhs=ident_bf[:], start=True, stop=True
                 )
-            return bank
-
-        def turn_q_keep(n, g):
-            q_bank[n, g] = turn_q(n, g)
 
         def row_op(n):
             if n < KVH:
@@ -290,7 +286,7 @@ def tile_localgqattention_pb_kernel(tc, q_rot, k_rot, x, wv, out):
 
         def score_old(quad, part):
             if part == 0:
-                bank = flip.tile([P, 4, KVH, CH], F32, tag="flip")
+                bank = banks_pool.tile([P, 4, KVH, CH], F32, tag="bank")
                 nc.tensor.matmul(
                     out=bank[:].rearrange("p c g j -> p (c g j)"), lhsT=spread_cols,
                     rhs=old_bias[:].rearrange("k n j -> k (n j)"), start=True, stop=False,
@@ -337,28 +333,36 @@ def tile_localgqattention_pb_kernel(tc, q_rot, k_rot, x, wv, out):
                     "sums": of_chunk["sums"],
                     "units": [],
                 }
-            banks = []
+            j = c % FULL
+            live = (j + 1) * HC
             if c < FULL // 2:
-                both = score_pool.tile([P, 2, 2, P], F32, tag="score")
+                both = banks_pool.tile([P, 2, 2, P], F32, tag="bank")
                 of_both[i] = both
+                for t in range(2):
+                    g = 2 * half + t
+                    nc.tensor.matmul(
+                        out=both[:, t, :, 0:live], lhsT=qT[:, c, g].rearrange("d h i -> d (h i)"),
+                        rhs=kT[:, g, 0, :, 0:live], start=(t == 0), stop=False,
+                    )
+                nc.tensor.matmul(
+                    out=both[:, :, :, live - HC : live], lhsT=spread_cols,
+                    rhs=own_bias[:].unsqueeze(1).to_broadcast([P, 2, 2, HC]), start=False, stop=True,
+                )
+                of_pair[i] = [both[:, 0], both[:, 1]]
+                return
+            banks = []
             for t in range(2):
                 g = 2 * half + t
-                if c < FULL // 2:
-                    bank = both[:, t]
-                else:
-                    own = score_pool.tile([P, 2, 2 * P], F32, tag="score")
-                    bank = own[:]
+                own = banks_pool.tile([P, 2, 2 * P], F32, tag="bank")
+                bank = own[:]
                 lhsT = qT[:, c, g].rearrange("d h i -> d (h i)")
-                j = c % FULL
-                live = (j + 1) * HC
                 if c >= FULL and live < 2 * P:
                     nc.tensor.matmul(
                         out=bank[:, :, live : 2 * P], lhsT=lhsT, rhs=kT[:, g, 0, :, live : 2 * P],
                         start=True, stop=True,
                     )
-                wide = live
                 nc.tensor.matmul(
-                    out=bank[:, :, 0:wide], lhsT=lhsT, rhs=kT[:, g, c // FULL, :, 0:wide], start=True, stop=False
+                    out=bank[:, :, 0:live], lhsT=lhsT, rhs=kT[:, g, c // FULL, :, 0:live], start=True, stop=False
                 )
                 nc.tensor.matmul(
                     out=bank[:, :, live - HC : live], lhsT=spread_cols, rhs=own_bias[:], start=False, stop=True
@@ -461,7 +465,7 @@ def tile_localgqattention_pb_kernel(tc, q_rot, k_rot, x, wv, out):
             return jobs
 
         def flip_e(c, units):
-            bank = flip.tile([P, 2, 2, P], F32, tag="flip")
+            bank = banks_pool.tile([P, 2, 2, P], F32, tag="bank")
             for n in range(len(units)):
                 for u in range(2):
                     nc.tensor.transpose(bank[:, n, u, :], units[n][:, u * P : (u + 1) * P], ident32[:])
@@ -498,7 +502,7 @@ def tile_localgqattention_pb_kernel(tc, q_rot, k_rot, x, wv, out):
             )
 
         def weigh(c):
-            o_sum = osum.tile([P, KVH, D], F32)
+            o_sum = banks_pool.tile([P, KVH, D], F32, tag="bank")
             units = of_chunk[c]["units"]
             flat = o_sum[:].rearrange("p g d -> p (g d)")
             if c < DIAG:
@@ -518,17 +522,10 @@ def tile_localgqattention_pb_kernel(tc, q_rot, k_rot, x, wv, out):
 
         def finish(c):
             o_sb = store_pool.tile([P, KVH, D], F32, name="o_sb")
-            if c % 4 == 1:
-                for g in range(KVH):
-                    nc.scalar.activation(
-                        out=o_sb[:, g, :], in_=of_chunk[c]["o_sum"][:, g, :], func=ACT.Copy,
-                        scale=of_chunk[c]["inverse"][:, g : g + 1],
-                    )
-            else:
-                nc.vector.tensor_tensor(
-                    out=o_sb[:], in0=of_chunk[c]["o_sum"][:],
-                    in1=of_chunk[c]["inverse"].unsqueeze(2).to_broadcast([P, KVH, D]), op=ALU.mult,
-                )
+            nc.vector.tensor_tensor(
+                out=o_sb[:], in0=of_chunk[c]["o_sum"][:],
+                in1=of_chunk[c]["inverse"].unsqueeze(2).to_broadcast([P, KVH, D]), op=ALU.mult,
+            )
             chunk_rows = out_rows[c * CH : (c + 1) * CH, :].rearrange("i (g h d) -> h i g d", g=KVH, h=R)
             for h in range(R):
                 nc.sync.dma_start(out=chunk_rows[h], in_=o_sb[h * CH : (h + 1) * CH, :, :])
@@ -541,10 +538,10 @@ def tile_localgqattention_pb_kernel(tc, q_rot, k_rot, x, wv, out):
         q_bank = {}
         v_bank = {}
         with tc.manual_schedule():
-            for n in range(2):
+            for first, count in ((0, 1), (1, 3), (4, 4)):
                 nc.sync.dma_start(
-                    out=k_raw[:, 4 * n : 4 * n + 4, :],
-                    in_=k_rows[n * W : (n + 1) * W, :].rearrange("(n p) f -> p n f", p=P),
+                    out=k_raw[:, first : first + count, :],
+                    in_=k_rows[first * P : (first + count) * P, :].rearrange("(n p) f -> p n f", p=P),
                 )
             load_q(0)
             w_ops = []
@@ -570,7 +567,9 @@ def tile_localgqattention_pb_kernel(tc, q_rot, k_rot, x, wv, out):
             for n in range(T // P):
                 lay_k(copies[n % 2], n, turn_k(n))
             for g in range(0, KVH, 2):
-                lay_q(copies[g // 2], 0, g, turn_q(0, g))
+                turn_q(0, g, 0)
+                turn_q(0, g, 1)
+                lay_q(copies[g // 2], 0, g, q_bank[0, g])
             load_q(4)
 
             lead = 2
@@ -622,11 +621,11 @@ def tile_localgqattention_pb_kernel(tc, q_rot, k_rot, x, wv, out):
                 for g in range(0, KVH, 2):
                     at = 2 + (2 * n - 2 + g // 2) * 4 // 2
                     assert at <= 8 * n - 3
-                    later(at, "plain", lambda n=n, g=g: turn_q_keep(n, g))
-                    on_s = False
-                    later(at, "S copy" if on_s else "V copy", lambda n=n, g=g, on_s=on_s: lay_q(nc.scalar.copy if on_s else nc.vector.tensor_copy, n, g, q_bank[n, g]))
+                    later(at, "plain", lambda n=n, g=g: turn_q(n, g, 0))
+                    later(at + 1, "plain", lambda n=n, g=g: turn_q(n, g, 1))
+                    later(at + 1, "V copy", lambda n=n, g=g: lay_q(nc.vector.tensor_copy, n, g, q_bank[n, g]))
                     if g == KVH - 2 and n + 4 < T // P:
-                        later(at, "V copy", lambda n=n: load_q(n + 4))
+                        later(at + 1, "V copy", lambda n=n: load_q(n + 4))
             for quad in range(4):
                 at = 8 * quad
                 later(at + 29, "plain", lambda quad=quad: score_old(quad, 0))

@@ -120,12 +120,9 @@ def tile_localgqattention_pb_kernel(tc, q_rot, k_rot, x, wv, out):
             t_dc = keep.tile([P, KVH * D], U32, align_bytes=64, name="diag_codes%d" % n)
             t_rc = keep.tile([P, KVH * D], U32, align_bytes=64, name="roll_codes%d" % n)
             t_rs = keep.tile([P, KVH * D], U8, align_bytes=64, name="roll_scales%d" % n)
-            t_ed = keep.tile([P, 2 * 2 * KVH * HQ], BF16, name="e_diag%d" % n)
-            nc.gpsimd.memset(t_ed[:], 0.0)
             diag_codes.append(t_dc)
             roll_codes.append(t_rc)
             roll_scales.append(t_rs)
-            e_diag.append(t_ed)
         old_planes = []
         for n in range(4):
             t_op = keep.tile([P, 4, KVH * D], U8, align_bytes=64, name="old_planes%d" % n)
@@ -133,6 +130,10 @@ def tile_localgqattention_pb_kernel(tc, q_rot, k_rot, x, wv, out):
         for n in range(2):
             t_eo = keep.tile([P, 2 * KVH * HQ], BF16, name="e_old%d" % n)
             e_old.append(t_eo)
+        for n in range(2):
+            t_ed = keep.tile([P, 2 * 2 * KVH * HQ], BF16, name="e_diag%d" % n)
+            nc.vector.memset(t_ed[:].bitcast(U32), 0)
+            e_diag.append(t_ed)
         e_row = []
         for n in range(6):
             t_er = keep.tile([P, 4 * P], BF16, name="e_row%d" % n)
@@ -142,7 +143,7 @@ def tile_localgqattention_pb_kernel(tc, q_rot, k_rot, x, wv, out):
             nc.gpsimd.memset(diag_codes[n][:], 0)
             nc.gpsimd.memset(diag_scales[:, n, :].bitcast(U32), 0)
         for n in range(6):
-            nc.gpsimd.memset(e_row[n][:], 0.0)
+            nc.gpsimd.memset(e_row[n][:].bitcast(U32), 0)
         for n in range(4):
             nc.gpsimd.memset(old_planes[n][:].rearrange("p j f -> p (j f)").bitcast(U32), 0)
 
@@ -414,7 +415,7 @@ def tile_localgqattention_pb_kernel(tc, q_rot, k_rot, x, wv, out):
                 g = 2 * half + t
                 bank = of_pair[i][t]
                 if c < DIAG:
-                    e = diag_view(e_diag[c % 4], 2)
+                    e = diag_view(e_diag[c % 2], 2)
                     quads, rest = (c + 1) // 4, (c + 1) % 4
                     if quads > 0:
                         soften_some(
@@ -456,7 +457,7 @@ def tile_localgqattention_pb_kernel(tc, q_rot, k_rot, x, wv, out):
             if c < DIAG:
                 if half == 0:
                     return []
-                words = e_diag[c % 4][:].bitcast(F32)
+                words = e_diag[c % 2][:].bitcast(F32)
                 units = [words[:, j * 2 * P : (j + 1) * 2 * P] for j in range(c // 4 + 1)]
                 return [units[n : n + 2] for n in range(0, len(units), 2)]
             jobs = [[e_row[2 * (i % 3) + t][:].bitcast(F32) for t in range(2)]]

@@ -138,14 +138,14 @@ def tile_localgqattention_pb_kernel(tc, q_rot, k_rot, x, wv, out):
         for n in range(6):
             t_er = keep.tile([P, 4 * P], BF16, name="e_row%d" % n)
             e_row.append(t_er)
-        nc.gpsimd.memset(v_scales[:].rearrange("p s f -> p (s f)").bitcast(U32), 0)
-        for n in range(4):
-            nc.gpsimd.memset(diag_codes[n][:], 0)
-            nc.gpsimd.memset(diag_scales[:, n, :].bitcast(U32), 0)
         for n in range(6):
-            nc.gpsimd.memset(e_row[n][:].bitcast(U32), 0)
+            nc.vector.memset(e_row[n][:].bitcast(U32), 0)
+        to_zero = [v_scales[:].rearrange("p s f -> p (s f)").bitcast(U32)]
+        to_zero.append(diag_scales[:].rearrange("p j f -> p (j f)").bitcast(U32))
         for n in range(4):
-            nc.gpsimd.memset(old_planes[n][:].rearrange("p j f -> p (j f)").bitcast(U32), 0)
+            to_zero.append(diag_codes[n][:])
+        for n in range(4):
+            to_zero.append(old_planes[n][:].rearrange("p j f -> p (j f)").bitcast(U32))
 
         def load_rows(in_):
             t_rows = rows_pool.tile([P, HID], BF16, name="rows")
@@ -627,6 +627,8 @@ def tile_localgqattention_pb_kernel(tc, q_rot, k_rot, x, wv, out):
                     later(at + 1, "V copy", lambda n=n, g=g: lay_q(nc.vector.tensor_copy, n, g, q_bank[n, g]))
                     if g == KVH - 2 and n + 4 < T // P:
                         later(at + 1, "V copy", lambda n=n: load_q(n + 4))
+            for n in range(len(to_zero)):
+                later(n // 2 - lead + 0, "V copy", lambda n=n: nc.vector.memset(to_zero[n], 0))
             for quad in range(4):
                 at = 8 * quad
                 later(at + 29, "plain", lambda quad=quad: score_old(quad, 0))

@@ -73,27 +73,27 @@ def tile_localgqattention_pb_kernel(tc, q_rot, k_rot, x, wv, out):
 
         spread = const.tile([P, R, CH], BF16)
         nc.vector.tensor_copy(out=spread[:], in_=ident_bf[:, 0:CH].unsqueeze(1).to_broadcast([P, R, CH]))
-        own_f32 = const.tile([P, P], F32)
+        own_f32 = const.tile([P, CH], F32)
         nc.gpsimd.memset(own_f32[:], 0.0)
         nc.gpsimd.affine_select(
             out=own_f32[:], in_=own_f32[:], compare_op=ALU.is_ge, fill=MASKED,
-            base=0, pattern=[[-1, P]], channel_multiplier=1,
+            base=0, pattern=[[-1, CH]], channel_multiplier=1,
         )
         own_bias = const.tile([P, 2, HC], BF16)
         nc.vector.tensor_copy(
             out=own_bias[:].rearrange("k u (p e) -> k u p e", e=2),
-            in_=own_f32[:, 0:CH].rearrange("k (p u e) -> k u p e", u=2, e=2),
+            in_=own_f32[:].rearrange("k (p u e) -> k u p e", u=2, e=2),
         )
-        old_f32 = const.tile([P, P], F32)
+        old_f32 = const.tile([P, CH], F32)
         nc.gpsimd.memset(old_f32[:], 0.0)
         nc.gpsimd.affine_select(
             out=old_f32[:], in_=old_f32[:], compare_op=ALU.is_ge, fill=MASKED,
-            base=0, pattern=[[1, P]], channel_multiplier=-1,
+            base=0, pattern=[[1, CH]], channel_multiplier=-1,
         )
         old_one = const.tile([P, 2, HC], BF16)
         nc.vector.tensor_copy(
             out=old_one[:].rearrange("k u (p e) -> k u p e", e=2),
-            in_=old_f32[:, 0:CH].rearrange("k (p u e) -> k u p e", u=2, e=2),
+            in_=old_f32[:].rearrange("k (p u e) -> k u p e", u=2, e=2),
         )
         old_bias = const.tile([P, FULL, CH], BF16)
         nc.vector.tensor_copy(
@@ -140,12 +140,9 @@ def tile_localgqattention_pb_kernel(tc, q_rot, k_rot, x, wv, out):
             e_row.append(t_er)
         for n in range(6):
             nc.vector.memset(e_row[n][:].bitcast(U32), 0)
-        to_zero = [v_scales[:].rearrange("p s f -> p (s f)").bitcast(U32)]
-        to_zero.append(diag_scales[:].rearrange("p j f -> p (j f)").bitcast(U32))
-        for n in range(4):
-            to_zero.append(diag_codes[n][:])
-        for n in range(4):
-            to_zero.append(old_planes[n][:].rearrange("p j f -> p (j f)").bitcast(U32))
+        nc.vector.memset(v_scales[:].rearrange("p s f -> p (s f)").bitcast(U32), 0)
+        zeros = diag_scales[:].rearrange("p j f -> p (j f)").bitcast(I32)
+        nc.vector.memset(diag_scales[:].rearrange("p j f -> p (j f)").bitcast(U32), 0)
 
         def load_rows(in_):
             t_rows = rows_pool.tile([P, HID], BF16, name="rows")
@@ -220,9 +217,8 @@ def tile_localgqattention_pb_kernel(tc, q_rot, k_rot, x, wv, out):
                     in_=v_scales[b : b + count, sp, cols].bitcast(I32),
                 )
 
-        def make_diag():
-            for quad in range(4):
-                for g in range(KVH):
+        def make_diag(quad):
+            for g in range(KVH):
                     move(diag_codes[quad], diag_scales[:, quad, :], 4 * g, 0, 4 * quad, 4, slice(g * D, (g + 1) * D))
 
         def make_old(b):
@@ -231,8 +227,8 @@ def tile_localgqattention_pb_kernel(tc, q_rot, k_rot, x, wv, out):
                 in_=diag_scales[b : P : QUAD].rearrange("p j f -> p (j f)").bitcast(I32),
             )
 
-        def make_roll():
-            for n in range(4):
+        def make_roll(n):
+            if True:
                 nc.sync.dma_start(out=roll_codes[n][:].bitcast(I32), in_=v_codes[:, 0, :].bitcast(I32))
                 nc.sync.dma_start(out=roll_scales[n][:].bitcast(I32), in_=v_scales[:, 0, :].bitcast(I32))
 
@@ -441,14 +437,17 @@ def tile_localgqattention_pb_kernel(tc, q_rot, k_rot, x, wv, out):
                             c, g, 1,
                         )
 
-        def invert(c):
+        def total(c):
             sums = of_chunk[c]["sums"]
+            if c >= FULL or 4 <= c < DIAG:
+                seats = 1 if c == DIAG - 1 else 2
+                nc.vector.tensor_tensor(
+                    out=sums[:, 0, 0:seats], in0=sums[:, 0, 0:seats], in1=sums[:, 1, 0:seats], op=ALU.add
+                )
+
+        def invert(c):
             inverse = stat.tile([P, 2, KVH], F32, name="inverse")
-            if c >= FULL or c < DIAG and c >= 4 and c % 4 == 1:
-                nc.gpsimd.tensor_tensor(out=sums[:, 0], in0=sums[:, 0], in1=sums[:, 1], op=ALU.add)
-            elif c < DIAG and c >= 4:
-                nc.gpsimd.tensor_tensor(out=sums[:, 0, 0, :], in0=sums[:, 0, 0, :], in1=sums[:, 1, 0, :], op=ALU.add)
-            nc.vector.reciprocal(out=inverse[:], in_=sums[:, 0])
+            nc.vector.reciprocal(out=inverse[:], in_=of_chunk[c]["sums"][:, 0])
             of_chunk[c - 1]["inverse"] = inverse[:, 0]
             of_chunk[c]["inverse"] = inverse[:, 1]
 
@@ -611,10 +610,10 @@ def tile_localgqattention_pb_kernel(tc, q_rot, k_rot, x, wv, out):
                     if g == KVH - 1:
                         later(at + 1, "V quantise", lambda sp=sp: quantise_v(sp))
                         if sp == 0:
-                            later(at + 1, "V quantise", make_diag)
-                            later(at + 1, "V quantise", make_roll)
-                            for b in range(4):
-                                later(at + 3, "V quantise", lambda b=b: make_old(b))
+                            for n in range(4):
+                                later(at + 1 + (0, 1, 6, 9)[n], "V quantise", lambda n=n: make_diag(n))
+                                later(at + 3 + n, "V quantise", lambda n=n: make_roll(n))
+                                later(at + 12 + n, "V quantise", lambda n=n: make_old(n))
                         else:
                             for j in range(4):
                                 later(at + 1, "V quantise", lambda j=j: advance_roll(j))
@@ -627,8 +626,11 @@ def tile_localgqattention_pb_kernel(tc, q_rot, k_rot, x, wv, out):
                     later(at + 1, "V copy", lambda n=n, g=g: lay_q(nc.vector.tensor_copy, n, g, q_bank[n, g]))
                     if g == KVH - 2 and n + 4 < T // P:
                         later(at + 1, "V copy", lambda n=n: load_q(n + 4))
-            for n in range(len(to_zero)):
-                later(n // 2 - lead + 0, "V copy", lambda n=n: nc.vector.memset(to_zero[n], 0))
+            for n in range(4):
+                later(8 + n, "V copy", lambda n=n: nc.sync.dma_start(out=diag_codes[n][:].bitcast(I32), in_=zeros))
+                later(8 + n, "V copy", lambda n=n: nc.sync.dma_start(
+                    out=old_planes[n][:].rearrange("p j f -> p (j f)").bitcast(I32), in_=zeros
+                ))
             for quad in range(4):
                 at = 8 * quad
                 later(at + 29, "plain", lambda quad=quad: score_old(quad, 0))
@@ -658,6 +660,8 @@ def tile_localgqattention_pb_kernel(tc, q_rot, k_rot, x, wv, out):
                     score(i + 2)
                 if 0 <= i + 1 < PAIRS:
                     peak(i + 1)
+                if i >= 4 and i % 4 == 0 and i // 2 <= CHUNKS:
+                    total(i // 2 - 1)
                 run_now(i, "V early")
                 for job in to_quantise:
                     quantise(job)

@@ -538,11 +538,14 @@ def tile_localgqattention_pb_kernel(tc, q_rot, k_rot, x, wv, out):
         q_bank = {}
         v_bank = {}
         with tc.manual_schedule():
-            for first, count in ((0, 1), (1, 3), (4, 4)):
+            def load_k(first, count):
                 nc.sync.dma_start(
                     out=k_raw[:, first : first + count, :],
                     in_=k_rows[first * P : (first + count) * P, :].rearrange("(n p) f -> p n f", p=P),
                 )
+
+            load_k(0, 1)
+            load_k(1, 3)
             load_q(0)
             w_ops = []
             x_ops = []
@@ -558,13 +561,22 @@ def tile_localgqattention_pb_kernel(tc, q_rot, k_rot, x, wv, out):
                 in_ = x_rows[n // PACK * K_PASS : (n // PACK + 1) * K_PASS, :].rearrange("(p t) k -> t p k", t=PACK)
                 x_ops.append({"rows": load_rows(in_[n % PACK])})
 
-            for n in range(PACK):
-                load_x(n)
+            load_k(4, 4)
             load_q(2)
+            load_x(0)
+            load_x(1)
             load_q(3)
+            load_x(2)
+            load_x(3)
+
+            warm_bank = banks_pool.tile([P, PACK, P], F32, tag="bank")
+            for n in range(9):
+                nc.tensor.matmul(
+                    out=warm_bank[:, n % PACK, :], lhsT=ident_bf[:], rhs=ident_bf[:], start=True, stop=True
+                )
 
             copies = (nc.scalar.copy, nc.vector.tensor_copy)
-            for n in range(T // P):
+            for n in range(4):
                 lay_k(copies[n % 2], n, turn_k(n))
             for g in range(0, KVH, 2):
                 turn_q(0, g, 0)
@@ -626,6 +638,14 @@ def tile_localgqattention_pb_kernel(tc, q_rot, k_rot, x, wv, out):
                     later(at + 1, "V copy", lambda n=n, g=g: lay_q(nc.vector.tensor_copy, n, g, q_bank[n, g]))
                     if g == KVH - 2 and n + 4 < T // P:
                         later(at + 1, "V copy", lambda n=n: load_q(n + 4))
+            k_bank = {}
+
+            def turn_k_keep(n):
+                k_bank[n] = turn_k(n)
+
+            for n in range(4, T // P):
+                later(2 * n - 3, "plain", lambda n=n: turn_k_keep(n))
+                later(2 * n - 3, ("S copy", "V copy")[n % 2], lambda n=n: lay_k(copies[n % 2], n, k_bank[n]))
             for n in range(4):
                 later(8 + n, "V copy", lambda n=n: nc.sync.dma_start(out=diag_codes[n][:].bitcast(I32), in_=zeros))
                 later(8 + n, "V copy", lambda n=n: nc.sync.dma_start(

import math

import concourse.mybir as mybir
from concourse.masks import make_identity

F32 = mybir.dt.float32
BF16 = mybir.dt.bfloat16
U32 = mybir.dt.uint32
I32 = mybir.dt.int32
U8 = mybir.dt.uint8
FP8X4 = mybir.dt.float8_e4m3fn_x4
ALU = mybir.AluOpType
ACT = mybir.ActivationFunctionType
AXIS_X = mybir.AxisListType.X
AXIS_XY = mybir.AxisListType.XY

P = 128
PACK = 4
K_PASS = P * PACK
QUAD = 32
BLK = 8

T = 1024
HID = 2048
KVH = 4
R = 4
D = 128
W = 512
CH = P // R
CHUNKS = T // CH
FULL = W // CH
DIAG = 8
X_PASSES = HID // K_PASS
S_PASSES = T // K_PASS
HC = CH // 2
HQ = 2 * QUAD
PAIRS = CHUNKS * KVH // 2
SCALE = 1.0 / math.sqrt(D)
MASKED = -1.0e30

POOLS = [(16, 17, 18, 19), (20, 21, 22, 23), (24, 25, 26, 27), (28, 29), (30,), (31,)]
POOL_OF = {c: n for n in range(len(POOLS)) for c in POOLS[n]}

FLOPS = 2 * T * HID * KVH * D + 2 * 2 * (KVH * R) * D * (W * W + W * 2 * W)


def tile_localgqattention_pb_kernel(tc, q_rot, k_rot, x, wv, out):
    nc = tc.nc
    q_rows = q_rot.rearrange("b t h d -> (b t) (h d)")
    k_rows = k_rot.rearrange("b t h d -> (b t) (h d)")
    x_rows = x.rearrange("b t k -> (b t) k")
    out_rows = out.rearrange("b t f -> (b t) f")

    with tc.tile_pool(name="const", bufs=1) as const, tc.tile_pool(name="keep", bufs=1) as keep, tc.tile_pool(
        name="rows", bufs=8
    ) as rows_pool, tc.tile_pool(name="qraw", bufs=4) as qraw_pool, tc.tile_pool(
        name="stage", bufs=3
    ) as stage, tc.tile_pool(name="xq", bufs=6) as xq_pool, tc.tile_pool(
        name="packed", bufs=20, reuse_waits="tile"
    ) as packed, tc.tile_pool(name="work", bufs=3, reuse_waits="tile") as work, tc.tile_pool(
        name="rest", bufs=2, reuse_waits="tile"
    ) as rest_pool, tc.tile_pool(name="store", bufs=5, reuse_waits="tile") as store_pool, tc.tile_pool(
        name="stat", bufs=16, reuse_waits="tile"
    ) as stat, tc.psum_pool(name="banks", bufs=8, reuse_waits="tile") as banks_pool:
        warm = const.tile([P, 1], F32)
        nc.vector.memset(warm[:], 0.0)
        nc.scalar.activation(out=warm[:], in_=warm[:], func=ACT.Exp)

        ident_bf = const.tile([P, P], BF16)
        make_identity(nc, ident_bf[:])
        ident32 = const.tile([P, P], F32)
        make_identity(nc, ident32[:])

        spread = const.tile([P, R, CH], BF16)
        nc.vector.tensor_copy(out=spread[:], in_=ident_bf[:, 0:CH].unsqueeze(1).to_broadcast([P, R, CH]))
        own_f32 = const.tile([P, CH], F32)
        nc.gpsimd.memset(own_f32[:], 0.0)
        nc.gpsimd.affine_select(
            out=own_f32[:], in_=own_f32[:], compare_op=ALU.is_ge, fill=MASKED,
            base=0, pattern=[[-1, CH]], channel_multiplier=1,
        )
        own_bias = const.tile([P, 2, HC], BF16)
        nc.vector.tensor_copy(
            out=own_bias[:].rearrange("k u (p e) -> k u p e", e=2),
            in_=own_f32[:].rearrange("k (p u e) -> k u p e", u=2, e=2),
        )
        old_f32 = const.tile([P, CH], F32)
        nc.gpsimd.memset(old_f32[:], 0.0)
        nc.gpsimd.affine_select(
            out=old_f32[:], in_=old_f32[:], compare_op=ALU.is_ge, fill=MASKED,
            base=0, pattern=[[1, CH]], channel_multiplier=-1,
        )
        old_one = const.tile([P, 2, HC], BF16)
        nc.vector.tensor_copy(
            out=old_one[:].rearrange("k u (p e) -> k u p e", e=2),
            in_=old_f32[:].rearrange("k (p u e) -> k u p e", u=2, e=2),
        )
        old_bias = const.tile([P, FULL, CH], BF16)
        nc.vector.tensor_copy(
            out=old_bias[:],
            in_=old_one[:].rearrange("k u c -> k (u c)").unsqueeze(1).to_broadcast([P, FULL, CH]),
        )
        spread_cols = spread[:].rearrange("k h i -> k (h i)")

        kT = keep.tile([P, KVH, S_PASSES, 2, 2 * P], BF16)
        qT = keep.tile([P, CHUNKS, KVH, R, CH], BF16)
        k_raw = keep.tile([P, T // P, KVH * D], BF16)
        w_codes = keep.tile([P, KVH, X_PASSES * D], U32, align_bytes=64)
        w_scales = keep.tile([P, KVH, X_PASSES * D], U8, align_bytes=64)
        v_grouped = keep.tile([P, KVH, D, PACK], BF16, align_bytes=64)
        v_codes = keep.tile([P, S_PASSES, KVH * D], U32, align_bytes=64)
        v_scales = keep.tile([P, S_PASSES, KVH * D], U8, align_bytes=64)
        diag_codes = []
        diag_scales = keep.tile([P, 4, KVH * D], U8, align_bytes=64)
        roll_codes = []
        roll_scales = []
        e_diag = []
        e_old = []
        for n in range(4):
            t_dc = keep.tile([P, KVH * D], U32, align_bytes=64, name="diag_codes%d" % n)
            t_rc = keep.tile([P, KVH * D], U32, align_bytes=64, name="roll_codes%d" % n)
            t_rs = keep.tile([P, KVH * D], U8, align_bytes=64, name="roll_scales%d" % n)
            diag_codes.append(t_dc)
            roll_codes.append(t_rc)
            roll_scales.append(t_rs)
        old_planes = []
        for n in range(4):
            t_op = keep.tile([P, 4, KVH * D], U8, align_bytes=64, name="old_planes%d" % n)
            old_planes.append(t_op)
        for n in range(2):
            t_eo = keep.tile([P, 2 * KVH * HQ], BF16, name="e_old%d" % n)
            e_old.append(t_eo)
        for n in range(2):
            t_ed = keep.tile([P, 2 * 2 * KVH * HQ], BF16, name="e_diag%d" % n)
            nc.vector.memset(t_ed[:].bitcast(U32), 0)
            e_diag.append(t_ed)
        e_row = []
        for n in range(6):
            t_er = keep.tile([P, 4 * P], BF16, name="e_row%d" % n)
            e_row.append(t_er)
        for n in range(6):
            nc.vector.memset(e_row[n][:].bitcast(U32), 0)
        nc.vector.memset(v_scales[:].rearrange("p s f -> p (s f)").bitcast(U32), 0)
        zeros = diag_scales[:].rearrange("p j f -> p (j f)").bitcast(I32)
        nc.vector.memset(diag_scales[:].rearrange("p j f -> p (j f)").bitcast(U32), 0)

        def load_rows(in_):
            t_rows = rows_pool.tile([P, HID], BF16, name="rows")
            nc.sync.dma_start(out=t_rows[:], in_=in_)
            return t_rows

        def load_q(n):
            t_q = qraw_pool.tile([P, KVH * R * D], BF16, name="q_raw")
            nc.sync.dma_start(out=t_q[:], in_=q_rows[n * P : (n + 1) * P, :])
            q_raw[n] = t_q

        def turn_rows(op, half):
            bank = banks_pool.tile([P, 4, P], F32, tag="bank")
            words = op["rows"][:].bitcast(F32)
            for n in range(4):
                first = (4 * half + n) * P
                nc.tensor.transpose(bank[:, n, :], words[:, first : first + P], ident32[:])
            op["bank"] = bank

        def lay_rows(op, half, copy):
            if half == 0:
                grouped = stage.tile([P, X_PASSES * P * PACK], BF16, align_bytes=64)
                op["grouped"] = grouped
            grouped32 = op["grouped"][:].bitcast(F32).rearrange("p (c r u) -> p c r u", c=X_PASSES, u=2)
            copy(
                out=grouped32[:, 2 * half : 2 * half + 2],
                in_=op["bank"][:].rearrange("p (c u) r -> p c r u", u=2),
            )

        def quantise_rows(op):
            nc.vector.quantize_mx(out=op["codes"].bitcast(FP8X4), scales=op["scales"], in_=op["grouped"][:])

        def project(sp, g):
            bank = banks_pool.tile([P, PACK, D], F32, tag="bank")
            for t in range(PACK):
                for kp in range(X_PASSES):
                    cols = slice(kp * P, (kp + 1) * P)
                    nc.tensor.matmul_mx(
                        out=bank[:, t, :],
                        lhsT=x_ops[PACK * sp + t]["codes"][:, cols].bitcast(FP8X4),
                        lhsT_scale=x_ops[PACK * sp + t]["scales"][:, cols],
                        rhs=w_codes[:, g, cols].bitcast(FP8X4),
                        rhs_scale=w_scales[:, g, cols],
                        start=(kp == 0),
                        stop=(kp == X_PASSES - 1),
                    )
            v_bank[g] = bank

        def lay_v(g, copy):
            copy(out=v_grouped[:, g, :, :], in_=v_bank[g][:].rearrange("p t d -> p d t"))

        def quantise_v(sp):
            nc.vector.quantize_mx(
                out=v_codes[:, sp, :].bitcast(FP8X4),
                scales=v_scales[:, sp, :],
                in_=v_grouped[:].rearrange("p g d t -> p (g d t)"),
            )

        def move(dst_codes, dst_scales, dst_block, sp, block, blocks, cols):
            nc.sync.dma_start(
                out=dst_codes[dst_block * BLK : (dst_block + blocks) * BLK, cols].bitcast(I32),
                in_=v_codes[block * BLK : (block + blocks) * BLK, sp, cols].bitcast(I32),
            )
            for quad in range(block // 4, (block + blocks - 1) // 4 + 1):
                low = max(block, 4 * quad)
                count = min(block + blocks, 4 * quad + 4) - low
                there = low + dst_block - block
                a = there // 4 * QUAD + there % 4
                b = quad * QUAD + low % 4
                nc.sync.dma_start(
                    out=dst_scales[a : a + count, cols].bitcast(I32),
                    in_=v_scales[b : b + count, sp, cols].bitcast(I32),
                )

        def make_diag(quad):
            for g in range(KVH):
                    move(diag_codes[quad], diag_scales[:, quad, :], 4 * g, 0, 4 * quad, 4, slice(g * D, (g + 1) * D))

        def make_old(b):
            nc.sync.dma_start(
                out=old_planes[b][b : P : QUAD].rearrange("p j f -> p (j f)").bitcast(I32),
                in_=diag_scales[b : P : QUAD].rearrange("p j f -> p (j f)").bitcast(I32),
            )

        def make_roll(n):
            if True:
                nc.sync.dma_start(out=roll_codes[n][:].bitcast(I32), in_=v_codes[:, 0, :].bitcast(I32))
                nc.sync.dma_start(out=roll_scales[n][:].bitcast(I32), in_=v_scales[:, 0, :].bitcast(I32))

        def advance_roll(j):
            first = max(j - 3, 0)
            move(roll_codes[j % 4], roll_scales[j % 4], first, 1, first, j + 1 - first, slice(0, KVH * D))

        def turn_k(n):
            bank = banks_pool.tile([P, KVH, P], BF16, tag="bank")
            for g in range(KVH):
                nc.tensor.matmul(
                    out=bank[:, g, :], lhsT=k_raw[:, n, g * D : (g + 1) * D], rhs=ident_bf[:], start=True, stop=True
                )
            return bank

        def lay_k(copy, n, bank):
            copy(
                out=kT[:].rearrange("d g s u c -> d (g s u c)").bitcast(F32).rearrange(
                    "d (g s u c) -> d g s u c", g=KVH, s=S_PASSES, u=2
                )[:, :, n // 4, :, (n % 4) * QUAD : (n % 4 + 1) * QUAD],
                in_=bank[:].rearrange("d g t -> d (g t)").bitcast(F32).rearrange(
                    "d (g p u) -> d g u p", g=KVH, u=2
                ),
            )

        def turn_q(n, g, half):
            if half == 0:
                bank = banks_pool.tile([P, 2 * R, P], BF16, tag="bank")
                q_bank[n, g] = bank
            for h in range(half * R, (half + 1) * R):
                first = (g * R + h) * D
                nc.tensor.matmul(
                    out=q_bank[n, g][:, h, :], lhsT=q_raw[n][:, first : first + D], rhs=ident_bf[:], start=True, stop=True
                )

        def row_op(n):
            if n < KVH:
                return w_ops[n]
            op = x_ops[n - KVH]
            if "codes" not in op:
                codes = xq_pool.tile([P, X_PASSES * P], U32, align_bytes=64, name="x_codes")
                scales = xq_pool.tile([P, X_PASSES * P], U8, align_bytes=64, name="x_scales")
                op["codes"] = codes[:]
                op["scales"] = scales[:]
            return op

        def lay_q(copy, n, g, bank):
            copy(
                out=qT[:, n * (P // CH) : (n + 1) * (P // CH), g : g + 2, :, :].rearrange("d c g h i -> d c (g h) i"),
                in_=bank[:].rearrange("d h (c i) -> d c h i", i=CH),
            )

        def score_old(quad, part):
            if part == 0:
                bank = banks_pool.tile([P, 4, KVH, CH], F32, tag="bank")
                nc.tensor.matmul(
                    out=bank[:].rearrange("p c g j -> p (c g j)"), lhsT=spread_cols,
                    rhs=old_bias[:].rearrange("k n j -> k (n j)"), start=True, stop=False,
                )
                of_quad[quad] = {"bank": bank}
            bank = of_quad[quad]["bank"]
            for b in (2 * part, 2 * part + 1):
                j = 4 * quad + b
                for g in range(KVH):
                    nc.tensor.matmul(
                        out=bank[:, b, g, :].rearrange("p (u c) -> p u c", u=2),
                        lhsT=qT[:, FULL + j, g].rearrange("d h i -> d (h i)"),
                        rhs=kT[:, g, 0, :, j * HC : (j + 1) * HC],
                        start=False,
                        stop=(b == 3 and g == KVH - 1),
                    )

        def old_peak(quad):
            bank = of_quad[quad]["bank"]
            old_max = stat.tile([P, 4, KVH], F32, name="old_max")
            nc.vector.tensor_reduce(out=old_max[:], in_=bank[:], axis=AXIS_X, op=ALU.max)
            neg_old = stat.tile([P, 4, KVH], F32, name="neg_old")
            of_quad[quad].update({"max": old_max, "neg": neg_old})

        def old_copy(quad):
            old_scores = rest_pool.tile([P, 4, KVH, CH], F32, name="old_scores")
            nc.scalar.copy(out=old_scores[:], in_=of_quad[quad]["bank"][:])
            of_quad[quad]["scores"] = old_scores

        def negate_old(quad):
            nc.vector.tensor_scalar(
                out=of_quad[quad]["neg"][:], in0=of_quad[quad]["max"][:], scalar1=-SCALE, scalar2=None, op0=ALU.mult
            )

        def score(i):
            c, half = i // 2, i % 2
            if half == 0:
                if c % 2 == 0:
                    t_sums = stat.tile([P, 2, 2, KVH], F32, name="sums")
                    of_chunk["sums"] = t_sums
                of_chunk[c] = {
                    "top": stat.tile([P, KVH], F32, name="top"),
                    "shift": stat.tile([P, KVH], F32, name="shift"),
                    "sums": of_chunk["sums"],
                    "units": [],
                }
            j = c % FULL
            live = (j + 1) * HC
            if c < FULL // 2:
                both = banks_pool.tile([P, 2, 2, P], F32, tag="bank")
                of_both[i] = both
                for t in range(2):
                    g = 2 * half + t
                    nc.tensor.matmul(
                        out=both[:, t, :, 0:live], lhsT=qT[:, c, g].rearrange("d h i -> d (h i)"),
                        rhs=kT[:, g, 0, :, 0:live], start=(t == 0), stop=False,
                    )
                nc.tensor.matmul(
                    out=both[:, :, :, live - HC : live], lhsT=spread_cols,
                    rhs=own_bias[:].unsqueeze(1).to_broadcast([P, 2, 2, HC]), start=False, stop=True,
                )
                of_pair[i] = [both[:, 0], both[:, 1]]
                return
            banks = []
            for t in range(2):
                g = 2 * half + t
                own = banks_pool.tile([P, 2, 2 * P], F32, tag="bank")
                bank = own[:]
                lhsT = qT[:, c, g].rearrange("d h i -> d (h i)")
                if c >= FULL and live < 2 * P:
                    nc.tensor.matmul(
                        out=bank[:, :, live : 2 * P], lhsT=lhsT, rhs=kT[:, g, 0, :, live : 2 * P],
                        start=True, stop=True,
                    )
                nc.tensor.matmul(
                    out=bank[:, :, 0:live], lhsT=lhsT, rhs=kT[:, g, c // FULL, :, 0:live], start=True, stop=False
                )
                nc.tensor.matmul(
                    out=bank[:, :, live - HC : live], lhsT=spread_cols, rhs=own_bias[:], start=False, stop=True
                )
                banks.append(bank)
            of_pair[i] = banks

        def peak(i):
            c, half = i // 2, i % 2
            live = (c % FULL + 1) * HC if c < FULL else 2 * P
            top = of_chunk[c]["top"]
            if c < FULL // 2:
                nc.vector.tensor_reduce(
                    out=top[:, 2 * half : 2 * half + 2], in_=of_both[i][:, :, :, 0:live],
                    axis=AXIS_XY, op=ALU.max,
                )
            else:
                for t in range(2):
                    g = 2 * half + t
                    nc.vector.tensor_reduce(
                        out=top[:, g : g + 1], in_=of_pair[i][t][:, :, 0:live], axis=AXIS_XY, op=ALU.max
                    )

        def set_shift(i):
            c, half = i // 2, i % 2
            cols = slice(2 * half, 2 * half + 2)
            top = of_chunk[c]["top"][:, cols]
            shift = of_chunk[c]["shift"][:, cols]
            if c < FULL:
                nc.vector.tensor_scalar(out=shift, in0=top, scalar1=-SCALE, scalar2=None, op0=ALU.mult)
            else:
                nc.vector.scalar_tensor_tensor(
                    out=shift, in0=top, scalar=-SCALE, in1=of_quad[(c - FULL) // 4]["neg"][:, c % 4, cols],
                    op0=ALU.mult, op1=ALU.min,
                )

        def soften_some(out_ap, in_ap, c, g, slot):
            nc.scalar.activation(
                out=out_ap, in_=in_ap, func=ACT.Exp, bias=of_chunk[c]["shift"][:, g : g + 1], scale=SCALE,
                accum_out=of_chunk[c]["sums"][:, slot, c % 2, g : g + 1],
            )

        def diag_view(tile_, quads):
            return tile_[:].rearrange("q (j u g w) -> q j u g w", j=quads, u=2, g=KVH)

        def soften(i):
            c, half = i // 2, i % 2
            for t in range(2):
                g = 2 * half + t
                bank = of_pair[i][t]
                if c < DIAG:
                    e = diag_view(e_diag[c % 2], 2)
                    quads, rest = (c + 1) // 4, (c + 1) % 4
                    if quads > 0:
                        soften_some(
                            e[:, 0:quads, :, g, :],
                            bank[:, :, 0 : quads * HQ].rearrange("q u (j w) -> q j u w", w=HQ),
                            c, g, 0,
                        )
                    if rest > 0:
                        soften_some(
                            e[:, quads, :, g, 0 : rest * HC],
                            bank[:, :, quads * HQ : quads * HQ + rest * HC],
                            c, g, 1 if quads > 0 else 0,
                        )
                else:
                    live = (c + 1) * HC if c < FULL else 2 * P
                    e = e_row[2 * (i % 3) + t][:].rearrange("q (u c) -> q u c", u=2)
                    soften_some(e[:, :, 0:live], bank[:, :, 0:live], c, g, 0)
                    if c >= FULL:
                        b = c % 4
                        soften_some(
                            diag_view(e_old[POOL_OF[c] % 2], 1)[:, 0, :, g, b * HC : (b + 1) * HC],
                            of_quad[(c - FULL) // 4]["scores"][:, b, g, :].rearrange("q (u c) -> q u c", u=2),
                            c, g, 1,
                        )

        def total(c):
            sums = of_chunk[c]["sums"]
            if c >= FULL or 4 <= c < DIAG:
                seats = 1 if c == DIAG - 1 else 2
                nc.vector.tensor_tensor(
                    out=sums[:, 0, 0:seats], in0=sums[:, 0, 0:seats], in1=sums[:, 1, 0:seats], op=ALU.add
                )

        def invert(c):
            inverse = stat.tile([P, 2, KVH], F32, name="inverse")
            nc.vector.reciprocal(out=inverse[:], in_=of_chunk[c]["sums"][:, 0])
            of_chunk[c - 1]["inverse"] = inverse[:, 0]
            of_chunk[c]["inverse"] = inverse[:, 1]

        def jobs_of(i):
            c, half = i // 2, i % 2
            if c < DIAG:
                if half == 0:
                    return []
                words = e_diag[c % 2][:].bitcast(F32)
                units = [words[:, j * 2 * P : (j + 1) * 2 * P] for j in range(c // 4 + 1)]
                return [units[n : n + 2] for n in range(0, len(units), 2)]
            jobs = [[e_row[2 * (i % 3) + t][:].bitcast(F32) for t in range(2)]]
            if c >= FULL and half == 1 and c == POOLS[POOL_OF[c]][-1]:
                jobs.append([e_old[POOL_OF[c] % 2][:].bitcast(F32)])
            return jobs

        def flip_e(c, units):
            bank = banks_pool.tile([P, 2, 2, P], F32, tag="bank")
            for n in range(len(units)):
                for u in range(2):
                    nc.tensor.transpose(bank[:, n, u, :], units[n][:, u * P : (u + 1) * P], ident32[:])
            return {"c": c, "n": len(units), "bank": bank}

        def regroup(job):
            n = job["n"]
            grouped = work.tile([P, 2 * P * PACK], BF16, align_bytes=64, name="e_grouped")
            nc.scalar.copy(
                out=grouped[:].bitcast(F32).rearrange("p (n t u) -> p n t u", n=2, u=2)[:, 0:n],
                in_=job["bank"][:, 0:n].rearrange("p n u t -> p n t u"),
            )
            job["grouped"] = grouped

        def quantise(job):
            n = job["n"]
            codes = packed.tile([P, 2 * P], U32, align_bytes=64, name="e_codes")
            scales = packed.tile([P, 2 * P], U8, align_bytes=64, name="e_scales")
            nc.vector.quantize_mx(
                out=codes[:, 0 : n * P].bitcast(FP8X4), scales=scales[:, 0 : n * P],
                in_=job["grouped"][:, 0 : n * P * PACK],
            )
            units = [(codes[:, m * P : (m + 1) * P], scales[:, m * P : (m + 1) * P]) for m in range(n)]
            if job["c"] >= FULL and n == 1:
                for c in POOLS[POOL_OF[job["c"]]]:
                    of_chunk[c]["old"] = units[0]
            else:
                of_chunk[job["c"]]["units"] += units

        def mx(out_ap, unit, codes, scales, start, stop):
            nc.tensor.matmul_mx(
                out=out_ap, lhsT=unit[0].bitcast(FP8X4), lhsT_scale=unit[1],
                rhs=codes.bitcast(FP8X4), rhs_scale=scales, start=start, stop=stop,
            )

        def weigh(c):
            o_sum = banks_pool.tile([P, KVH, D], F32, tag="bank")
            units = of_chunk[c]["units"]
            flat = o_sum[:].rearrange("p g d -> p (g d)")
            if c < DIAG:
                for j in range(len(units)):
                    mx(flat, units[j], diag_codes[j][:], diag_scales[:, j, :], j == 0, j == len(units) - 1)
            else:
                if c >= FULL:
                    quad, b = (c - FULL) // 4, c % 4
                    mx(flat, of_chunk[c]["old"], diag_codes[quad][:], old_planes[b][:, quad, :], True, False)
                    codes, scales = roll_codes[c % 4][:], roll_scales[c % 4][:]
                else:
                    codes, scales = v_codes[:, 0, :], v_scales[:, 0, :]
                for g in range(KVH):
                    cols = slice(g * D, (g + 1) * D)
                    mx(o_sum[:, g, :], units[g], codes[:, cols], scales[:, cols], c < FULL, c < FULL or g == KVH - 1)
            of_chunk[c]["o_sum"] = o_sum

        def finish(c):
            o_sb = store_pool.tile([P, KVH, D], F32, name="o_sb")
            nc.vector.tensor_tensor(
                out=o_sb[:], in0=of_chunk[c]["o_sum"][:],
                in1=of_chunk[c]["inverse"].unsqueeze(2).to_broadcast([P, KVH, D]), op=ALU.mult,
            )
            chunk_rows = out_rows[c * CH : (c + 1) * CH, :].rearrange("i (g h d) -> h i g d", g=KVH, h=R)
            for h in range(R):
                nc.sync.dma_start(out=chunk_rows[h], in_=o_sb[h * CH : (h + 1) * CH, :, :])

        of_chunk = {}
        of_pair = {}
        of_both = {}
        of_quad = {}
        q_raw = {}
        q_bank = {}
        v_bank = {}
        with tc.manual_schedule():
            def load_k(first, count):
                nc.sync.dma_start(
                    out=k_raw[:, first : first + count, :],
                    in_=k_rows[first * P : (first + count) * P, :].rearrange("(n p) f -> p n f", p=P),
                )

            load_k(0, 1)
            load_k(1, 3)
            load_q(0)
            w_ops = []
            x_ops = []
            for g in range(KVH):
                w_ops.append({
                    "rows": load_rows(wv[g * D : (g + 1) * D, :]),
                    "codes": w_codes[:, g, :], "scales": w_scales[:, g, :],
                })
                if g == 1:
                    load_q(1)

            def load_x(n):
                in_ = x_rows[n // PACK * K_PASS : (n // PACK + 1) * K_PASS, :].rearrange("(p t) k -> t p k", t=PACK)
                x_ops.append({"rows": load_rows(in_[n % PACK])})

            load_k(4, 4)
            load_q(2)
            load_x(0)
            load_x(1)
            load_q(3)
            load_x(2)
            load_x(3)

            warm_bank = banks_pool.tile([P, PACK, P], F32, tag="bank")
            for n in range(9):
                nc.tensor.matmul(
                    out=warm_bank[:, n % PACK, :], lhsT=ident_bf[:], rhs=ident_bf[:], start=True, stop=True
                )

            copies = (nc.scalar.copy, nc.vector.tensor_copy)
            for n in range(4):
                lay_k(copies[n % 2], n, turn_k(n))
            for g in range(0, KVH, 2):
                turn_q(0, g, 0)
                turn_q(0, g, 1)
                lay_q(copies[g // 2], 0, g, q_bank[0, g])
            load_q(4)

            lead = 2
            prep = []
            for r in range(2 * (KVH + PACK)):
                prep.append((r - lead, ("rows", r // 2, r % 2)))
            for g in range(KVH):
                prep.append((15 + 2 * g, ("v", 0, g)))
            for r in range(2 * PACK):
                prep.append((16 + r * 4 // 2, ("rows", KVH + PACK + r // 2, r % 2)))
            for g in range(KVH):
                prep.append((32 + 2 * g, ("v", 1, g)))
            due = []
            to_quantise = []
            weighed = 0
            of_step = {}

            def later(step, what, fn):
                of_step.setdefault((step, what), []).append(fn)

            def run_now(step, what):
                for fn in of_step.get((step, what), []):
                    fn()

            for at, piece in prep:
                if piece[0] == "rows":
                    n, half = piece[1], piece[2]
                    later(at, "T", lambda n=n, half=half: turn_rows(row_op(n), half))
                    on_v = False
                    later(at + 0, "V copy" if on_v else "S copy", lambda n=n, half=half, on_v=on_v: lay_rows(row_op(n), half, nc.vector.tensor_copy if on_v else nc.scalar.copy))
                    if half == 1:
                        later(at + 1, "V quantise", lambda n=n: quantise_rows(row_op(n)))
                else:
                    sp, g = piece[1], piece[2]
                    later(at, "MX", lambda sp=sp, g=g: project(sp, g))
                    on_v = False
                    later(at, "V copy" if on_v else "S copy", lambda g=g, on_v=on_v: lay_v(g, nc.vector.tensor_copy if on_v else nc.scalar.copy))
                    if g == KVH - 1:
                        later(at + 1, "V quantise", lambda sp=sp: quantise_v(sp))
                        if sp == 0:
                            for n in range(4):
                                later(at + 1 + (0, 1, 6, 9)[n], "V quantise", lambda n=n: make_diag(n))
                                later(at + 3 + n, "V quantise", lambda n=n: make_roll(n))
                                later(at + 12 + n, "V quantise", lambda n=n: make_old(n))
                        else:
                            for j in range(4):
                                later(at + 1, "V quantise", lambda j=j: advance_roll(j))
            for n in range(1, T // P):
                for g in range(0, KVH, 2):
                    at = 2 + (2 * n - 2 + g // 2) * 4 // 2
                    assert at <= 8 * n - 3
                    later(at, "plain", lambda n=n, g=g: turn_q(n, g, 0))
                    later(at + 1, "plain", lambda n=n, g=g: turn_q(n, g, 1))
                    later(at + 1, "V copy", lambda n=n, g=g: lay_q(nc.vector.tensor_copy, n, g, q_bank[n, g]))
                    if g == KVH - 2 and n + 4 < T // P:
                        later(at + 1, "V copy", lambda n=n: load_q(n + 4))
            k_bank = {}

            def turn_k_keep(n):
                k_bank[n] = turn_k(n)

            for n in range(4, T // P):
                later(2 * n - 3, "plain", lambda n=n: turn_k_keep(n))
                later(2 * n - 3, ("S copy", "V copy")[n % 2], lambda n=n: lay_k(copies[n % 2], n, k_bank[n]))
            for n in range(4):
                later(8 + n, "V copy", lambda n=n: nc.sync.dma_start(out=diag_codes[n][:].bitcast(I32), in_=zeros))
                later(8 + n, "V copy", lambda n=n: nc.sync.dma_start(
                    out=old_planes[n][:].rearrange("p j f -> p (j f)").bitcast(I32), in_=zeros
                ))
            for quad in range(4):
                at = 8 * quad
                later(at + 29, "plain", lambda quad=quad: score_old(quad, 0))
                later(at + 29, "plain", lambda quad=quad: score_old(quad, 1))
                later(at + 29, "V copy", lambda quad=quad: old_peak(quad))
                later(at + 29 + 1, "S copy", lambda quad=quad: old_copy(quad))
                later(at + 29 + 1, "V early", lambda quad=quad: negate_old(quad))

            for i in range(-lead, PAIRS + 4):
                jobs = []
                if 0 <= i - 1 < PAIRS:
                    for units in jobs_of(i - 1):
                        jobs.append(flip_e((i - 1) // 2, units))
                run_now(i, "T")
                done = []
                if weighed < CHUNKS and i >= max(2 * (POOLS[POOL_OF[weighed]][-1] if weighed >= FULL else weighed) + 4, 27 + 5 * weighed // 4):
                    weigh(weighed)
                    done.append(weighed)
                    weighed += 1
                run_now(i, "MX")
                if 0 <= i < PAIRS:
                    soften(i)
                for job in jobs:
                    regroup(job)
                run_now(i, "plain")
                if 0 <= i + 2 < PAIRS:
                    score(i + 2)
                if 0 <= i + 1 < PAIRS:
                    peak(i + 1)
                if i >= 4 and i % 4 == 0 and i // 2 <= CHUNKS:
                    total(i // 2 - 1)
                run_now(i, "V early")
                for job in to_quantise:
                    quantise(job)
                to_quantise = jobs
                if 0 <= i + 1 < PAIRS:
                    set_shift(i + 1)
                if i >= 4 and i % 4 == 0 and i // 2 <= CHUNKS:
                    invert(i // 2 - 1)
                for c in done:
                    finish(c)
                    if FULL <= c < CHUNKS - 4:
                        advance_roll(c - FULL + 4)
                run_now(i, "V quantise")
                run_now(i, "V copy")
                run_now(i, "S copy")
                if 0 <= i < 2 * PACK and i % 2 == 0:
                    load_x(PACK + i // 2)
